import numpy as np
import ml_dtypes


def mxq(x, axis, fmt="e4m3"):
    dtype, down = {"e4m3": (ml_dtypes.float8_e4m3fn, 7), "e5m2": (ml_dtypes.float8_e5m2, 14)}[fmt]
    v = np.moveaxis(np.asarray(x, np.float32).astype(ml_dtypes.bfloat16).astype(np.float64), axis, -1)
    blocks = v.reshape(v.shape[:-1] + (-1, 32))
    amax = np.abs(blocks).max(-1, keepdims=True)
    byte = np.maximum(np.where(amax > 0, np.frexp(amax)[1] - 1 + 127, 0) - down, 1)
    scale = np.exp2(byte - 127.0)
    codes = (blocks / scale).astype(np.float32).astype(dtype).astype(np.float64)
    return np.moveaxis((codes * scale).reshape(v.shape), -1, axis)


WIDE = False


def mx_kscale(k):
    if not WIDE:
        return np.ones(k)
    levels = np.array([10, -10, 5, -5, 0])
    a = np.random.permutation(np.resize(levels, k // 512 * 4)).reshape(k // 512, 4)
    idx = np.arange(k)
    return np.exp2(a[idx // 512, idx % 128 // 32])


BF16 = ml_dtypes.bfloat16


def bf(x):
    return np.asarray(x, np.float32).astype(BF16)


def f64(x):
    return np.asarray(x).astype(np.float64)


B, N_OUT, SO, SI, NV, NC, N_PHI, N_DIST, N_SIGMA = 4, 128, 16, 32, 1, 32, 8, 8, 2
DIST_UNIT = 2.0
MIN_SIGMA = 1e-10


def sigmoid(v):
    return 1.0 / (1.0 + np.exp(-v))


def setup_inputs():
    n_in = N_OUT * SO * SI
    a = 2.0 * np.maximum(np.log2(mx_kscale(SO * SI)), 0.0)
    x = bf(np.random.standard_normal((B, n_in, 1, NV, NC)) * 2.0 * np.tile(2.0 ** a, N_OUT)[None, :, None, None, None])
    ux = np.random.uniform(-DIST_UNIT, DIST_UNIT, (1, N_OUT, SO, SI))
    uy = np.random.uniform(-DIST_UNIT, DIST_UNIT, (1, N_OUT, SO, SI))
    phis = bf(np.linspace(-np.pi, np.pi, N_PHI + 1)[:-1] + 0.05 * np.random.standard_normal(N_PHI))
    d = np.arange(1, 2 * N_DIST, 2) / (N_DIST * 2)
    dists_param = bf(-np.log(1.0 / d - 1.0) + 0.1 * np.random.standard_normal(N_DIST))
    s = 0.1 * np.arange(1, N_SIGMA + 1)
    sigma_param = bf(-np.log(1.0 / s - 1.0) + 0.1 * np.random.standard_normal(N_SIGMA))
    dmax = (DIST_UNIT * sigmoid(f64(dists_param))).max()
    smax = (DIST_UNIT * sigmoid(f64(sigma_param))).max()
    A = a.reshape(1, 1, SO, SI)
    R = dmax + smax * np.sqrt(2.0 * np.log(2.0) * A)
    r = np.hypot(ux, uy)
    coords_x = bf(np.where(A > 0, ux / r * R, ux))
    coords_y = bf(np.where(A > 0, uy / r * R, uy))
    return {"x": x, "coords_x": coords_x, "coords_y": coords_y, "phis": phis, "dists_param": dists_param, "sigma_param": sigma_param}


def reference(x, coords_x, coords_y, phis, dists_param, sigma_param):
    x, coords_x, coords_y = f64(x), f64(coords_x), f64(coords_y)
    phis, dists_param, sigma_param = f64(phis), f64(dists_param), f64(sigma_param)
    b = x.shape[0]
    nv, nc = x.shape[-2], x.shape[-1]
    n_out, so, si = coords_x.shape[1], coords_x.shape[2], coords_x.shape[3]
    n_p, n_d, n_s = phis.shape[0], dists_param.shape[0], sigma_param.shape[0]

    dists = DIST_UNIT * sigmoid(dists_param)
    mu_x = np.cos(phis)[:, None] * dists[None, :]
    mu_y = np.sin(phis)[:, None] * dists[None, :]
    sigma = np.maximum(DIST_UNIT * sigmoid(sigma_param), MIN_SIGMA)

    dx = coords_x[0][..., None, None] - mu_x
    dy = coords_y[0][..., None, None] - mu_y
    w = np.exp(-0.5 * (dx * dx + dy * dy)[..., None] / (sigma * sigma))
    w = w / (w.sum(axis=(1, 2), keepdims=True) + 1e-20)

    wq = mxq(w.reshape(n_out, so * si, n_p * n_d * n_s), 1, "e4m3")
    xq = mxq(x.reshape(b, n_out, so * si, nv, nc), 2, "e4m3")
    out = wq.transpose(0, 2, 1)[None, :, None] @ xq.transpose(0, 1, 3, 2, 4)
    return out.reshape(b, n_out, nv, n_p, n_d, n_s, nc)

@@ -1,0 +1,271 @@
+import math
+from contextlib import ExitStack
+
+import concourse.mybir as mybir
+from concourse.masks import make_identity
+
+F32 = mybir.dt.float32
+BF16 = mybir.dt.bfloat16
+I32 = mybir.dt.int32
+U32 = mybir.dt.uint32
+U8 = mybir.dt.uint8
+FP8X4 = mybir.dt.float8_e4m3fn_x4
+ALU = mybir.AluOpType
+ACT = mybir.ActivationFunctionType
+
+P = 128
+NODES = 128
+BATCH = 4
+CH = 32
+NPHI = 8
+NDIST = 8
+NB = 8
+BLOCKS = NODES // NB
+CJ = NB * 4
+
+FLOPS = 2 * NODES * 512 * 128 * (BATCH * CH)
+
+TWO_PI = 2.0 * math.pi
+TWO_PI_HI = 6.28125
+TWO_PI_LO = TWO_PI - TWO_PI_HI
+
+
+def tile_polnormal_nolayer_t_kernel(tc, x, coords_x, coords_y, phis, dists_param, sigma_param, out):
+    nc = tc.nc
+    xv = x.rearrange("b (o p j) u v c -> b p o (j u v c)", o=NODES, p=P, j=4)
+    ov = out.rearrange("b o v f d s c -> b (v f d s) o c")
+
+    with ExitStack() as ctx:
+        const = ctx.enter_context(tc.tile_pool(name="const", bufs=1))
+        xin = ctx.enter_context(tc.tile_pool(name="xin", bufs=3))
+        work = ctx.enter_context(tc.tile_pool(name="work", bufs=2))
+        ps_small = ctx.enter_context(tc.psum_pool(name="ps_small", bufs=2))
+        ps_t = ctx.enter_context(tc.psum_pool(name="ps_t", bufs=2))
+        ps_w = ctx.enter_context(tc.psum_pool(name="ps_w", bufs=2))
+        ps_o = ctx.enter_context(tc.psum_pool(name="ps_o", bufs=2))
+
+        cxk = const.tile([P, 512], BF16)
+        cyk = const.tile([P, 512], BF16)
+        ph_b = const.tile([P, NPHI], BF16)
+        dp_b = const.tile([P, NDIST], BF16)
+        sp_b = const.tile([P, 2], BF16)
+        nc.sync.dma_start(out=ph_b[:], in_=phis.partition_broadcast(P))
+        nc.sync.dma_start(out=dp_b[:], in_=dists_param.partition_broadcast(P))
+        nc.sync.dma_start(out=sp_b[:], in_=sigma_param.partition_broadcast(P))
+        nc.sync.dma_start(out=cxk[:], in_=coords_x.rearrange("a o i j -> (a o) (i j)"))
+        nc.sync.dma_start(out=cyk[:], in_=coords_y.rearrange("a o i j -> (a o) (i j)"))
+
+        identf = const.tile([P, P], F32)
+        make_identity(nc, identf[:])
+        identb = const.tile([P, P], BF16)
+        nc.vector.tensor_copy(out=identb[:], in_=identf[:])
+        perm = const.tile([P, P], BF16)
+        nc.vector.tensor_copy(
+            out=perm[:].rearrange("q (f d l) -> q f d l", f=NPHI, d=NDIST, l=2),
+            in_=identb[:].rearrange("q (l d f) -> q f d l", l=2, d=NDIST, f=NPHI),
+        )
+        qsum = const.tile([P, 2, 64], F32)
+        nc.vector.tensor_tensor(
+            out=qsum[:],
+            in0=identf[:, 0:64].unsqueeze(1).to_broadcast([P, 2, 64]),
+            in1=identf[:, 64:128].unsqueeze(1).to_broadcast([P, 2, 64]),
+            op=ALU.add,
+        )
+
+        ph = const.tile([P, NPHI], F32)
+        nc.vector.tensor_copy(out=ph[:], in_=ph_b[:])
+        turns_i = const.tile([P, NPHI], I32)
+        nc.vector.tensor_scalar(out=turns_i[:], in0=ph[:], scalar1=1.0 / TWO_PI, scalar2=None, op0=ALU.mult)
+        turns = const.tile([P, NPHI], F32)
+        nc.vector.tensor_copy(out=turns[:], in_=turns_i[:])
+        ra = const.tile([P, NPHI], F32)
+        nc.vector.scalar_tensor_tensor(out=ra[:], in0=turns[:], scalar=-TWO_PI_HI, in1=ph[:], op0=ALU.mult, op1=ALU.add)
+        rb = const.tile([P, NPHI], F32)
+        nc.vector.scalar_tensor_tensor(out=rb[:], in0=turns[:], scalar=-TWO_PI_LO, in1=ra[:], op0=ALU.mult, op1=ALU.add)
+        over = const.tile([P, NPHI], F32)
+        nc.vector.tensor_scalar(out=over[:], in0=rb[:], scalar1=math.pi, scalar2=None, op0=ALU.is_gt)
+        under = const.tile([P, NPHI], F32)
+        nc.vector.tensor_scalar(out=under[:], in0=rb[:], scalar1=-math.pi, scalar2=None, op0=ALU.is_lt)
+        rc = const.tile([P, NPHI], F32)
+        nc.vector.scalar_tensor_tensor(out=rc[:], in0=over[:], scalar=-TWO_PI, in1=rb[:], op0=ALU.mult, op1=ALU.add)
+        ang = const.tile([P, 2 * NPHI], F32)
+        nc.vector.scalar_tensor_tensor(out=ang[:, 0:NPHI], in0=under[:], scalar=TWO_PI, in1=rc[:], op0=ALU.mult, op1=ALU.add)
+        rneg = const.tile([P, NPHI], F32)
+        nc.vector.tensor_scalar(out=rneg[:], in0=ang[:, 0:NPHI], scalar1=-1.0, scalar2=None, op0=ALU.mult)
+        rabs = const.tile([P, NPHI], F32)
+        nc.vector.tensor_tensor(out=rabs[:], in0=ang[:, 0:NPHI], in1=rneg[:], op=ALU.max)
+        nc.vector.tensor_scalar(
+            out=ang[:, NPHI : 2 * NPHI], in0=rabs[:], scalar1=-1.0, scalar2=0.5 * math.pi, op0=ALU.mult, op1=ALU.add
+        )
+        trig = const.tile([P, 2 * NPHI], F32)
+        nc.scalar.activation(out=trig[:], in_=ang[:], func=ACT.Sin)
+
+        pr = const.tile([P, NDIST + 2], F32)
+        nc.vector.tensor_copy(out=pr[:, 0:NDIST], in_=dp_b[:])
+        nc.vector.tensor_copy(out=pr[:, NDIST : NDIST + 2], in_=sp_b[:])
+        th = const.tile([P, NDIST + 2], F32)
+        nc.scalar.activation(out=th[:], in_=pr[:], func=ACT.Tanh, scale=0.5)
+        ds = const.tile([P, NDIST + 2], F32)
+        nc.vector.tensor_scalar(out=ds[:], in0=th[:], scalar1=1.0, scalar2=None, op0=ALU.add)
+        m2d = const.tile([P, NDIST], F32)
+        nc.vector.tensor_scalar(out=m2d[:], in0=ds[:, 0:NDIST], scalar1=-2.0, scalar2=None, op0=ALU.mult)
+        d2 = const.tile([P, NDIST], F32)
+        nc.vector.tensor_tensor(out=d2[:], in0=ds[:, 0:NDIST], in1=ds[:, 0:NDIST], op=ALU.mult)
+        sg = const.tile([P, 2], F32)
+        nc.vector.tensor_scalar(out=sg[:], in0=ds[:, NDIST : NDIST + 2], scalar1=1e-10, scalar2=None, op0=ALU.max)
+        sg2 = const.tile([P, 2], F32)
+        nc.vector.tensor_tensor(out=sg2[:], in0=sg[:], in1=sg[:], op=ALU.mult)
+        rsg = const.tile([P, 2], F32)
+        nc.vector.reciprocal(out=rsg[:], in_=sg2[:])
+        na = const.tile([P, 2], F32)
+        nc.vector.tensor_scalar(out=na[:], in0=rsg[:], scalar1=-0.5, scalar2=None, op0=ALU.mult)
+
+        bsd = const.tile([P, 2, NDIST], F32)
+        nc.vector.tensor_tensor(
+            out=bsd[:],
+            in0=d2[:].unsqueeze(1).to_broadcast([P, 2, NDIST]),
+            in1=na[:].unsqueeze(2).to_broadcast([P, 2, NDIST]),
+            op=ALU.mult,
+        )
+        brow = const.tile([P, 2, 2, NDIST, NPHI], F32)
+        for l in range(2):
+            nc.vector.tensor_copy(
+                out=brow[:, :, l, :, :], in_=bsd[:].unsqueeze(3).to_broadcast([P, 2, NDIST, NPHI])
+            )
+        bps = ps_small.tile([P, 2, P], F32, tag="small")
+        for s in range(2):
+            nc.tensor.transpose(
+                out=bps[:, s, :], in_=brow[:, s, :, :, :].rearrange("p l d f -> p (l d f)"), identity=identf[:]
+            )
+        biasc = const.tile([P, 2], F32)
+        nc.vector.tensor_copy(out=biasc[:], in_=bps[:, :, 0:1].rearrange("q s o -> q (s o)"))
+
+        cps = ps_small.tile([P, 2, 4, P], BF16, tag="small")
+        for c, src in enumerate((cxk, cyk)):
+            view = src[:].rearrange("o (p j) -> o j p", j=4)
+            for j in range(4):
+                nc.tensor.transpose(out=cps[:, c, j, :], in_=view[:, j, :], identity=identb[:])
+        cxy = const.tile([P, 2, NODES, 4], F32)
+        nc.vector.tensor_copy(out=cxy[:], in_=cps[:].rearrange("p c j o -> p c o j"))
+        sq = const.tile([P, 2, NODES * 4], F32)
+        cflat = cxy[:].rearrange("p c o j -> p c (o j)")
+        nc.vector.tensor_tensor(out=sq[:], in0=cflat, in1=cflat, op=ALU.mult)
+        r2 = const.tile([P, NODES * 4], F32)
+        nc.vector.tensor_tensor(out=r2[:], in0=sq[:, 0, :], in1=sq[:, 1, :], op=ALU.add)
+
+        sinb = trig[:, 0:NPHI].unsqueeze(1).to_broadcast([P, CJ, NPHI])
+        cosb = trig[:, NPHI : 2 * NPHI].unsqueeze(1).to_broadcast([P, CJ, NPHI])
+
+        for blk in range(BLOCKS):
+            o0 = blk * NB
+            cs = slice(blk * CJ, (blk + 1) * CJ)
+
+            xr = xin.tile([P, BATCH, NB, 4 * CH], BF16)
+            for b in range(BATCH):
+                nc.sync.dma_start(out=xr[:, b, :, :], in_=xv[b, :, o0 : o0 + NB, :])
+            xg = work.tile([P, NB, BATCH, CH, 4], BF16, align_bytes=64)
+            for b in range(BATCH):
+                nc.vector.tensor_copy(
+                    out=xg[:, :, b, :, :].rearrange("p o (g i) t -> p o g t i", i=4),
+                    in_=xr[:, b, :, :].rearrange("p o (t g i) -> p o g t i", t=4, i=4),
+                )
+            xq = work.tile([P, NB * P], U32, align_bytes=64)
+            xs = work.tile([P, NB * P], U8, align_bytes=64)
+            nc.vector.quantize_mx(
+                out=xq[:].bitcast(FP8X4), scales=xs[:], in_=xg[:].rearrange("p o b c t -> p (o b c t)")
+            )
+
+            ua = work.tile([P, CJ, NPHI], F32)
+            nc.vector.tensor_tensor(
+                out=ua[:], in0=cflat[:, 0, cs].unsqueeze(2).to_broadcast([P, CJ, NPHI]), in1=cosb, op=ALU.mult
+            )
+            ub = work.tile([P, CJ, NPHI], F32)
+            nc.vector.tensor_tensor(
+                out=ub[:], in0=cflat[:, 1, cs].unsqueeze(2).to_broadcast([P, CJ, NPHI]), in1=sinb, op=ALU.mult
+            )
+            u = work.tile([P, CJ, NPHI], F32)
+            nc.vector.tensor_tensor(out=u[:], in0=ua[:], in1=ub[:], op=ALU.add)
+            ta = work.tile([P, NB, 2, 2, NDIST, NPHI], F32)
+            tview = ta[:].rearrange("p o h l d f -> p (o h l) d f")
+            r2b = r2[:, cs].unsqueeze(2).to_broadcast([P, CJ, NPHI])
+            for d in range(NDIST):
+                nc.vector.scalar_tensor_tensor(
+                    out=tview[:, :, d, :], in0=u[:], scalar=m2d[:, d : d + 1], in1=r2b, op0=ALU.mult, op1=ALU.add
+                )
+
+            gc = work.tile([P, NB, 2, 2 * P], F32)
+            spart = work.tile([P, NB * 2], F32)
+            for pair in range(NB // 2):
+                tcp = ps_t.tile([P, 2, 2, P], F32)
+                for o2 in range(2):
+                    for h in range(2):
+                        nc.tensor.transpose(
+                            out=tcp[:, o2, h, :],
+                            in_=ta[:, 2 * pair + o2, h, :, :, :].rearrange("p l d f -> p (l d f)"),
+                            identity=identf[:],
+                        )
+                for o2 in range(2):
+                    o = 2 * pair + o2
+                    for s in range(2):
+                        nc.scalar.activation(
+                            out=gc[:, o, s, :],
+                            in_=tcp[:, o2, :, :].rearrange("q h p -> q (h p)"),
+                            func=ACT.Exp,
+                            bias=biasc[:, s : s + 1],
+                            scale=na[:, s : s + 1],
+                            accum_out=spart[:, 2 * o + s : 2 * o + s + 1],
+                        )
+            stot = ps_small.tile([P, NB * 2], F32, tag="small")
+            nc.tensor.matmul(out=stot[:], lhsT=qsum[:].rearrange("q h c -> q (h c)"), rhs=spart[:], start=True, stop=True)
+            den = work.tile([P, NB * 2], F32)
+            nc.vector.tensor_scalar(out=den[:], in0=stot[:], scalar1=1e-20, scalar2=None, op0=ALU.add)
+            inv = work.tile([P, NB * 2], F32)
+            nc.vector.reciprocal(out=inv[:], in_=den[:])
+
+            wc = work.tile([P, NB, 2, 2 * P], BF16)
+            wsb = work.tile([P, NB, 4 * P], BF16, align_bytes=64)
+            for pair in range(NB // 2):
+                wps = ps_w.tile([P, 2, 64, 2, 2, 2], BF16)
+                for o2 in range(2):
+                    o = 2 * pair + o2
+                    for s in range(2):
+                        nc.vector.tensor_scalar(
+                            out=wc[:, o, s, :],
+                            in0=gc[:, o, s, :],
+                            scalar1=inv[:, 2 * o + s : 2 * o + s + 1],
+                            scalar2=None,
+                            op0=ALU.mult,
+                        )
+                        for h in range(2):
+                            nc.tensor.transpose(
+                                out=wps[:, o2, :, s, h, :], in_=wc[:, o, s, h * P : (h + 1) * P], identity=perm[:]
+                            )
+                nc.scalar.copy(
+                    out=wsb[:, 2 * pair : 2 * pair + 2, :].rearrange("p o n -> p (o n)"),
+                    in_=wps[:].rearrange("p o m s h l -> p (o m s h l)"),
+                )
+            wq = work.tile([P, NB * P], U32, align_bytes=64)
+            ws = work.tile([P, NB * P], U8, align_bytes=64)
+            nc.vector.quantize_mx(out=wq[:].bitcast(FP8X4), scales=ws[:], in_=wsb[:].rearrange("p o n -> p (o n)"))
+
+            osb = work.tile([P, NB, BATCH * CH], F32)
+            for quad in range(NB // 4):
+                ops = ps_o.tile([P, 4, BATCH * CH], F32)
+                for i in range(4):
+                    o = quad * 4 + i
+                    cols = slice(o * P, (o + 1) * P)
+                    nc.tensor.matmul_mx(
+                        out=ops[:, i, :],
+                        lhsT=wq[:, cols].bitcast(FP8X4),
+                        lhsT_scale=ws[:, cols],
+                        rhs=xq[:, cols].bitcast(FP8X4),
+                        rhs_scale=xs[:, cols],
+                        start=True,
+                        stop=True,
+                    )
+                nc.scalar.copy(
+                    out=osb[:, quad * 4 : quad * 4 + 4, :].rearrange("m o n -> m (o n)"),
+                    in_=ops[:].rearrange("m o n -> m (o n)"),
+                )
+            for b in range(BATCH):
+                nc.scalar.dma_start(out=ov[b, :, o0 : o0 + NB, :], in_=osb[:, :, b * CH : (b + 1) * CH])

@@ -156,36 +156,47 @@ def tile_polnormal_nolayer_t_kernel(tc, x, coords_x, coords_y, phis, dists_param
         sinb = trig[:, 0:NPHI].unsqueeze(1).to_broadcast([P, CJ, NPHI])
         cosb = trig[:, NPHI : 2 * NPHI].unsqueeze(1).to_broadcast([P, CJ, NPHI])
 
-        for blk in range(BLOCKS):
-            o0 = blk * NB
-            cs = slice(blk * CJ, (blk + 1) * CJ)
+        xr_t, xq_t, xs_t, ta_t, gc_t, sp_t, inv_t, wc_t, wsb_t, wq_t, ws_t, osb_t, tcp_t, ops_t = (
+            {}, {}, {}, {}, {}, {}, {}, {}, {}, {}, {}, {}, {}, {},
+        )
 
-            xr = xin.tile([P, BATCH, NB, 4 * CH], BF16)
+        def live(n):
+            return 0 <= n < BLOCKS
+
+        def load_x(n):
+            xr = xin.tile([P, BATCH, NB, 4 * CH], BF16, name="xr")
+            xr_t[n] = xr
             for b in range(BATCH):
-                nc.sync.dma_start(out=xr[:, b, :, :], in_=xv[b, :, o0 : o0 + NB, :])
-            xg = work.tile([P, NB, BATCH, CH, 4], BF16, align_bytes=64)
+                nc.sync.dma_start(out=xr[:, b, :, :], in_=xv[b, :, n * NB : (n + 1) * NB, :])
+
+        def quantise_x(n):
+            xr = xr_t[n]
+            xg = work.tile([P, NB, BATCH, CH, 4], BF16, align_bytes=64, name="xg")
             for b in range(BATCH):
                 nc.vector.tensor_copy(
                     out=xg[:, :, b, :, :].rearrange("p o (g i) t -> p o g t i", i=4),
                     in_=xr[:, b, :, :].rearrange("p o (t g i) -> p o g t i", t=4, i=4),
                 )
-            xq = work.tile([P, NB * P], U32, align_bytes=64)
-            xs = work.tile([P, NB * P], U8, align_bytes=64)
+            xq_t[n] = work.tile([P, NB * P], U32, align_bytes=64, name="xq")
+            xs_t[n] = work.tile([P, NB * P], U8, align_bytes=64, name="xs")
             nc.vector.quantize_mx(
-                out=xq[:].bitcast(FP8X4), scales=xs[:], in_=xg[:].rearrange("p o b c t -> p (o b c t)")
+                out=xq_t[n][:].bitcast(FP8X4), scales=xs_t[n][:], in_=xg[:].rearrange("p o b c t -> p (o b c t)")
             )
 
-            ua = work.tile([P, CJ, NPHI], F32)
+        def distances(n):
+            cs = slice(n * CJ, (n + 1) * CJ)
+            ua = work.tile([P, CJ, NPHI], F32, name="ua")
             nc.vector.tensor_tensor(
                 out=ua[:], in0=cflat[:, 0, cs].unsqueeze(2).to_broadcast([P, CJ, NPHI]), in1=cosb, op=ALU.mult
             )
-            ub = work.tile([P, CJ, NPHI], F32)
+            ub = work.tile([P, CJ, NPHI], F32, name="ub")
             nc.vector.tensor_tensor(
                 out=ub[:], in0=cflat[:, 1, cs].unsqueeze(2).to_broadcast([P, CJ, NPHI]), in1=sinb, op=ALU.mult
             )
-            u = work.tile([P, CJ, NPHI], F32)
+            u = work.tile([P, CJ, NPHI], F32, name="u")
             nc.vector.tensor_tensor(out=u[:], in0=ua[:], in1=ub[:], op=ALU.add)
-            ta = work.tile([P, NB, 2, 2, NDIST, NPHI], F32)
+            ta = work.tile([P, NB, 2, 2, NDIST, NPHI], F32, name="ta")
+            ta_t[n] = ta
             tview = ta[:].rearrange("p o h l d f -> p (o h l) d f")
             r2b = r2[:, cs].unsqueeze(2).to_broadcast([P, CJ, NPHI])
             for d in range(NDIST):
@@ -193,79 +204,144 @@ def tile_polnormal_nolayer_t_kernel(tc, x, coords_x, coords_y, phis, dists_param
                     out=tview[:, :, d, :], in0=u[:], scalar=m2d[:, d : d + 1], in1=r2b, op0=ALU.mult, op1=ALU.add
                 )
 
-            gc = work.tile([P, NB, 2, 2 * P], F32)
-            spart = work.tile([P, NB * 2], F32)
-            for pair in range(NB // 2):
-                tcp = ps_t.tile([P, 2, 2, P], F32)
-                for o2 in range(2):
+        def to_components(n, pair):
+            tcp = ps_t.tile([P, 2, 2, P], F32, name="tcp")
+            tcp_t[(n, pair)] = tcp
+            for o2 in range(2):
+                for h in range(2):
+                    nc.tensor.transpose(
+                        out=tcp[:, o2, h, :],
+                        in_=ta_t[n][:, 2 * pair + o2, h, :, :, :].rearrange("p l d f -> p (l d f)"),
+                        identity=identf[:],
+                    )
+
+        def exponentials(n, pair):
+            if pair == 0:
+                gc_t[n] = work.tile([P, NB, 2, 2 * P], F32, name="gc")
+                sp_t[n] = work.tile([P, NB * 2], F32, name="spart")
+            tcp = tcp_t[(n, pair)]
+            for o2 in range(2):
+                o = 2 * pair + o2
+                for s in range(2):
+                    nc.scalar.activation(
+                        out=gc_t[n][:, o, s, :],
+                        in_=tcp[:, o2, :, :].rearrange("q h p -> q (h p)"),
+                        func=ACT.Exp,
+                        bias=biasc[:, s : s + 1],
+                        scale=na[:, s : s + 1],
+                        accum_out=sp_t[n][:, 2 * o + s : 2 * o + s + 1],
+                    )
+
+        stot_t = {}
+
+        def sums(n):
+            stot_t[n] = ps_small.tile([P, NB * 2], F32, tag="small", name="stot")
+            nc.tensor.matmul(
+                out=stot_t[n][:], lhsT=qsum[:].rearrange("q h c -> q (h c)"), rhs=sp_t[n][:], start=True, stop=True
+            )
+
+        def reciprocals(n):
+            den = work.tile([P, NB * 2], F32, name="den")
+            nc.vector.tensor_scalar(out=den[:], in0=stot_t[n][:], scalar1=1e-20, scalar2=None, op0=ALU.add)
+            inv_t[n] = work.tile([P, NB * 2], F32, name="inv")
+            nc.vector.reciprocal(out=inv_t[n][:], in_=den[:])
+            wc_t[n] = work.tile([P, NB, 2, 2 * P], BF16, name="wc")
+
+        wps_t = {}
+
+        def normalise(n, pair):
+            wps = ps_w.tile([P, 2, 64, 2, 2, 2], BF16, name="wps")
+            wps_t[(n, pair)] = wps
+            for o2 in range(2):
+                o = 2 * pair + o2
+                for s in range(2):
+                    nc.vector.tensor_scalar(
+                        out=wc_t[n][:, o, s, :],
+                        in0=gc_t[n][:, o, s, :],
+                        scalar1=inv_t[n][:, 2 * o + s : 2 * o + s + 1],
+                        scalar2=None,
+                        op0=ALU.mult,
+                    )
                     for h in range(2):
                         nc.tensor.transpose(
-                            out=tcp[:, o2, h, :],
-                            in_=ta[:, 2 * pair + o2, h, :, :, :].rearrange("p l d f -> p (l d f)"),
-                            identity=identf[:],
+                            out=wps[:, o2, :, s, h, :], in_=wc_t[n][:, o, s, h * P : (h + 1) * P], identity=perm[:]
                         )
-                for o2 in range(2):
-                    o = 2 * pair + o2
-                    for s in range(2):
-                        nc.scalar.activation(
-                            out=gc[:, o, s, :],
-                            in_=tcp[:, o2, :, :].rearrange("q h p -> q (h p)"),
-                            func=ACT.Exp,
-                            bias=biasc[:, s : s + 1],
-                            scale=na[:, s : s + 1],
-                            accum_out=spart[:, 2 * o + s : 2 * o + s + 1],
-                        )
-            stot = ps_small.tile([P, NB * 2], F32, tag="small")
-            nc.tensor.matmul(out=stot[:], lhsT=qsum[:].rearrange("q h c -> q (h c)"), rhs=spart[:], start=True, stop=True)
-            den = work.tile([P, NB * 2], F32)
-            nc.vector.tensor_scalar(out=den[:], in0=stot[:], scalar1=1e-20, scalar2=None, op0=ALU.add)
-            inv = work.tile([P, NB * 2], F32)
-            nc.vector.reciprocal(out=inv[:], in_=den[:])
 
-            wc = work.tile([P, NB, 2, 2 * P], BF16)
-            wsb = work.tile([P, NB, 4 * P], BF16, align_bytes=64)
-            for pair in range(NB // 2):
-                wps = ps_w.tile([P, 2, 64, 2, 2, 2], BF16)
-                for o2 in range(2):
-                    o = 2 * pair + o2
-                    for s in range(2):
-                        nc.vector.tensor_scalar(
-                            out=wc[:, o, s, :],
-                            in0=gc[:, o, s, :],
-                            scalar1=inv[:, 2 * o + s : 2 * o + s + 1],
-                            scalar2=None,
-                            op0=ALU.mult,
-                        )
-                        for h in range(2):
-                            nc.tensor.transpose(
-                                out=wps[:, o2, :, s, h, :], in_=wc[:, o, s, h * P : (h + 1) * P], identity=perm[:]
-                            )
-                nc.scalar.copy(
-                    out=wsb[:, 2 * pair : 2 * pair + 2, :].rearrange("p o n -> p (o n)"),
-                    in_=wps[:].rearrange("p o m s h l -> p (o m s h l)"),
-                )
-            wq = work.tile([P, NB * P], U32, align_bytes=64)
-            ws = work.tile([P, NB * P], U8, align_bytes=64)
-            nc.vector.quantize_mx(out=wq[:].bitcast(FP8X4), scales=ws[:], in_=wsb[:].rearrange("p o n -> p (o n)"))
+        def weights_out(n, pair):
+            if pair == 0:
+                wsb_t[n] = work.tile([P, NB, 4 * P], BF16, align_bytes=64, name="wsb")
+            nc.scalar.copy(
+                out=wsb_t[n][:, 2 * pair : 2 * pair + 2, :].rearrange("p o n -> p (o n)"),
+                in_=wps_t[(n, pair)][:].rearrange("p o m s h l -> p (o m s h l)"),
+            )
 
-            osb = work.tile([P, NB, BATCH * CH], F32)
+        def quantise_w(n):
+            wq_t[n] = work.tile([P, NB * P], U32, align_bytes=64, name="wq")
+            ws_t[n] = work.tile([P, NB * P], U8, align_bytes=64, name="ws")
+            nc.vector.quantize_mx(
+                out=wq_t[n][:].bitcast(FP8X4), scales=ws_t[n][:], in_=wsb_t[n][:].rearrange("p o n -> p (o n)")
+            )
+
+        def pool_nodes(n):
             for quad in range(NB // 4):
-                ops = ps_o.tile([P, 4, BATCH * CH], F32)
+                ops = ps_o.tile([P, 4, BATCH * CH], F32, name="ops")
+                ops_t[(n, quad)] = ops
                 for i in range(4):
-                    o = quad * 4 + i
-                    cols = slice(o * P, (o + 1) * P)
+                    cols = slice((quad * 4 + i) * P, (quad * 4 + i + 1) * P)
                     nc.tensor.matmul_mx(
                         out=ops[:, i, :],
-                        lhsT=wq[:, cols].bitcast(FP8X4),
-                        lhsT_scale=ws[:, cols],
-                        rhs=xq[:, cols].bitcast(FP8X4),
-                        rhs_scale=xs[:, cols],
+                        lhsT=wq_t[n][:, cols].bitcast(FP8X4),
+                        lhsT_scale=ws_t[n][:, cols],
+                        rhs=xq_t[n][:, cols].bitcast(FP8X4),
+                        rhs_scale=xs_t[n][:, cols],
                         start=True,
                         stop=True,
                     )
+
+        def store(n):
+            osb = work.tile([P, NB, BATCH * CH], F32, name="osb")
+            for quad in range(NB // 4):
                 nc.scalar.copy(
                     out=osb[:, quad * 4 : quad * 4 + 4, :].rearrange("m o n -> m (o n)"),
-                    in_=ops[:].rearrange("m o n -> m (o n)"),
+                    in_=ops_t[(n, quad)][:].rearrange("m o n -> m (o n)"),
                 )
             for b in range(BATCH):
-                nc.scalar.dma_start(out=ov[b, :, o0 : o0 + NB, :], in_=osb[:, :, b * CH : (b + 1) * CH])
+                nc.scalar.dma_start(out=ov[b, :, n * NB : (n + 1) * NB, :], in_=osb[:, :, b * CH : (b + 1) * CH])
+
+        with tc.manual_schedule():
+            load_x(0)
+            load_x(1)
+            distances(0)
+            to_components(0, 0)
+            to_components(0, 1)
+            for n in range(BLOCKS + 2):
+                if live(n + 2):
+                    load_x(n + 2)
+                if live(n - 1):
+                    sums(n - 1)
+                if live(n - 2):
+                    quantise_w(n - 2)
+                    pool_nodes(n - 2)
+                if live(n - 1):
+                    reciprocals(n - 1)
+                    normalise(n - 1, 0)
+                if live(n):
+                    exponentials(n, 0)
+                    exponentials(n, 1)
+                for pair in range(4):
+                    if live(n - 1):
+                        weights_out(n - 1, pair)
+                    if live(n) and pair < 2:
+                        to_components(n, pair + 2)
+                    if live(n - 1) and pair < 3:
+                        normalise(n - 1, pair + 1)
+                    if live(n) and pair < 2:
+                        exponentials(n, pair + 2)
+                if live(n - 2):
+                    store(n - 2)
+                if live(n + 1):
+                    distances(n + 1)
+                    to_components(n + 1, 0)
+                    to_components(n + 1, 1)
+                if live(n):
+                    quantise_x(n)

@@ -166,8 +166,10 @@ def tile_polnormal_nolayer_t_kernel(tc, x, coords_x, coords_y, phis, dists_param
         def load_x(n):
             xr = xin.tile([P, BATCH, NB, 4 * CH], BF16, name="xr")
             xr_t[n] = xr
-            for b in range(BATCH):
-                nc.sync.dma_start(out=xr[:, b, :, :], in_=xv[b, :, n * NB : (n + 1) * NB, :])
+            for half in range(NB // 4):
+                lo = half * 4
+                for b in range(BATCH):
+                    nc.sync.dma_start(out=xr[:, b, lo : lo + 4, :], in_=xv[b, :, n * NB + lo : n * NB + lo + 4, :])
 
         def quantise_x(n):
             xr = xr_t[n]
@@ -301,12 +303,15 @@ def tile_polnormal_nolayer_t_kernel(tc, x, coords_x, coords_y, phis, dists_param
         def store(n):
             osb = work.tile([P, NB, BATCH * CH], F32, name="osb")
             for quad in range(NB // 4):
+                lo = quad * 4
                 nc.scalar.copy(
-                    out=osb[:, quad * 4 : quad * 4 + 4, :].rearrange("m o n -> m (o n)"),
+                    out=osb[:, lo : lo + 4, :].rearrange("m o n -> m (o n)"),
                     in_=ops_t[(n, quad)][:].rearrange("m o n -> m (o n)"),
                 )
-            for b in range(BATCH):
-                nc.scalar.dma_start(out=ov[b, :, n * NB : (n + 1) * NB, :], in_=osb[:, :, b * CH : (b + 1) * CH])
+                for b in range(BATCH):
+                    nc.sync.dma_start(
+                        out=ov[b, :, n * NB + lo : n * NB + lo + 4, :], in_=osb[:, lo : lo + 4, b * CH : (b + 1) * CH]
+                    )
 
         with tc.manual_schedule():
             load_x(0)

@@ -44,16 +44,19 @@ def tile_polnormal_nolayer_t_kernel(tc, x, coords_x, coords_y, phis, dists_param
         ps_w = ctx.enter_context(tc.psum_pool(name="ps_w", bufs=2))
         ps_o = ctx.enter_context(tc.psum_pool(name="ps_o", bufs=2))
 
-        cxk = const.tile([P, 512], BF16)
-        cyk = const.tile([P, 512], BF16)
+        ccb = [const.tile([P, 512], BF16, name="ccb%d" % half) for half in range(2)]
         ph_b = const.tile([P, NPHI], BF16)
         dp_b = const.tile([P, NDIST], BF16)
         sp_b = const.tile([P, 2], BF16)
         nc.sync.dma_start(out=ph_b[:], in_=phis.partition_broadcast(P))
         nc.sync.dma_start(out=dp_b[:], in_=dists_param.partition_broadcast(P))
         nc.sync.dma_start(out=sp_b[:], in_=sigma_param.partition_broadcast(P))
-        nc.sync.dma_start(out=cxk[:], in_=coords_x.rearrange("a o i j -> (a o) (i j)"))
-        nc.sync.dma_start(out=cyk[:], in_=coords_y.rearrange("a o i j -> (a o) (i j)"))
+        for half in range(2):
+            for c, coords in enumerate((coords_x, coords_y)):
+                nc.sync.dma_start(
+                    out=ccb[half][c * 64 : (c + 1) * 64, :],
+                    in_=coords.rearrange("a o i j -> (a o) (i j)")[half * 64 : (half + 1) * 64, :],
+                )
 
         identf = const.tile([P, P], F32)
         make_identity(nc, identf[:])
@@ -140,21 +143,38 @@ def tile_polnormal_nolayer_t_kernel(tc, x, coords_x, coords_y, phis, dists_param
         biasc = const.tile([P, 2], F32)
         nc.vector.tensor_copy(out=biasc[:], in_=bps[:, :, 0:1].rearrange("q s o -> q (s o)"))
 
-        cps = ps_small.tile([P, 2, 4, P], BF16, tag="small")
-        for c, src in enumerate((cxk, cyk)):
-            view = src[:].rearrange("o (p j) -> o j p", j=4)
+        cps = ps_small.tile([P, 2, 4, 2, 64], BF16, tag="small")
+        for half in range(2):
+            view = ccb[half][:].rearrange("q (p j) -> q j p", j=4)
             for j in range(4):
-                nc.tensor.transpose(out=cps[:, c, j, :], in_=view[:, j, :], identity=identb[:])
+                nc.tensor.transpose(
+                    out=cps[:, half, j, :, :].rearrange("p c o -> p (c o)"), in_=view[:, j, :], identity=identb[:]
+                )
         cxy = const.tile([P, 2, NODES, 4], F32)
-        nc.vector.tensor_copy(out=cxy[:], in_=cps[:].rearrange("p c j o -> p c o j"))
+        for half in range(2):
+            nc.vector.tensor_copy(
+                out=cxy[:, :, half * 64 : (half + 1) * 64, :],
+                in_=cps[:, half, :, :, :].rearrange("p j c o -> p c o j"),
+            )
+        ccf = [const.tile([P, 4, P], F32, name="ccf%d" % half) for half in range(2)]
+        for half in range(2):
+            nc.vector.tensor_copy(out=ccf[half][:], in_=ccb[half][:].rearrange("q (p j) -> q j p", j=4))
+        trg = const.tile([P, NPHI], F32)
+        nc.vector.tensor_copy(out=trg[0:64, :], in_=trig[0:64, NPHI : 2 * NPHI])
+        nc.vector.tensor_copy(out=trg[64:128, :], in_=trig[64:128, 0:NPHI])
+        proj = const.tile([P, 64, NPHI], F32)
+        nc.vector.tensor_tensor(
+            out=proj[:],
+            in0=qsum[:, 0, :].unsqueeze(2).to_broadcast([P, 64, NPHI]),
+            in1=trg[:].unsqueeze(1).to_broadcast([P, 64, NPHI]),
+            op=ALU.mult,
+        )
         sq = const.tile([P, 2, NODES * 4], F32)
         cflat = cxy[:].rearrange("p c o j -> p c (o j)")
         nc.vector.tensor_tensor(out=sq[:], in0=cflat, in1=cflat, op=ALU.mult)
         r2 = const.tile([P, NODES * 4], F32)
         nc.vector.tensor_tensor(out=r2[:], in0=sq[:, 0, :], in1=sq[:, 1, :], op=ALU.add)
 
-        sinb = trig[:, 0:NPHI].unsqueeze(1).to_broadcast([P, CJ, NPHI])
-        cosb = trig[:, NPHI : 2 * NPHI].unsqueeze(1).to_broadcast([P, CJ, NPHI])
 
         xr_t, xq_t, xs_t, ta_t, gc_t, sp_t, inv_t, wc_t, wsb_t, wq_t, ws_t, osb_t, tcp_t, ops_t = (
             {}, {}, {}, {}, {}, {}, {}, {}, {}, {}, {}, {}, {}, {},
@@ -185,25 +205,31 @@ def tile_polnormal_nolayer_t_kernel(tc, x, coords_x, coords_y, phis, dists_param
                 out=xq_t[n][:].bitcast(FP8X4), scales=xs_t[n][:], in_=xg[:].rearrange("p o b c t -> p (o b c t)")
             )
 
+        ups_t = {}
+
+        def project(n):
+            half, first = divmod(n * NB, 64)
+            ups = ps_small.tile([P, NB, 4, NPHI], F32, tag="small", name="ups")
+            ups_t[n] = ups
+            for j in range(4):
+                nc.tensor.matmul(
+                    out=ups[:, :, j, :],
+                    lhsT=ccf[half][:, j, :],
+                    rhs=proj[:, first : first + NB, :],
+                    start=True,
+                    stop=True,
+                )
+
         def distances(n):
             cs = slice(n * CJ, (n + 1) * CJ)
-            ua = work.tile([P, CJ, NPHI], F32, name="ua")
-            nc.vector.tensor_tensor(
-                out=ua[:], in0=cflat[:, 0, cs].unsqueeze(2).to_broadcast([P, CJ, NPHI]), in1=cosb, op=ALU.mult
-            )
-            ub = work.tile([P, CJ, NPHI], F32, name="ub")
-            nc.vector.tensor_tensor(
-                out=ub[:], in0=cflat[:, 1, cs].unsqueeze(2).to_broadcast([P, CJ, NPHI]), in1=sinb, op=ALU.mult
-            )
-            u = work.tile([P, CJ, NPHI], F32, name="u")
-            nc.vector.tensor_tensor(out=u[:], in0=ua[:], in1=ub[:], op=ALU.add)
+            u = ups_t[n][:].rearrange("p o j f -> p (o j) f")
             ta = work.tile([P, NB, 2, 2, NDIST, NPHI], F32, name="ta")
             ta_t[n] = ta
             tview = ta[:].rearrange("p o h l d f -> p (o h l) d f")
             r2b = r2[:, cs].unsqueeze(2).to_broadcast([P, CJ, NPHI])
             for d in range(NDIST):
                 nc.vector.scalar_tensor_tensor(
-                    out=tview[:, :, d, :], in0=u[:], scalar=m2d[:, d : d + 1], in1=r2b, op0=ALU.mult, op1=ALU.add
+                    out=tview[:, :, d, :], in0=u, scalar=m2d[:, d : d + 1], in1=r2b, op0=ALU.mult, op1=ALU.add
                 )
 
         def to_components(n, pair):
@@ -316,6 +342,7 @@ def tile_polnormal_nolayer_t_kernel(tc, x, coords_x, coords_y, phis, dists_param
         with tc.manual_schedule():
             load_x(0)
             load_x(1)
+            project(0)
             distances(0)
             to_components(0, 0)
             to_components(0, 1)
@@ -327,6 +354,8 @@ def tile_polnormal_nolayer_t_kernel(tc, x, coords_x, coords_y, phis, dists_param
                 if live(n - 2):
                     quantise_w(n - 2)
                     pool_nodes(n - 2)
+                if live(n + 1):
+                    project(n + 1)
                 if live(n - 1):
                     reciprocals(n - 1)
                     normalise(n - 1, 0)

@@ -37,7 +37,8 @@ def tile_polnormal_nolayer_t_kernel(tc, x, coords_x, coords_y, phis, dists_param
 
     with ExitStack() as ctx:
         const = ctx.enter_context(tc.tile_pool(name="const", bufs=1))
-        xin = ctx.enter_context(tc.tile_pool(name="xin", bufs=3))
+        xin = ctx.enter_context(tc.tile_pool(name="xin", bufs=4))
+        xgp = ctx.enter_context(tc.tile_pool(name="xgp", bufs=1))
         work = ctx.enter_context(tc.tile_pool(name="work", bufs=2))
         ps_small = ctx.enter_context(tc.psum_pool(name="ps_small", bufs=2))
         ps_t = ctx.enter_context(tc.psum_pool(name="ps_t", bufs=2))
@@ -191,14 +192,29 @@ def tile_polnormal_nolayer_t_kernel(tc, x, coords_x, coords_y, phis, dists_param
                 for b in range(BATCH):
                     nc.sync.dma_start(out=xr[:, b, lo : lo + 4, :], in_=xv[b, :, n * NB + lo : n * NB + lo + 4, :])
 
-        def quantise_x(n):
-            xr = xr_t[n]
-            xg = work.tile([P, NB, BATCH, CH, 4], BF16, align_bytes=64, name="xg")
-            for b in range(BATCH):
-                nc.vector.tensor_copy(
-                    out=xg[:, :, b, :, :].rearrange("p o (g i) t -> p o g t i", i=4),
-                    in_=xr[:, b, :, :].rearrange("p o (t g i) -> p o g t i", t=4, i=4),
+        xg_t = {}
+
+        def interleave_on_gpsimd(n):
+            xg_t[n] = xgp.tile([P, NB, BATCH, CH, 4], BF16, align_bytes=64, name="xg")
+            for b in range(0, 2):
+                nc.gpsimd.tensor_scalar(
+                    out=xg_t[n][:, :, b, :, :],
+                    in0=xr_t[n][:, b, :, :].rearrange("p o (t c) -> p o c t", t=4),
+                    scalar1=1.0,
+                    scalar2=0.0,
+                    op0=ALU.mult,
+                    op1=ALU.add,
                 )
+
+        def interleave_on_vector(n):
+            for b in range(2, BATCH):
+                nc.vector.tensor_copy(
+                    out=xg_t[n][:, :, b, :, :].rearrange("p o (g i) t -> p o g t i", i=4),
+                    in_=xr_t[n][:, b, :, :].rearrange("p o (t g i) -> p o g t i", t=4, i=4),
+                )
+
+        def quantise_x(n):
+            xg = xg_t[n]
             xq_t[n] = work.tile([P, NB * P], U32, align_bytes=64, name="xq")
             xs_t[n] = work.tile([P, NB * P], U8, align_bytes=64, name="xs")
             nc.vector.quantize_mx(
@@ -342,6 +358,7 @@ def tile_polnormal_nolayer_t_kernel(tc, x, coords_x, coords_y, phis, dists_param
         with tc.manual_schedule():
             load_x(0)
             load_x(1)
+            interleave_on_gpsimd(0)
             project(0)
             distances(0)
             to_components(0, 0)
@@ -367,15 +384,18 @@ def tile_polnormal_nolayer_t_kernel(tc, x, coords_x, coords_y, phis, dists_param
                         weights_out(n - 1, pair)
                     if live(n) and pair < 2:
                         to_components(n, pair + 2)
+                    if live(n) and pair == 2:
+                        interleave_on_vector(n)
                     if live(n - 1) and pair < 3:
                         normalise(n - 1, pair + 1)
                     if live(n) and pair < 2:
                         exponentials(n, pair + 2)
                 if live(n - 2):
                     store(n - 2)
+                if live(n):
+                    quantise_x(n)
                 if live(n + 1):
+                    interleave_on_gpsimd(n + 1)
                     distances(n + 1)
                     to_components(n + 1, 0)
                     to_components(n + 1, 1)
-                if live(n):
-                    quantise_x(n)

@@ -12,6 +12,7 @@ U8 = mybir.dt.uint8
 FP8X4 = mybir.dt.float8_e4m3fn_x4
 ALU = mybir.AluOpType
 ACT = mybir.ActivationFunctionType
+AXES = mybir.AxisListType
 
 P = 128
 NODES = 128
@@ -19,11 +20,14 @@ BATCH = 4
 CH = 32
 NPHI = 8
 NDIST = 8
-NB = 8
-BLOCKS = NODES // NB
-CJ = NB * 4
+T = 4
+BN = 8
+GN = 16
+BLOCKS = NODES // BN
+GROUPS = NODES // GN
+CELLS = P * T
 
-FLOPS = 2 * NODES * 512 * 128 * (BATCH * CH)
+FLOPS = 2 * NODES * CELLS * 128 * (BATCH * CH)
 
 TWO_PI = 2.0 * math.pi
 TWO_PI_HI = 6.28125
@@ -32,370 +36,447 @@ TWO_PI_LO = TWO_PI - TWO_PI_HI
 
 def tile_polnormal_nolayer_t_kernel(tc, x, coords_x, coords_y, phis, dists_param, sigma_param, out):
     nc = tc.nc
-    xv = x.rearrange("b (o p j) u v c -> b p o (j u v c)", o=NODES, p=P, j=4)
-    ov = out.rearrange("b o v f d s c -> b (v f d s) o c")
+    xv = x.rearrange("b (o p t) u v c -> b p o (t u v c)", o=NODES, p=P, t=T)
+    ov = out.rearrange("b (n i o) v f d s c -> n b (o v f d) i (s c)", i=BN // 2, o=2)
+    coords = [c.rearrange("a o i j -> (a o) (i j)") for c in (coords_x, coords_y)]
 
     with ExitStack() as ctx:
         const = ctx.enter_context(tc.tile_pool(name="const", bufs=1))
         xin = ctx.enter_context(tc.tile_pool(name="xin", bufs=4))
         xgp = ctx.enter_context(tc.tile_pool(name="xgp", bufs=1))
         work = ctx.enter_context(tc.tile_pool(name="work", bufs=2))
-        ps_small = ctx.enter_context(tc.psum_pool(name="ps_small", bufs=2))
+        ps_s = ctx.enter_context(tc.psum_pool(name="ps_s", bufs=2))
         ps_t = ctx.enter_context(tc.psum_pool(name="ps_t", bufs=2))
         ps_w = ctx.enter_context(tc.psum_pool(name="ps_w", bufs=2))
         ps_o = ctx.enter_context(tc.psum_pool(name="ps_o", bufs=2))
+        ctx.enter_context(tc.manual_schedule())
 
-        ccb = [const.tile([P, 512], BF16, name="ccb%d" % half) for half in range(2)]
         ph_b = const.tile([P, NPHI], BF16)
-        dp_b = const.tile([P, NDIST], BF16)
-        sp_b = const.tile([P, 2], BF16)
+        pr_b = const.tile([P, NDIST + 2], BF16, name="pr_b")
+        sp_b = const.tile([P, 2], BF16, name="sp_b")
+        ccb = [const.tile([P, CELLS], BF16, name="ccb%d" % half) for half in range(2)]
+        cg = const.tile([P, GROUPS, CELLS], BF16)
         nc.sync.dma_start(out=ph_b[:], in_=phis.partition_broadcast(P))
-        nc.sync.dma_start(out=dp_b[:], in_=dists_param.partition_broadcast(P))
+        nc.sync.dma_start(out=pr_b[:, 0:NDIST], in_=dists_param.partition_broadcast(P))
         nc.sync.dma_start(out=sp_b[:], in_=sigma_param.partition_broadcast(P))
-        for half in range(2):
-            for c, coords in enumerate((coords_x, coords_y)):
+
+        def load_rows(half):
+            for c in range(2):
                 nc.sync.dma_start(
-                    out=ccb[half][c * 64 : (c + 1) * 64, :],
-                    in_=coords.rearrange("a o i j -> (a o) (i j)")[half * 64 : (half + 1) * 64, :],
+                    out=ccb[half][c * 64 : (c + 1) * 64, :], in_=coords[c][half * 64 : (half + 1) * 64, :]
                 )
+
+        def load_groups(lo, hi):
+            for c in range(2):
+                rows = coords[c][lo * GN : hi * GN, :].rearrange("(g o) n -> o g n", o=GN)
+                for piece in range(4):
+                    r = c * 64 + piece * GN
+                    nc.sync.dma_start(out=cg[r : r + GN, lo:hi, :], in_=rows)
+
+        load_rows(0)
+        load_groups(0, 1)
 
         identf = const.tile([P, P], F32)
         make_identity(nc, identf[:])
+        seed = const.tile([P, 1], F32)
+        nc.vector.memset(seed[:], 0.0)
+        warm = const.tile([P, 2], F32)
+        nc.scalar.activation(out=warm[:, 0:1], in_=seed[:], func=ACT.Tanh)
         identb = const.tile([P, P], BF16)
         nc.vector.tensor_copy(out=identb[:], in_=identf[:])
-        perm = const.tile([P, P], BF16)
-        nc.vector.tensor_copy(
-            out=perm[:].rearrange("q (f d l) -> q f d l", f=NPHI, d=NDIST, l=2),
-            in_=identb[:].rearrange("q (l d f) -> q f d l", l=2, d=NDIST, f=NPHI),
+        same = const.tile([P, GN], F32)
+        nc.vector.tensor_reduce(
+            out=same[:], in_=identf[:].rearrange("k (j o) -> k o j", o=GN), axis=AXES.X, op=ALU.add
         )
-        qsum = const.tile([P, 2, 64], F32)
-        nc.vector.tensor_tensor(
-            out=qsum[:],
-            in0=identf[:, 0:64].unsqueeze(1).to_broadcast([P, 2, 64]),
-            in1=identf[:, 64:128].unsqueeze(1).to_broadcast([P, 2, 64]),
-            op=ALU.add,
+        mask = const.tile([P, 4], F32)
+        nc.vector.tensor_reduce(
+            out=mask[:], in_=identf[:].rearrange("k (c q o) -> k q c o", c=2, q=4), axis=AXES.XY, op=ALU.add
         )
 
-        ph = const.tile([P, NPHI], F32)
-        nc.vector.tensor_copy(out=ph[:], in_=ph_b[:])
+        pick = const.tile([P, NDIST], F32)
+        nc.vector.tensor_reduce(
+            out=pick[:], in_=identf[:].rearrange("q (l d f) -> q d l f", l=2, d=NDIST), axis=AXES.XY, op=ALU.add
+        )
+
+        a0 = const.tile([P, NPHI], F32)
+        nc.vector.tensor_scalar(out=a0[0:64, :], in0=ph_b[0:64, :], scalar1=0.5 * math.pi, scalar2=None, op0=ALU.add)
+        nc.vector.tensor_copy(out=a0[64:128, :], in_=ph_b[64:128, :])
         turns_i = const.tile([P, NPHI], I32)
-        nc.vector.tensor_scalar(out=turns_i[:], in0=ph[:], scalar1=1.0 / TWO_PI, scalar2=None, op0=ALU.mult)
+        nc.vector.tensor_scalar(out=turns_i[:], in0=a0[:], scalar1=1.0 / TWO_PI, scalar2=None, op0=ALU.mult)
+        pr = const.tile([P, NDIST + 2], F32)
+        nc.vector.tensor_copy(out=pr[:, 0:NDIST], in_=pr_b[:, 0:NDIST])
         turns = const.tile([P, NPHI], F32)
         nc.vector.tensor_copy(out=turns[:], in_=turns_i[:])
-        ra = const.tile([P, NPHI], F32)
-        nc.vector.scalar_tensor_tensor(out=ra[:], in0=turns[:], scalar=-TWO_PI_HI, in1=ph[:], op0=ALU.mult, op1=ALU.add)
-        rb = const.tile([P, NPHI], F32)
-        nc.vector.scalar_tensor_tensor(out=rb[:], in0=turns[:], scalar=-TWO_PI_LO, in1=ra[:], op0=ALU.mult, op1=ALU.add)
-        over = const.tile([P, NPHI], F32)
-        nc.vector.tensor_scalar(out=over[:], in0=rb[:], scalar1=math.pi, scalar2=None, op0=ALU.is_gt)
-        under = const.tile([P, NPHI], F32)
-        nc.vector.tensor_scalar(out=under[:], in0=rb[:], scalar1=-math.pi, scalar2=None, op0=ALU.is_lt)
-        rc = const.tile([P, NPHI], F32)
-        nc.vector.scalar_tensor_tensor(out=rc[:], in0=over[:], scalar=-TWO_PI, in1=rb[:], op0=ALU.mult, op1=ALU.add)
-        ang = const.tile([P, 2 * NPHI], F32)
-        nc.vector.scalar_tensor_tensor(out=ang[:, 0:NPHI], in0=under[:], scalar=TWO_PI, in1=rc[:], op0=ALU.mult, op1=ALU.add)
-        rneg = const.tile([P, NPHI], F32)
-        nc.vector.tensor_scalar(out=rneg[:], in0=ang[:, 0:NPHI], scalar1=-1.0, scalar2=None, op0=ALU.mult)
-        rabs = const.tile([P, NPHI], F32)
-        nc.vector.tensor_tensor(out=rabs[:], in0=ang[:, 0:NPHI], in1=rneg[:], op=ALU.max)
-        nc.vector.tensor_scalar(
-            out=ang[:, NPHI : 2 * NPHI], in0=rabs[:], scalar1=-1.0, scalar2=0.5 * math.pi, op0=ALU.mult, op1=ALU.add
-        )
-        trig = const.tile([P, 2 * NPHI], F32)
-        nc.scalar.activation(out=trig[:], in_=ang[:], func=ACT.Sin)
-
-        pr = const.tile([P, NDIST + 2], F32)
-        nc.vector.tensor_copy(out=pr[:, 0:NDIST], in_=dp_b[:])
         nc.vector.tensor_copy(out=pr[:, NDIST : NDIST + 2], in_=sp_b[:])
+        a1 = const.tile([P, NPHI], F32)
+        nc.vector.scalar_tensor_tensor(out=a1[:], in0=turns[:], scalar=-TWO_PI_HI, in1=a0[:], op0=ALU.mult, op1=ALU.add)
         th = const.tile([P, NDIST + 2], F32)
         nc.scalar.activation(out=th[:], in_=pr[:], func=ACT.Tanh, scale=0.5)
+        a2 = const.tile([P, NPHI], F32)
+        nc.vector.scalar_tensor_tensor(out=a2[:], in0=turns[:], scalar=-TWO_PI_LO, in1=a1[:], op0=ALU.mult, op1=ALU.add)
+        over = const.tile([P, NPHI], F32)
+        nc.vector.tensor_scalar(
+            out=over[:], in0=a2[:], scalar1=math.pi, scalar2=-TWO_PI, op0=ALU.is_gt, op1=ALU.mult
+        )
+        under = const.tile([P, NPHI], F32)
+        nc.vector.tensor_scalar(
+            out=under[:], in0=a2[:], scalar1=-math.pi, scalar2=TWO_PI, op0=ALU.is_lt, op1=ALU.mult
+        )
+        a3 = const.tile([P, NPHI], F32)
+        nc.vector.tensor_tensor(out=a3[:], in0=over[:], in1=a2[:], op=ALU.add)
         ds = const.tile([P, NDIST + 2], F32)
         nc.vector.tensor_scalar(out=ds[:], in0=th[:], scalar1=1.0, scalar2=None, op0=ALU.add)
+        ang = const.tile([P, NPHI], F32)
+        nc.vector.tensor_tensor(out=ang[:], in0=under[:], in1=a3[:], op=ALU.add)
+        trig = const.tile([P, NPHI], F32)
+        nc.scalar.activation(out=trig[:], in_=ang[:], func=ACT.Sin)
         m2d = const.tile([P, NDIST], F32)
         nc.vector.tensor_scalar(out=m2d[:], in0=ds[:, 0:NDIST], scalar1=-2.0, scalar2=None, op0=ALU.mult)
         d2 = const.tile([P, NDIST], F32)
         nc.vector.tensor_tensor(out=d2[:], in0=ds[:, 0:NDIST], in1=ds[:, 0:NDIST], op=ALU.mult)
+
+        r2_t = {}
+
+        def squares(half):
+            cps = ps_w.tile([P, T, 2, 64], BF16, tag="wps", name="cps")
+            view = ccb[half][:].rearrange("q (p t) -> q t p", t=T)
+            for t in range(T):
+                nc.tensor.transpose(
+                    out=cps[:, t, :, :].rearrange("p c o -> p (c o)"), in_=view[:, t, :], identity=identb[:]
+                )
+            sq = work.tile([P, T, 2, 64], F32, name="sq")
+            nc.scalar.activation(
+                out=sq[:].rearrange("p t c o -> p (t c o)"),
+                in_=cps[:].rearrange("p t c o -> p (t c o)"),
+                func=ACT.Square,
+            )
+            return sq
+
+        def add_squares(engine, half, sq):
+            r2_t[half] = const.tile([P, 64, 2, 2], F32, name="r2_%d" % half)
+            engine.tensor_tensor(
+                out=r2_t[half][:],
+                in0=sq[:, :, 0, :].rearrange("p (l h) o -> p o h l", h=2),
+                in1=sq[:, :, 1, :].rearrange("p (l h) o -> p o h l", h=2),
+                op=ALU.add,
+            )
+
+        sq0 = squares(0)
+        nc.scalar.activation(out=warm[:, 1:2], in_=seed[:], func=ACT.Exp)
+
+        hi = const.tile([P, NPHI], BF16)
+        nc.vector.tensor_copy(out=hi[:], in_=trig[:])
         sg = const.tile([P, 2], F32)
         nc.vector.tensor_scalar(out=sg[:], in0=ds[:, NDIST : NDIST + 2], scalar1=1e-10, scalar2=None, op0=ALU.max)
+        rest1 = const.tile([P, NPHI], F32)
+        nc.vector.tensor_tensor(out=rest1[:], in0=trig[:], in1=hi[:], op=ALU.subtract)
+        add_squares(nc.vector, 0, sq0)
         sg2 = const.tile([P, 2], F32)
         nc.vector.tensor_tensor(out=sg2[:], in0=sg[:], in1=sg[:], op=ALU.mult)
+        mid = const.tile([P, NPHI], BF16)
+        nc.vector.tensor_copy(out=mid[:], in_=rest1[:])
+        piece0 = const.tile([P, NPHI], F32)
+        nc.vector.tensor_scalar(out=piece0[:], in0=hi[:], scalar1=mask[:, 0:1], scalar2=None, op0=ALU.mult)
+        rest2 = const.tile([P, NPHI], F32)
+        nc.vector.tensor_tensor(out=rest2[:], in0=rest1[:], in1=mid[:], op=ALU.subtract)
+        piece1 = const.tile([P, NPHI], F32)
+        nc.vector.scalar_tensor_tensor(
+            out=piece1[:], in0=mid[:], scalar=mask[:, 1:2], in1=piece0[:], op0=ALU.mult, op1=ALU.add
+        )
         rsg = const.tile([P, 2], F32)
         nc.vector.reciprocal(out=rsg[:], in_=sg2[:])
+        piece2 = const.tile([P, NPHI], F32)
+        nc.vector.scalar_tensor_tensor(
+            out=piece2[:], in0=rest2[:], scalar=mask[:, 2:3], in1=piece1[:], op0=ALU.mult, op1=ALU.add
+        )
         na = const.tile([P, 2], F32)
         nc.vector.tensor_scalar(out=na[:], in0=rsg[:], scalar1=-0.5, scalar2=None, op0=ALU.mult)
-
-        bsd = const.tile([P, 2, NDIST], F32)
-        nc.vector.tensor_tensor(
-            out=bsd[:],
-            in0=d2[:].unsqueeze(1).to_broadcast([P, 2, NDIST]),
-            in1=na[:].unsqueeze(2).to_broadcast([P, 2, NDIST]),
-            op=ALU.mult,
-        )
-        brow = const.tile([P, 2, 2, NDIST, NPHI], F32)
-        for l in range(2):
-            nc.vector.tensor_copy(
-                out=brow[:, :, l, :, :], in_=bsd[:].unsqueeze(3).to_broadcast([P, 2, NDIST, NPHI])
-            )
-        bps = ps_small.tile([P, 2, P], F32, tag="small")
-        for s in range(2):
-            nc.tensor.transpose(
-                out=bps[:, s, :], in_=brow[:, s, :, :, :].rearrange("p l d f -> p (l d f)"), identity=identf[:]
-            )
-        biasc = const.tile([P, 2], F32)
-        nc.vector.tensor_copy(out=biasc[:], in_=bps[:, :, 0:1].rearrange("q s o -> q (s o)"))
-
-        cps = ps_small.tile([P, 2, 4, 2, 64], BF16, tag="small")
-        for half in range(2):
-            view = ccb[half][:].rearrange("q (p j) -> q j p", j=4)
-            for j in range(4):
-                nc.tensor.transpose(
-                    out=cps[:, half, j, :, :].rearrange("p c o -> p (c o)"), in_=view[:, j, :], identity=identb[:]
-                )
-        cxy = const.tile([P, 2, NODES, 4], F32)
-        for half in range(2):
-            nc.vector.tensor_copy(
-                out=cxy[:, :, half * 64 : (half + 1) * 64, :],
-                in_=cps[:, half, :, :, :].rearrange("p j c o -> p c o j"),
-            )
-        ccf = [const.tile([P, 4, P], F32, name="ccf%d" % half) for half in range(2)]
-        for half in range(2):
-            nc.vector.tensor_copy(out=ccf[half][:], in_=ccb[half][:].rearrange("q (p j) -> q j p", j=4))
-        trg = const.tile([P, NPHI], F32)
-        nc.vector.tensor_copy(out=trg[0:64, :], in_=trig[0:64, NPHI : 2 * NPHI])
-        nc.vector.tensor_copy(out=trg[64:128, :], in_=trig[64:128, 0:NPHI])
-        proj = const.tile([P, 64, NPHI], F32)
+        proj = const.tile([P, GN, NPHI], BF16)
         nc.vector.tensor_tensor(
             out=proj[:],
-            in0=qsum[:, 0, :].unsqueeze(2).to_broadcast([P, 64, NPHI]),
-            in1=trg[:].unsqueeze(1).to_broadcast([P, 64, NPHI]),
+            in0=same[:].unsqueeze(2).to_broadcast([P, GN, NPHI]),
+            in1=piece2[:].unsqueeze(1).to_broadcast([P, GN, NPHI]),
             op=ALU.mult,
         )
-        sq = const.tile([P, 2, NODES * 4], F32)
-        cflat = cxy[:].rearrange("p c o j -> p c (o j)")
-        nc.vector.tensor_tensor(out=sq[:], in0=cflat, in1=cflat, op=ALU.mult)
-        r2 = const.tile([P, NODES * 4], F32)
-        nc.vector.tensor_tensor(out=r2[:], in0=sq[:, 0, :], in1=sq[:, 1, :], op=ALU.add)
+        d2_of = const.tile([P, NDIST], F32)
+        nc.vector.tensor_tensor(out=d2_of[:], in0=pick[:], in1=d2[:], op=ALU.mult)
+        d2_q = const.tile([P, 1], F32)
+        nc.vector.reduce_sum(out=d2_q[:], in_=d2_of[:], axis=AXES.X)
+        bias = const.tile([P, 2], F32)
+        nc.vector.tensor_scalar(out=bias[:], in0=na[:], scalar1=d2_q[:, 0:1], scalar2=None, op0=ALU.mult)
 
+        xr_t, xg_t, xq_t, xs_t, ups_t, ta_t, tcp_t, gc_t, part_t = {}, {}, {}, {}, {}, {}, {}, {}, {}
+        stot_t, den_t, inv_t, wc_t, wps_t, wsb_t, ops_t, osb_t = {}, {}, {}, {}, {}, {}, {}, {}
 
-        xr_t, xq_t, xs_t, ta_t, gc_t, sp_t, inv_t, wc_t, wsb_t, wq_t, ws_t, osb_t, tcp_t, ops_t = (
-            {}, {}, {}, {}, {}, {}, {}, {}, {}, {}, {}, {}, {}, {},
-        )
+        fold = const.tile([P, 2, 64], F32)
+        perm = const.tile([P, P], F32)
+        UNITS = BN
+        wq = [const.tile([P, UNITS * 192], U32, align_bytes=64, name="wq%d" % i) for i in range(2)]
+        ws = [const.tile([P, UNITS * 192], U8, align_bytes=64, name="ws%d" % i) for i in range(2)]
+
+        def late_constants():
+            nc.vector.tensor_tensor(
+                out=fold[:],
+                in0=identf[:, 0:64].unsqueeze(1).to_broadcast([P, 2, 64]),
+                in1=identf[:, 64:128].unsqueeze(1).to_broadcast([P, 2, 64]),
+                op=ALU.add,
+            )
+            nc.vector.tensor_copy(
+                out=perm[:].rearrange("q (f d l) -> q f d l", f=NPHI, d=NDIST),
+                in_=identf[:].rearrange("q (l d f) -> q f d l", l=2, d=NDIST),
+            )
+
+        def zero_runs():
+            for i in range(2):
+                nc.gpsimd.memset(
+                    wq[i][:].bitcast(F32).rearrange("p (u w) -> p u w", u=UNITS)[:, :, 64:128], 0.0
+                )
+                nc.gpsimd.memset(
+                    ws[i][:].bitcast(F32).rearrange("p (u w) -> p u w", u=UNITS)[:, :, 16:32], 0.0
+                )
 
         def live(n):
             return 0 <= n < BLOCKS
 
         def load_x(n):
-            xr = xin.tile([P, BATCH, NB, 4 * CH], BF16, name="xr")
-            xr_t[n] = xr
-            for half in range(NB // 4):
-                lo = half * 4
+            xr_t[n] = xin.tile([P, BATCH, BN, T * CH], BF16, name="xr")
+            for lo in range(0, BN, 4):
                 for b in range(BATCH):
-                    nc.sync.dma_start(out=xr[:, b, lo : lo + 4, :], in_=xv[b, :, n * NB + lo : n * NB + lo + 4, :])
-
-        xg_t = {}
+                    nc.sync.dma_start(
+                        out=xr_t[n][:, b, lo : lo + 4, :], in_=xv[b, :, n * BN + lo : n * BN + lo + 4, :]
+                    )
 
         def interleave_on_gpsimd(n):
-            xg_t[n] = xgp.tile([P, NB, BATCH, CH, 4], BF16, align_bytes=64, name="xg")
+            xg_t[n] = xgp.tile([P, BN, BATCH, CH, T], BF16, align_bytes=64, name="xg")
             for b in range(0, 2):
-                nc.gpsimd.tensor_scalar(
-                    out=xg_t[n][:, :, b, :, :],
-                    in0=xr_t[n][:, b, :, :].rearrange("p o (t c) -> p o c t", t=4),
-                    scalar1=1.0,
-                    scalar2=0.0,
+                nc.gpsimd.tensor_copy(
+                    out=xg_t[n][:, :, b, :, :], in_=xr_t[n][:, b, :, :].rearrange("p o (t c) -> p o c t", t=T)
+                )
+
+        def interleave_on_vector(n, b):
+            nc.vector.tensor_copy(
+                out=xg_t[n][:, :, b, :, :].rearrange("p o (g i) t -> p o g t i", i=4),
+                in_=xr_t[n][:, b, :, :].rearrange("p o (t g i) -> p o g t i", t=T, i=4),
+            )
+
+        def quantise_x(n):
+            xq_t[n] = work.tile([P, BN * P], U32, align_bytes=64, name="xq")
+            xs_t[n] = work.tile([P, BN * P], U8, align_bytes=64, name="xs")
+            nc.vector.quantize_mx(
+                out=xq_t[n][:].bitcast(FP8X4),
+                scales=xs_t[n][:],
+                in_=xg_t[n][:].rearrange("p o b c t -> p (o b c t)"),
+            )
+
+        def project(n):
+            group, first = divmod(n * BN, GN)
+            ups_t[n] = ps_s.tile([P, BN, 2, 2, NPHI], F32, tag="s", name="ups")
+            view = cg[:, group, :].rearrange("k (p t) -> k t p", t=T)
+            for h in range(2):
+                for l in range(2):
+                    nc.tensor.matmul(
+                        out=ups_t[n][:, :, h, l, :],
+                        lhsT=view[:, 2 * l + h, :],
+                        rhs=proj[:, first : first + BN, :],
+                        start=True,
+                        stop=True,
+                    )
+
+        def distances(n, lo=0, hi_o=BN):
+            if lo == 0:
+                ta_t[n] = work.tile([P, BN, 2, 2, NDIST, NPHI], F32, name="ta")
+            half, first = divmod(n * BN, 64)
+            r2 = r2_t[half][:, first + lo : first + hi_o, :, :].rearrange("p o h l -> p (o h l)")
+            for d in range(NDIST):
+                nc.vector.scalar_tensor_tensor(
+                    out=ta_t[n][:, lo:hi_o, :, :, d, :].rearrange("p o h l f -> p (o h l) f"),
+                    in0=ups_t[n][:, lo:hi_o, :, :, :].rearrange("p o h l f -> p (o h l) f"),
+                    scalar=m2d[:, d : d + 1],
+                    in1=r2.unsqueeze(2).to_broadcast([P, (hi_o - lo) * T, NPHI]),
                     op0=ALU.mult,
                     op1=ALU.add,
                 )
 
-        def interleave_on_vector(n):
-            for b in range(2, BATCH):
-                nc.vector.tensor_copy(
-                    out=xg_t[n][:, :, b, :, :].rearrange("p o (g i) t -> p o g t i", i=4),
-                    in_=xr_t[n][:, b, :, :].rearrange("p o (t g i) -> p o g t i", t=4, i=4),
-                )
-
-        def quantise_x(n):
-            xg = xg_t[n]
-            xq_t[n] = work.tile([P, NB * P], U32, align_bytes=64, name="xq")
-            xs_t[n] = work.tile([P, NB * P], U8, align_bytes=64, name="xs")
-            nc.vector.quantize_mx(
-                out=xq_t[n][:].bitcast(FP8X4), scales=xs_t[n][:], in_=xg[:].rearrange("p o b c t -> p (o b c t)")
-            )
-
-        ups_t = {}
-
-        def project(n):
-            half, first = divmod(n * NB, 64)
-            ups = ps_small.tile([P, NB, 4, NPHI], F32, tag="small", name="ups")
-            ups_t[n] = ups
-            for j in range(4):
-                nc.tensor.matmul(
-                    out=ups[:, :, j, :],
-                    lhsT=ccf[half][:, j, :],
-                    rhs=proj[:, first : first + NB, :],
-                    start=True,
-                    stop=True,
-                )
-
-        def distances(n):
-            cs = slice(n * CJ, (n + 1) * CJ)
-            u = ups_t[n][:].rearrange("p o j f -> p (o j) f")
-            ta = work.tile([P, NB, 2, 2, NDIST, NPHI], F32, name="ta")
-            ta_t[n] = ta
-            tview = ta[:].rearrange("p o h l d f -> p (o h l) d f")
-            r2b = r2[:, cs].unsqueeze(2).to_broadcast([P, CJ, NPHI])
-            for d in range(NDIST):
-                nc.vector.scalar_tensor_tensor(
-                    out=tview[:, :, d, :], in0=u, scalar=m2d[:, d : d + 1], in1=r2b, op0=ALU.mult, op1=ALU.add
-                )
-
         def to_components(n, pair):
-            tcp = ps_t.tile([P, 2, 2, P], F32, name="tcp")
-            tcp_t[(n, pair)] = tcp
-            for o2 in range(2):
+            tcp_t[(n, pair)] = ps_t.tile([P, 2, 2, P], F32, tag="tcp", name="tcp")
+            for o in range(2):
                 for h in range(2):
                     nc.tensor.transpose(
-                        out=tcp[:, o2, h, :],
-                        in_=ta_t[n][:, 2 * pair + o2, h, :, :, :].rearrange("p l d f -> p (l d f)"),
+                        out=tcp_t[(n, pair)][:, o, h, :],
+                        in_=ta_t[n][:, 2 * pair + o, h, :, :, :].rearrange("p l d f -> p (l d f)"),
                         identity=identf[:],
                     )
 
         def exponentials(n, pair):
             if pair == 0:
-                gc_t[n] = work.tile([P, NB, 2, 2 * P], F32, name="gc")
-                sp_t[n] = work.tile([P, NB * 2], F32, name="spart")
-            tcp = tcp_t[(n, pair)]
-            for o2 in range(2):
-                o = 2 * pair + o2
+                gc_t[n] = work.tile([P, BN, 2, P, 2], F32, name="gc")
+                part_t[n] = work.tile([P, BN * 2], F32, name="part")
+            for o in range(2):
                 for s in range(2):
+                    col = 2 * (2 * pair + o) + s
                     nc.scalar.activation(
-                        out=gc_t[n][:, o, s, :],
-                        in_=tcp[:, o2, :, :].rearrange("q h p -> q (h p)"),
+                        out=gc_t[n][:, 2 * pair + o, s, :, :],
+                        in_=tcp_t[(n, pair)][:, o, :, :].rearrange("q h p -> q p h"),
                         func=ACT.Exp,
-                        bias=biasc[:, s : s + 1],
+                        bias=bias[:, s : s + 1],
                         scale=na[:, s : s + 1],
-                        accum_out=sp_t[n][:, 2 * o + s : 2 * o + s + 1],
+                        accum_out=part_t[n][:, col : col + 1],
                     )
 
-        stot_t = {}
-
         def sums(n):
-            stot_t[n] = ps_small.tile([P, NB * 2], F32, tag="small", name="stot")
+            stot_t[n] = ps_s.tile([P, BN * 2], F32, tag="s", name="stot")
             nc.tensor.matmul(
-                out=stot_t[n][:], lhsT=qsum[:].rearrange("q h c -> q (h c)"), rhs=sp_t[n][:], start=True, stop=True
+                out=stot_t[n][:], lhsT=fold[:].rearrange("q h c -> q (h c)"), rhs=part_t[n][:], start=True, stop=True
             )
 
-        def reciprocals(n):
-            den = work.tile([P, NB * 2], F32, name="den")
-            nc.vector.tensor_scalar(out=den[:], in0=stot_t[n][:], scalar1=1e-20, scalar2=None, op0=ALU.add)
-            inv_t[n] = work.tile([P, NB * 2], F32, name="inv")
-            nc.vector.reciprocal(out=inv_t[n][:], in_=den[:])
-            wc_t[n] = work.tile([P, NB, 2, 2 * P], BF16, name="wc")
+        def denominators(n):
+            den_t[n] = work.tile([P, BN * 2], F32, name="den")
+            nc.vector.tensor_scalar(out=den_t[n][:], in0=stot_t[n][:], scalar1=1e-20, scalar2=None, op0=ALU.add)
 
-        wps_t = {}
+        def reciprocals(n):
+            inv_t[n] = work.tile([P, BN * 2], F32, name="inv")
+            nc.vector.reciprocal(out=inv_t[n][:], in_=den_t[n][:])
+            wc_t[n] = work.tile([P, BN, 2, 2 * P], BF16, name="wc")
 
         def normalise(n, pair):
-            wps = ps_w.tile([P, 2, 64, 2, 2, 2], BF16, name="wps")
-            wps_t[(n, pair)] = wps
-            for o2 in range(2):
-                o = 2 * pair + o2
+            wps_t[(n, pair)] = ps_w.tile([P, 2, 2, P], F32, tag="wps", name="wps")
+            for o in range(2):
                 for s in range(2):
+                    node = 2 * pair + o
                     nc.vector.tensor_scalar(
-                        out=wc_t[n][:, o, s, :],
-                        in0=gc_t[n][:, o, s, :],
-                        scalar1=inv_t[n][:, 2 * o + s : 2 * o + s + 1],
+                        out=wc_t[n][:, node, s, :],
+                        in0=gc_t[n][:, node, s, :, :].rearrange("q p h -> q (p h)"),
+                        scalar1=inv_t[n][:, 2 * node + s : 2 * node + s + 1],
                         scalar2=None,
                         op0=ALU.mult,
                     )
-                    for h in range(2):
-                        nc.tensor.transpose(
-                            out=wps[:, o2, :, s, h, :], in_=wc_t[n][:, o, s, h * P : (h + 1) * P], identity=perm[:]
-                        )
+                    nc.tensor.transpose(
+                        out=wps_t[(n, pair)][:, o, s, :], in_=wc_t[n][:, node, s, :].bitcast(F32), identity=perm[:]
+                    )
 
         def weights_out(n, pair):
             if pair == 0:
-                wsb_t[n] = work.tile([P, NB, 4 * P], BF16, align_bytes=64, name="wsb")
+                wsb_t[n] = work.tile([P, BN * 4 * P], BF16, align_bytes=64, name="wsb")
+            words = wsb_t[n][:].bitcast(F32)[:, pair * 4 * P : (pair + 1) * 4 * P]
             nc.scalar.copy(
-                out=wsb_t[n][:, 2 * pair : 2 * pair + 2, :].rearrange("p o n -> p (o n)"),
-                in_=wps_t[(n, pair)][:].rearrange("p o m s h l -> p (o m s h l)"),
+                out=words.rearrange("p (s o w) -> p s o w", s=2, o=2),
+                in_=wps_t[(n, pair)][:].rearrange("p o s w -> p s o w"),
             )
 
-        def quantise_w(n):
-            wq_t[n] = work.tile([P, NB * P], U32, align_bytes=64, name="wq")
-            ws_t[n] = work.tile([P, NB * P], U8, align_bytes=64, name="ws")
-            nc.vector.quantize_mx(
-                out=wq_t[n][:].bitcast(FP8X4), scales=ws_t[n][:], in_=wsb_t[n][:].rearrange("p o n -> p (o n)")
-            )
-
-        def pool_nodes(n):
-            for quad in range(NB // 4):
-                ops = ps_o.tile([P, 4, BATCH * CH], F32, name="ops")
-                ops_t[(n, quad)] = ops
-                for i in range(4):
-                    cols = slice((quad * 4 + i) * P, (quad * 4 + i + 1) * P)
-                    nc.tensor.matmul_mx(
-                        out=ops[:, i, :],
-                        lhsT=wq_t[n][:, cols].bitcast(FP8X4),
-                        lhsT_scale=ws_t[n][:, cols],
-                        rhs=xq_t[n][:, cols].bitcast(FP8X4),
-                        rhs_scale=xs_t[n][:, cols],
-                        start=True,
-                        stop=True,
-                    )
-
-        def store(n):
-            osb = work.tile([P, NB, BATCH * CH], F32, name="osb")
-            for quad in range(NB // 4):
-                lo = quad * 4
-                nc.scalar.copy(
-                    out=osb[:, lo : lo + 4, :].rearrange("m o n -> m (o n)"),
-                    in_=ops_t[(n, quad)][:].rearrange("m o n -> m (o n)"),
+        def quantise_w(n, half):
+            first, last = half * UNITS, half * UNITS + UNITS - 1
+            run = first
+            while run <= last:
+                count = 2 if run % 2 == 1 and run < last else 1
+                word = 192 * (run // 2) + 128 * (run % 2)
+                nc.vector.quantize_mx(
+                    out=wq[n % 2][:, word : word + 64 * count].bitcast(FP8X4),
+                    scales=ws[n % 2][:, word : word + 64 * count],
+                    in_=wsb_t[n][:, run * 256 : (run + count) * 256],
                 )
-                for b in range(BATCH):
-                    nc.sync.dma_start(
-                        out=ov[b, :, n * NB + lo : n * NB + lo + 4, :], in_=osb[:, lo : lo + 4, b * CH : (b + 1) * CH]
-                    )
+                run += count
 
-        with tc.manual_schedule():
-            load_x(0)
-            load_x(1)
-            interleave_on_gpsimd(0)
-            project(0)
-            distances(0)
-            to_components(0, 0)
-            to_components(0, 1)
-            for n in range(BLOCKS + 2):
-                if live(n + 2):
-                    load_x(n + 2)
-                if live(n - 1):
-                    sums(n - 1)
-                if live(n - 2):
-                    quantise_w(n - 2)
-                    pool_nodes(n - 2)
-                if live(n + 1):
-                    project(n + 1)
-                if live(n - 1):
-                    reciprocals(n - 1)
-                    normalise(n - 1, 0)
-                if live(n):
-                    exponentials(n, 0)
-                    exponentials(n, 1)
-                for pair in range(4):
-                    if live(n - 1):
-                        weights_out(n - 1, pair)
-                    if live(n) and pair < 2:
-                        to_components(n, pair + 2)
-                    if live(n) and pair == 2:
-                        interleave_on_vector(n)
-                    if live(n - 1) and pair < 3:
-                        normalise(n - 1, pair + 1)
-                    if live(n) and pair < 2:
-                        exponentials(n, pair + 2)
-                if live(n - 2):
-                    store(n - 2)
-                if live(n):
-                    quantise_x(n)
-                if live(n + 1):
-                    interleave_on_gpsimd(n + 1)
-                    distances(n + 1)
-                    to_components(n + 1, 0)
-                    to_components(n + 1, 1)
+        def pool_nodes(n, half):
+            ops_t[(n, half)] = ps_o.tile([P, 2, 2, P], F32, name="ops")
+            for i in range(2):
+                for s in range(2):
+                    for o in range(2):
+                        pair = 2 * half + i
+                        word = 192 * (2 * pair + s) + 64 * o
+                        cols = slice((2 * pair + o) * P, (2 * pair + o + 1) * P)
+                        nc.tensor.matmul_mx(
+                            out=ops_t[(n, half)][:, i, s, :],
+                            lhsT=wq[n % 2][:, word : word + P].bitcast(FP8X4),
+                            lhsT_scale=ws[n % 2][:, word : word + P],
+                            rhs=xq_t[n][:, cols].bitcast(FP8X4),
+                            rhs_scale=xs_t[n][:, cols],
+                            start=o == 0,
+                            stop=o == 1,
+                        )
+
+        def rows_out(n, half, on_vector=False):
+            if half == 0:
+                osb_t[n] = work.tile([P, BATCH, BN // 2, 2, CH], F32, name="osb")
+            for i in range(2):
+                dst = osb_t[n][:, :, 2 * half + i, :, :]
+                src = ops_t[(n, half)][:, i, :, :].rearrange("p s (b c) -> p b s c", b=BATCH)
+                if on_vector:
+                    nc.vector.tensor_copy(out=dst, in_=src)
+                else:
+                    nc.scalar.copy(out=dst, in_=src)
+
+        def store(n, lo, hi_pair):
+            for b in range(BATCH):
+                nc.sync.dma_start(
+                    out=ov[n, b, :, lo:hi_pair, :],
+                    in_=osb_t[n][:, b, lo:hi_pair, :, :].rearrange("p i s c -> p i (s c)"),
+                )
+
+        zero_runs()
+        load_x(0)
+        project(0)
+        distances(0, 0, 4)
+        to_components(0, 0)
+        to_components(0, 1)
+        distances(0, 4, BN)
+        load_rows(1)
+        load_groups(1, GROUPS)
+        load_x(1)
+        late_constants()
+        interleave_on_gpsimd(0)
+        for n in range(BLOCKS + 2):
+            if live(n + 2):
+                load_x(n + 2)
+            if live(n - 1):
+                sums(n - 1)
+                denominators(n - 1)
+            if live(n):
+                exponentials(n, 0)
+                exponentials(n, 1)
+                to_components(n, 2)
+            if n == 0:
+                add_squares(nc.gpsimd, 1, squares(1))
+            if live(n - 2):
+                for half in range(2):
+                    quantise_w(n - 2, half)
+                    pool_nodes(n - 2, half)
+            if live(n - 1):
+                reciprocals(n - 1)
+            if live(n + 1):
+                project(n + 1)
+            if live(n):
+                interleave_on_vector(n, 2)
+                exponentials(n, 2)
+            if live(n - 1):
+                normalise(n - 1, 0)
+            if live(n):
+                to_components(n, 3)
+            if live(n - 1):
+                weights_out(n - 1, 0)
+            if live(n):
+                exponentials(n, 3)
+            if live(n - 1):
+                for pair in range(1, 4):
+                    if pair == 3 and live(n):
+                        interleave_on_vector(n, 3)
+                    normalise(n - 1, pair)
+                    weights_out(n - 1, pair)
+            elif live(n):
+                interleave_on_vector(n, 3)
+            if live(n - 2):
+                if n - 2 < BLOCKS - 1:
+                    rows_out(n - 2, 0)
+                    rows_out(n - 2, 1)
+                    store(n - 2, 0, 4)
+                else:
+                    rows_out(n - 2, 0)
+                    store(n - 2, 0, 2)
+                    rows_out(n - 2, 1, on_vector=True)
+                    store(n - 2, 2, 4)
+            if live(n):
+                quantise_x(n)
+            if live(n + 1):
+                interleave_on_gpsimd(n + 1)
+                distances(n + 1)
+                to_components(n + 1, 0)
+                to_components(n + 1, 1)

@@ -22,9 +22,7 @@ NPHI = 8
 NDIST = 8
 T = 4
 BN = 8
-GN = 16
 BLOCKS = NODES // BN
-GROUPS = NODES // GN
 CELLS = P * T
 
 FLOPS = 2 * NODES * CELLS * 128 * (BATCH * CH)
@@ -37,13 +35,14 @@ TWO_PI_LO = TWO_PI - TWO_PI_HI
 def tile_polnormal_nolayer_t_kernel(tc, x, coords_x, coords_y, phis, dists_param, sigma_param, out):
     nc = tc.nc
     xv = x.rearrange("b (o p t) u v c -> b p o (t u v c)", o=NODES, p=P, t=T)
-    ov = out.rearrange("b (n i o) v f d s c -> n b (o v f d) i (s c)", i=BN // 2, o=2)
+    ov = out.rearrange("b o v f d s c -> b (v f d s) o c")
     coords = [c.rearrange("a o i j -> (a o) (i j)") for c in (coords_x, coords_y)]
 
     with ExitStack() as ctx:
         const = ctx.enter_context(tc.tile_pool(name="const", bufs=1))
         xin = ctx.enter_context(tc.tile_pool(name="xin", bufs=4))
         xgp = ctx.enter_context(tc.tile_pool(name="xgp", bufs=1))
+        xqp = ctx.enter_context(tc.tile_pool(name="xqp", bufs=3))
         work = ctx.enter_context(tc.tile_pool(name="work", bufs=2))
         ps_s = ctx.enter_context(tc.psum_pool(name="ps_s", bufs=2))
         ps_t = ctx.enter_context(tc.psum_pool(name="ps_t", bufs=2))
@@ -55,7 +54,7 @@ def tile_polnormal_nolayer_t_kernel(tc, x, coords_x, coords_y, phis, dists_param
         pr_b = const.tile([P, NDIST + 2], BF16, name="pr_b")
         sp_b = const.tile([P, 2], BF16, name="sp_b")
         ccb = [const.tile([P, CELLS], BF16, name="ccb%d" % half) for half in range(2)]
-        cg = const.tile([P, GROUPS, CELLS], BF16)
+        ccf = [const.tile([P, T, P], F32, name="ccf%d" % half) for half in range(2)]
         nc.sync.dma_start(out=ph_b[:], in_=phis.partition_broadcast(P))
         nc.sync.dma_start(out=pr_b[:, 0:NDIST], in_=dists_param.partition_broadcast(P))
         nc.sync.dma_start(out=sp_b[:], in_=sigma_param.partition_broadcast(P))
@@ -66,15 +65,7 @@ def tile_polnormal_nolayer_t_kernel(tc, x, coords_x, coords_y, phis, dists_param
                     out=ccb[half][c * 64 : (c + 1) * 64, :], in_=coords[c][half * 64 : (half + 1) * 64, :]
                 )
 
-        def load_groups(lo, hi):
-            for c in range(2):
-                rows = coords[c][lo * GN : hi * GN, :].rearrange("(g o) n -> o g n", o=GN)
-                for piece in range(4):
-                    r = c * 64 + piece * GN
-                    nc.sync.dma_start(out=cg[r : r + GN, lo:hi, :], in_=rows)
-
         load_rows(0)
-        load_groups(0, 1)
 
         identf = const.tile([P, P], F32)
         make_identity(nc, identf[:])
@@ -84,15 +75,13 @@ def tile_polnormal_nolayer_t_kernel(tc, x, coords_x, coords_y, phis, dists_param
         nc.scalar.activation(out=warm[:, 0:1], in_=seed[:], func=ACT.Tanh)
         identb = const.tile([P, P], BF16)
         nc.vector.tensor_copy(out=identb[:], in_=identf[:])
-        same = const.tile([P, GN], F32)
-        nc.vector.tensor_reduce(
-            out=same[:], in_=identf[:].rearrange("k (j o) -> k o j", o=GN), axis=AXES.X, op=ALU.add
+        fold = const.tile([P, 2, 64], F32)
+        nc.vector.tensor_tensor(
+            out=fold[:],
+            in0=identf[:, 0:64].unsqueeze(1).to_broadcast([P, 2, 64]),
+            in1=identf[:, 64:128].unsqueeze(1).to_broadcast([P, 2, 64]),
+            op=ALU.add,
         )
-        mask = const.tile([P, 4], F32)
-        nc.vector.tensor_reduce(
-            out=mask[:], in_=identf[:].rearrange("k (c q o) -> k q c o", c=2, q=4), axis=AXES.XY, op=ALU.add
-        )
-
         pick = const.tile([P, NDIST], F32)
         nc.vector.tensor_reduce(
             out=pick[:], in_=identf[:].rearrange("q (l d f) -> q d l f", l=2, d=NDIST), axis=AXES.XY, op=ALU.add
@@ -112,6 +101,11 @@ def tile_polnormal_nolayer_t_kernel(tc, x, coords_x, coords_y, phis, dists_param
         nc.vector.scalar_tensor_tensor(out=a1[:], in0=turns[:], scalar=-TWO_PI_HI, in1=a0[:], op0=ALU.mult, op1=ALU.add)
         th = const.tile([P, NDIST + 2], F32)
         nc.scalar.activation(out=th[:], in_=pr[:], func=ACT.Tanh, scale=0.5)
+
+        def rows_to_float(half):
+            nc.scalar.copy(out=ccf[half][:], in_=ccb[half][:].rearrange("q (p t) -> q t p", t=T))
+
+        rows_to_float(0)
         a2 = const.tile([P, NPHI], F32)
         nc.vector.scalar_tensor_tensor(out=a2[:], in0=turns[:], scalar=-TWO_PI_LO, in1=a1[:], op0=ALU.mult, op1=ALU.add)
         over = const.tile([P, NPHI], F32)
@@ -164,76 +158,44 @@ def tile_polnormal_nolayer_t_kernel(tc, x, coords_x, coords_y, phis, dists_param
         sq0 = squares(0)
         nc.scalar.activation(out=warm[:, 1:2], in_=seed[:], func=ACT.Exp)
 
-        hi = const.tile([P, NPHI], BF16)
-        nc.vector.tensor_copy(out=hi[:], in_=trig[:])
+        proj = const.tile([P, 64, NPHI], F32)
+
+        def project_table(lo, hi):
+            nc.vector.tensor_tensor(
+                out=proj[:, lo:hi, :],
+                in0=fold[:, 0, lo:hi].unsqueeze(2).to_broadcast([P, hi - lo, NPHI]),
+                in1=trig[:].unsqueeze(1).to_broadcast([P, hi - lo, NPHI]),
+                op=ALU.mult,
+            )
+
+        project_table(0, BN)
         sg = const.tile([P, 2], F32)
         nc.vector.tensor_scalar(out=sg[:], in0=ds[:, NDIST : NDIST + 2], scalar1=1e-10, scalar2=None, op0=ALU.max)
-        rest1 = const.tile([P, NPHI], F32)
-        nc.vector.tensor_tensor(out=rest1[:], in0=trig[:], in1=hi[:], op=ALU.subtract)
         add_squares(nc.vector, 0, sq0)
         sg2 = const.tile([P, 2], F32)
         nc.vector.tensor_tensor(out=sg2[:], in0=sg[:], in1=sg[:], op=ALU.mult)
-        mid = const.tile([P, NPHI], BF16)
-        nc.vector.tensor_copy(out=mid[:], in_=rest1[:])
-        piece0 = const.tile([P, NPHI], F32)
-        nc.vector.tensor_scalar(out=piece0[:], in0=hi[:], scalar1=mask[:, 0:1], scalar2=None, op0=ALU.mult)
-        rest2 = const.tile([P, NPHI], F32)
-        nc.vector.tensor_tensor(out=rest2[:], in0=rest1[:], in1=mid[:], op=ALU.subtract)
-        piece1 = const.tile([P, NPHI], F32)
-        nc.vector.scalar_tensor_tensor(
-            out=piece1[:], in0=mid[:], scalar=mask[:, 1:2], in1=piece0[:], op0=ALU.mult, op1=ALU.add
-        )
-        rsg = const.tile([P, 2], F32)
-        nc.vector.reciprocal(out=rsg[:], in_=sg2[:])
-        piece2 = const.tile([P, NPHI], F32)
-        nc.vector.scalar_tensor_tensor(
-            out=piece2[:], in0=rest2[:], scalar=mask[:, 2:3], in1=piece1[:], op0=ALU.mult, op1=ALU.add
-        )
-        na = const.tile([P, 2], F32)
-        nc.vector.tensor_scalar(out=na[:], in0=rsg[:], scalar1=-0.5, scalar2=None, op0=ALU.mult)
-        proj = const.tile([P, GN, NPHI], BF16)
-        nc.vector.tensor_tensor(
-            out=proj[:],
-            in0=same[:].unsqueeze(2).to_broadcast([P, GN, NPHI]),
-            in1=piece2[:].unsqueeze(1).to_broadcast([P, GN, NPHI]),
-            op=ALU.mult,
-        )
         d2_of = const.tile([P, NDIST], F32)
         nc.vector.tensor_tensor(out=d2_of[:], in0=pick[:], in1=d2[:], op=ALU.mult)
+        rsg = const.tile([P, 2], F32)
+        nc.vector.reciprocal(out=rsg[:], in_=sg2[:])
         d2_q = const.tile([P, 1], F32)
         nc.vector.reduce_sum(out=d2_q[:], in_=d2_of[:], axis=AXES.X)
+        na = const.tile([P, 2], F32)
+        nc.vector.tensor_scalar(out=na[:], in0=rsg[:], scalar1=-0.5, scalar2=None, op0=ALU.mult)
         bias = const.tile([P, 2], F32)
         nc.vector.tensor_scalar(out=bias[:], in0=na[:], scalar1=d2_q[:, 0:1], scalar2=None, op0=ALU.mult)
 
         xr_t, xg_t, xq_t, xs_t, ups_t, ta_t, tcp_t, gc_t, part_t = {}, {}, {}, {}, {}, {}, {}, {}, {}
-        stot_t, den_t, inv_t, wc_t, wps_t, wsb_t, ops_t, osb_t = {}, {}, {}, {}, {}, {}, {}, {}
+        stot_t, den_t, inv_t, wc_t, wps_t, wsb_t, wq_t, ws_t, ops_t, osb_t = {}, {}, {}, {}, {}, {}, {}, {}, {}, {}
 
-        fold = const.tile([P, 2, 64], F32)
         perm = const.tile([P, P], F32)
-        UNITS = BN
-        wq = [const.tile([P, UNITS * 192], U32, align_bytes=64, name="wq%d" % i) for i in range(2)]
-        ws = [const.tile([P, UNITS * 192], U8, align_bytes=64, name="ws%d" % i) for i in range(2)]
 
         def late_constants():
-            nc.vector.tensor_tensor(
-                out=fold[:],
-                in0=identf[:, 0:64].unsqueeze(1).to_broadcast([P, 2, 64]),
-                in1=identf[:, 64:128].unsqueeze(1).to_broadcast([P, 2, 64]),
-                op=ALU.add,
-            )
+            project_table(BN, 64)
             nc.vector.tensor_copy(
                 out=perm[:].rearrange("q (f d l) -> q f d l", f=NPHI, d=NDIST),
                 in_=identf[:].rearrange("q (l d f) -> q f d l", l=2, d=NDIST),
             )
-
-        def zero_runs():
-            for i in range(2):
-                nc.gpsimd.memset(
-                    wq[i][:].bitcast(F32).rearrange("p (u w) -> p u w", u=UNITS)[:, :, 64:128], 0.0
-                )
-                nc.gpsimd.memset(
-                    ws[i][:].bitcast(F32).rearrange("p (u w) -> p u w", u=UNITS)[:, :, 16:32], 0.0
-                )
 
         def live(n):
             return 0 <= n < BLOCKS
@@ -260,27 +222,26 @@ def tile_polnormal_nolayer_t_kernel(tc, x, coords_x, coords_y, phis, dists_param
             )
 
         def quantise_x(n):
-            xq_t[n] = work.tile([P, BN * P], U32, align_bytes=64, name="xq")
-            xs_t[n] = work.tile([P, BN * P], U8, align_bytes=64, name="xs")
+            xq_t[n] = xqp.tile([P, BN * P], U32, align_bytes=64, name="xq")
+            xs_t[n] = xqp.tile([P, BN * P], U8, align_bytes=64, name="xs")
             nc.vector.quantize_mx(
                 out=xq_t[n][:].bitcast(FP8X4),
                 scales=xs_t[n][:],
                 in_=xg_t[n][:].rearrange("p o b c t -> p (o b c t)"),
             )
 
-        def project(n):
-            group, first = divmod(n * BN, GN)
-            ups_t[n] = ps_s.tile([P, BN, 2, 2, NPHI], F32, tag="s", name="ups")
-            view = cg[:, group, :].rearrange("k (p t) -> k t p", t=T)
-            for h in range(2):
-                for l in range(2):
-                    nc.tensor.matmul(
-                        out=ups_t[n][:, :, h, l, :],
-                        lhsT=view[:, 2 * l + h, :],
-                        rhs=proj[:, first : first + BN, :],
-                        start=True,
-                        stop=True,
-                    )
+        def project(n, h):
+            half, first = divmod(n * BN, 64)
+            if h == 0:
+                ups_t[n] = ps_s.tile([P, BN, 2, 2, NPHI], F32, tag="s", name="ups")
+            for l in range(2):
+                nc.tensor.matmul(
+                    out=ups_t[n][:, :, h, l, :],
+                    lhsT=ccf[half][:, 2 * l + h, :],
+                    rhs=proj[:, first : first + BN, :],
+                    start=True,
+                    stop=True,
+                )
 
         def distances(n, lo=0, hi_o=BN):
             if lo == 0:
@@ -339,7 +300,7 @@ def tile_polnormal_nolayer_t_kernel(tc, x, coords_x, coords_y, phis, dists_param
             wc_t[n] = work.tile([P, BN, 2, 2 * P], BF16, name="wc")
 
         def normalise(n, pair):
-            wps_t[(n, pair)] = ps_w.tile([P, 2, 2, P], F32, tag="wps", name="wps")
+            wps_t[(n, pair)] = ps_w.tile([P, 2, 64, 2, 2], F32, tag="wps", name="wps")
             for o in range(2):
                 for s in range(2):
                     node = 2 * pair + o
@@ -351,132 +312,127 @@ def tile_polnormal_nolayer_t_kernel(tc, x, coords_x, coords_y, phis, dists_param
                         op0=ALU.mult,
                     )
                     nc.tensor.transpose(
-                        out=wps_t[(n, pair)][:, o, s, :], in_=wc_t[n][:, node, s, :].bitcast(F32), identity=perm[:]
+                        out=wps_t[(n, pair)][:, o, :, s, :], in_=wc_t[n][:, node, s, :].bitcast(F32), identity=perm[:]
                     )
 
         def weights_out(n, pair):
             if pair == 0:
                 wsb_t[n] = work.tile([P, BN * 4 * P], BF16, align_bytes=64, name="wsb")
             words = wsb_t[n][:].bitcast(F32)[:, pair * 4 * P : (pair + 1) * 4 * P]
-            nc.scalar.copy(
-                out=words.rearrange("p (s o w) -> p s o w", s=2, o=2),
-                in_=wps_t[(n, pair)][:].rearrange("p o s w -> p s o w"),
-            )
+            nc.scalar.copy(out=words, in_=wps_t[(n, pair)][:].rearrange("p o m s l -> p (o m s l)"))
 
         def quantise_w(n, half):
-            first, last = half * UNITS, half * UNITS + UNITS - 1
-            run = first
-            while run <= last:
-                count = 2 if run % 2 == 1 and run < last else 1
-                word = 192 * (run // 2) + 128 * (run % 2)
-                nc.vector.quantize_mx(
-                    out=wq[n % 2][:, word : word + 64 * count].bitcast(FP8X4),
-                    scales=ws[n % 2][:, word : word + 64 * count],
-                    in_=wsb_t[n][:, run * 256 : (run + count) * 256],
-                )
-                run += count
+            if half == 0:
+                wq_t[n] = work.tile([P, BN * P], U32, align_bytes=64, name="wq")
+                ws_t[n] = work.tile([P, BN * P], U8, align_bytes=64, name="ws")
+            cols = slice(half * 4 * P, (half + 1) * 4 * P)
+            nc.vector.quantize_mx(
+                out=wq_t[n][:, cols].bitcast(FP8X4),
+                scales=ws_t[n][:, cols],
+                in_=wsb_t[n][:, half * 16 * P : (half + 1) * 16 * P],
+            )
 
         def pool_nodes(n, half):
-            ops_t[(n, half)] = ps_o.tile([P, 2, 2, P], F32, name="ops")
-            for i in range(2):
-                for s in range(2):
-                    for o in range(2):
-                        pair = 2 * half + i
-                        word = 192 * (2 * pair + s) + 64 * o
-                        cols = slice((2 * pair + o) * P, (2 * pair + o + 1) * P)
-                        nc.tensor.matmul_mx(
-                            out=ops_t[(n, half)][:, i, s, :],
-                            lhsT=wq[n % 2][:, word : word + P].bitcast(FP8X4),
-                            lhsT_scale=ws[n % 2][:, word : word + P],
-                            rhs=xq_t[n][:, cols].bitcast(FP8X4),
-                            rhs_scale=xs_t[n][:, cols],
-                            start=o == 0,
-                            stop=o == 1,
-                        )
+            ops_t[(n, half)] = ps_o.tile([P, 4, BATCH * CH], F32, name="ops")
+            for i in range(4):
+                cols = slice((half * 4 + i) * P, (half * 4 + i + 1) * P)
+                nc.tensor.matmul_mx(
+                    out=ops_t[(n, half)][:, i, :],
+                    lhsT=wq_t[n][:, cols].bitcast(FP8X4),
+                    lhsT_scale=ws_t[n][:, cols],
+                    rhs=xq_t[n][:, cols].bitcast(FP8X4),
+                    rhs_scale=xs_t[n][:, cols],
+                    start=True,
+                    stop=True,
+                )
 
         def rows_out(n, half, on_vector=False):
             if half == 0:
-                osb_t[n] = work.tile([P, BATCH, BN // 2, 2, CH], F32, name="osb")
-            for i in range(2):
-                dst = osb_t[n][:, :, 2 * half + i, :, :]
-                src = ops_t[(n, half)][:, i, :, :].rearrange("p s (b c) -> p b s c", b=BATCH)
-                if on_vector:
-                    nc.vector.tensor_copy(out=dst, in_=src)
-                else:
-                    nc.scalar.copy(out=dst, in_=src)
+                osb_t[n] = work.tile([P, BN, BATCH * CH], F32, name="osb")
+            dst = osb_t[n][:, half * 4 : half * 4 + 4, :].rearrange("m o n -> m (o n)")
+            src = ops_t[(n, half)][:].rearrange("m o n -> m (o n)")
+            if on_vector:
+                nc.vector.tensor_copy(out=dst, in_=src)
+            else:
+                nc.scalar.copy(out=dst, in_=src)
 
-        def store(n, lo, hi_pair):
+        def store(n, half):
+            lo = half * 4
             for b in range(BATCH):
                 nc.sync.dma_start(
-                    out=ov[n, b, :, lo:hi_pair, :],
-                    in_=osb_t[n][:, b, lo:hi_pair, :, :].rearrange("p i s c -> p i (s c)"),
+                    out=ov[b, :, n * BN + lo : n * BN + lo + 4, :],
+                    in_=osb_t[n][:, lo : lo + 4, b * CH : (b + 1) * CH],
                 )
 
-        zero_runs()
+        project(0, 0)
+        project(0, 1)
         load_x(0)
-        project(0)
         distances(0, 0, 4)
         to_components(0, 0)
         to_components(0, 1)
         distances(0, 4, BN)
         load_rows(1)
-        load_groups(1, GROUPS)
-        load_x(1)
         late_constants()
-        interleave_on_gpsimd(0)
+        rows_to_float(1)
+        project(1, 0)
+        project(1, 1)
+        load_x(1)
         for n in range(BLOCKS + 2):
             if live(n + 2):
                 load_x(n + 2)
-            if live(n - 1):
-                sums(n - 1)
-                denominators(n - 1)
             if live(n):
-                exponentials(n, 0)
-                exponentials(n, 1)
-                to_components(n, 2)
+                interleave_on_gpsimd(n)
             if n == 0:
                 add_squares(nc.gpsimd, 1, squares(1))
+            if live(n + 1):
+                distances(n + 1)
+            if live(n + 2):
+                project(n + 2, 0)
+                project(n + 2, 1)
+            if live(n - 1):
+                denominators(n - 1)
             if live(n - 2):
-                for half in range(2):
-                    quantise_w(n - 2, half)
-                    pool_nodes(n - 2, half)
+                quantise_w(n - 2, 0)
             if live(n - 1):
                 reciprocals(n - 1)
-            if live(n + 1):
-                project(n + 1)
             if live(n):
                 interleave_on_vector(n, 2)
+            if live(n):
+                exponentials(n, 0)
+                to_components(n, 2)
+                exponentials(n, 1)
+                to_components(n, 3)
                 exponentials(n, 2)
             if live(n - 1):
                 normalise(n - 1, 0)
-            if live(n):
-                to_components(n, 3)
-            if live(n - 1):
                 weights_out(n - 1, 0)
             if live(n):
                 exponentials(n, 3)
             if live(n - 1):
-                for pair in range(1, 4):
-                    if pair == 3 and live(n):
-                        interleave_on_vector(n, 3)
-                    normalise(n - 1, pair)
-                    weights_out(n - 1, pair)
-            elif live(n):
-                interleave_on_vector(n, 3)
+                normalise(n - 1, 1)
+                weights_out(n - 1, 1)
+            if live(n + 1):
+                to_components(n + 1, 0)
             if live(n - 2):
-                if n - 2 < BLOCKS - 1:
-                    rows_out(n - 2, 0)
-                    rows_out(n - 2, 1)
-                    store(n - 2, 0, 4)
-                else:
-                    rows_out(n - 2, 0)
-                    store(n - 2, 0, 2)
-                    rows_out(n - 2, 1, on_vector=True)
-                    store(n - 2, 2, 4)
+                quantise_w(n - 2, 1)
+                pool_nodes(n - 2, 0)
+            if live(n - 1):
+                normalise(n - 1, 2)
+                weights_out(n - 1, 2)
+            if live(n):
+                interleave_on_vector(n, 3)
+            if live(n + 1):
+                to_components(n + 1, 1)
+            if live(n):
+                sums(n)
+            if live(n - 1):
+                normalise(n - 1, 3)
+                weights_out(n - 1, 3)
+            if live(n - 2):
+                pool_nodes(n - 2, 1)
+                rows_out(n - 2, 0)
+                store(n - 2, 0)
+                rows_out(n - 2, 1, on_vector=n - 2 == BLOCKS - 1)
+                store(n - 2, 1)
             if live(n):
                 quantise_x(n)
-            if live(n + 1):
-                interleave_on_gpsimd(n + 1)
-                distances(n + 1)
-                to_components(n + 1, 0)
-                to_components(n + 1, 1)

@@ -168,7 +168,7 @@ def tile_polnormal_nolayer_t_kernel(tc, x, coords_x, coords_y, phis, dists_param
                 op=ALU.mult,
             )
 
-        project_table(0, BN)
+        project_table(0, 2 * BN)
         sg = const.tile([P, 2], F32)
         nc.vector.tensor_scalar(out=sg[:], in0=ds[:, NDIST : NDIST + 2], scalar1=1e-10, scalar2=None, op0=ALU.max)
         add_squares(nc.vector, 0, sq0)
@@ -191,7 +191,7 @@ def tile_polnormal_nolayer_t_kernel(tc, x, coords_x, coords_y, phis, dists_param
         perm = const.tile([P, P], F32)
 
         def late_constants():
-            project_table(BN, 64)
+            project_table(2 * BN, 64)
             nc.vector.tensor_copy(
                 out=perm[:].rearrange("q (f d l) -> q f d l", f=NPHI, d=NDIST),
                 in_=identf[:].rearrange("q (l d f) -> q f d l", l=2, d=NDIST),
@@ -368,25 +368,24 @@ def tile_polnormal_nolayer_t_kernel(tc, x, coords_x, coords_y, phis, dists_param
         project(0, 1)
         load_x(0)
         distances(0, 0, 4)
+        project(1, 0)
         to_components(0, 0)
         to_components(0, 1)
+        project(1, 1)
         distances(0, 4, BN)
         load_rows(1)
         late_constants()
-        rows_to_float(1)
-        project(1, 0)
-        project(1, 1)
         load_x(1)
         for n in range(BLOCKS + 2):
             if live(n + 2):
                 load_x(n + 2)
             if live(n):
                 interleave_on_gpsimd(n)
-            if n == 0:
-                add_squares(nc.gpsimd, 1, squares(1))
+            if n == 1:
+                add_squares(nc.gpsimd, 1, sq1)
             if live(n + 1):
                 distances(n + 1)
-            if live(n + 2):
+            if n > 0 and live(n + 2):
                 project(n + 2, 0)
                 project(n + 2, 1)
             if live(n - 1):
@@ -402,32 +401,40 @@ def tile_polnormal_nolayer_t_kernel(tc, x, coords_x, coords_y, phis, dists_param
                 to_components(n, 2)
                 exponentials(n, 1)
                 to_components(n, 3)
+                if n == 0:
+                    project(2, 0)
+                    project(2, 1)
                 exponentials(n, 2)
             if live(n - 1):
                 normalise(n - 1, 0)
                 weights_out(n - 1, 0)
-            if live(n):
-                exponentials(n, 3)
+            if live(n - 2):
+                quantise_w(n - 2, 1)
             if live(n - 1):
                 normalise(n - 1, 1)
                 weights_out(n - 1, 1)
-            if live(n + 1):
-                to_components(n + 1, 0)
-            if live(n - 2):
-                quantise_w(n - 2, 1)
-                pool_nodes(n - 2, 0)
+            if live(n):
+                exponentials(n, 3)
             if live(n - 1):
                 normalise(n - 1, 2)
                 weights_out(n - 1, 2)
+            if live(n + 1):
+                to_components(n + 1, 0)
+            if live(n - 2):
+                pool_nodes(n - 2, 0)
             if live(n):
                 interleave_on_vector(n, 3)
+            if live(n - 1):
+                normalise(n - 1, 3)
+                weights_out(n - 1, 3)
             if live(n + 1):
                 to_components(n + 1, 1)
             if live(n):
                 sums(n)
-            if live(n - 1):
-                normalise(n - 1, 3)
-                weights_out(n - 1, 3)
+            if n == 0:
+                sq1 = squares(1)
+            if n == 1:
+                rows_to_float(1)
             if live(n - 2):
                 pool_nodes(n - 2, 1)
                 rows_out(n - 2, 0)

@@ -210,15 +210,17 @@ def tile_polnormal_nolayer_t_kernel(tc, x, coords_x, coords_y, phis, dists_param
 
         def interleave_on_gpsimd(n):
             xg_t[n] = xgp.tile([P, BN, BATCH, CH, T], BF16, align_bytes=64, name="xg")
-            for b in range(0, 2):
+            for b, nodes in ((0, BN), (1, 4)):
                 nc.gpsimd.tensor_copy(
-                    out=xg_t[n][:, :, b, :, :], in_=xr_t[n][:, b, :, :].rearrange("p o (t c) -> p o c t", t=T)
+                    out=xg_t[n][:, 0:nodes, b, :, :],
+                    in_=xr_t[n][:, b, 0:nodes, :].rearrange("p o (t c) -> p o c t", t=T),
                 )
 
         def interleave_on_vector(n, b):
+            lo = 4 if b == 1 else 0
             nc.vector.tensor_copy(
-                out=xg_t[n][:, :, b, :, :].rearrange("p o (g i) t -> p o g t i", i=4),
-                in_=xr_t[n][:, b, :, :].rearrange("p o (t g i) -> p o g t i", t=T, i=4),
+                out=xg_t[n][:, lo:BN, b, :, :].rearrange("p o (g i) t -> p o g t i", i=4),
+                in_=xr_t[n][:, b, lo:BN, :].rearrange("p o (t g i) -> p o g t i", t=T, i=4),
             )
 
         def quantise_x(n):
@@ -396,6 +398,7 @@ def tile_polnormal_nolayer_t_kernel(tc, x, coords_x, coords_y, phis, dists_param
                 reciprocals(n - 1)
             if live(n):
                 interleave_on_vector(n, 2)
+                interleave_on_vector(n, 1)
             if live(n):
                 exponentials(n, 0)
                 to_components(n, 2)
@@ -413,30 +416,31 @@ def tile_polnormal_nolayer_t_kernel(tc, x, coords_x, coords_y, phis, dists_param
             if live(n - 1):
                 normalise(n - 1, 1)
                 weights_out(n - 1, 1)
+            if live(n - 2):
+                pool_nodes(n - 2, 0)
             if live(n):
                 exponentials(n, 3)
             if live(n - 1):
                 normalise(n - 1, 2)
                 weights_out(n - 1, 2)
-            if live(n + 1):
-                to_components(n + 1, 0)
-            if live(n - 2):
-                pool_nodes(n - 2, 0)
             if live(n):
                 interleave_on_vector(n, 3)
             if live(n - 1):
                 normalise(n - 1, 3)
                 weights_out(n - 1, 3)
             if live(n + 1):
-                to_components(n + 1, 1)
+                to_components(n + 1, 0)
             if live(n):
                 sums(n)
+            if live(n - 2):
+                pool_nodes(n - 2, 1)
+            if live(n + 1):
+                to_components(n + 1, 1)
             if n == 0:
                 sq1 = squares(1)
             if n == 1:
                 rows_to_float(1)
             if live(n - 2):
-                pool_nodes(n - 2, 1)
                 rows_out(n - 2, 0)
                 store(n - 2, 0)
                 rows_out(n - 2, 1, on_vector=n - 2 == BLOCKS - 1)

@@ -84,7 +84,7 @@ def tile_polnormal_nolayer_t_kernel(tc, x, coords_x, coords_y, phis, dists_param
         )
         pick = const.tile([P, NDIST], F32)
         nc.vector.tensor_reduce(
-            out=pick[:], in_=identf[:].rearrange("q (l d f) -> q d l f", l=2, d=NDIST), axis=AXES.XY, op=ALU.add
+            out=pick[:], in_=identf[:].rearrange("q (o d f) -> q d o f", o=2, d=NDIST), axis=AXES.XY, op=ALU.add
         )
 
         a0 = const.tile([P, NPHI], F32)
@@ -147,11 +147,11 @@ def tile_polnormal_nolayer_t_kernel(tc, x, coords_x, coords_y, phis, dists_param
             return sq
 
         def add_squares(engine, half, sq):
-            r2_t[half] = const.tile([P, 64, 2, 2], F32, name="r2_%d" % half)
+            r2_t[half] = const.tile([P, 32, T, 2], F32, name="r2_%d" % half)
             engine.tensor_tensor(
                 out=r2_t[half][:],
-                in0=sq[:, :, 0, :].rearrange("p (l h) o -> p o h l", h=2),
-                in1=sq[:, :, 1, :].rearrange("p (l h) o -> p o h l", h=2),
+                in0=sq[:, :, 0, :].rearrange("p t (r o) -> p r t o", o=2),
+                in1=sq[:, :, 1, :].rearrange("p t (r o) -> p r t o", o=2),
                 op=ALU.add,
             )
 
@@ -186,15 +186,15 @@ def tile_polnormal_nolayer_t_kernel(tc, x, coords_x, coords_y, phis, dists_param
         nc.vector.tensor_scalar(out=bias[:], in0=na[:], scalar1=d2_q[:, 0:1], scalar2=None, op0=ALU.mult)
 
         xr_t, xg_t, xq_t, xs_t, ups_t, ta_t, tcp_t, gc_t, part_t = {}, {}, {}, {}, {}, {}, {}, {}, {}
-        stot_t, den_t, inv_t, wc_t, wps_t, wsb_t, wq_t, ws_t, ops_t, osb_t = {}, {}, {}, {}, {}, {}, {}, {}, {}, {}
+        den_t, inv_t, wc_t, wps_t, wsb_t, wq_t, ws_t, ops_t, osb_t = {}, {}, {}, {}, {}, {}, {}, {}, {}
 
         perm = const.tile([P, P], F32)
 
         def late_constants():
             project_table(2 * BN, 64)
             nc.vector.tensor_copy(
-                out=perm[:].rearrange("q (f d l) -> q f d l", f=NPHI, d=NDIST),
-                in_=identf[:].rearrange("q (l d f) -> q f d l", l=2, d=NDIST),
+                out=perm[:].rearrange("q (o f d) -> q o f d", o=2, f=NPHI),
+                in_=identf[:].rearrange("q (o d f) -> q o f d", o=2, d=NDIST),
             )
 
         def live(n):
@@ -235,93 +235,89 @@ def tile_polnormal_nolayer_t_kernel(tc, x, coords_x, coords_y, phis, dists_param
         def project(n, h):
             half, first = divmod(n * BN, 64)
             if h == 0:
-                ups_t[n] = ps_s.tile([P, BN, 2, 2, NPHI], F32, tag="s", name="ups")
-            for l in range(2):
+                ups_t[n] = ps_s.tile([P, BN // 2, T, 2, NPHI], F32, tag="s", name="ups")
+            for t in (2 * h, 2 * h + 1):
                 nc.tensor.matmul(
-                    out=ups_t[n][:, :, h, l, :],
-                    lhsT=ccf[half][:, 2 * l + h, :],
+                    out=ups_t[n][:, :, t, :, :],
+                    lhsT=ccf[half][:, t, :],
                     rhs=proj[:, first : first + BN, :],
                     start=True,
                     stop=True,
                 )
 
-        def distances(n, lo=0, hi_o=BN):
+        def distances(n, lo=0, hi=BN // 2):
             if lo == 0:
-                ta_t[n] = work.tile([P, BN, 2, 2, NDIST, NPHI], F32, name="ta")
-            half, first = divmod(n * BN, 64)
-            r2 = r2_t[half][:, first + lo : first + hi_o, :, :].rearrange("p o h l -> p (o h l)")
+                ta_t[n] = work.tile([P, BN // 2, T, 2, NDIST, NPHI], F32, name="ta")
+            half, first = divmod(n * BN // 2, 32)
+            r2 = r2_t[half][:, first + lo : first + hi, :, :].rearrange("p r t o -> p (r t o)")
             for d in range(NDIST):
                 nc.vector.scalar_tensor_tensor(
-                    out=ta_t[n][:, lo:hi_o, :, :, d, :].rearrange("p o h l f -> p (o h l) f"),
-                    in0=ups_t[n][:, lo:hi_o, :, :, :].rearrange("p o h l f -> p (o h l) f"),
+                    out=ta_t[n][:, lo:hi, :, :, d, :].rearrange("p r t o f -> p (r t o) f"),
+                    in0=ups_t[n][:, lo:hi, :, :, :].rearrange("p r t o f -> p (r t o) f"),
                     scalar=m2d[:, d : d + 1],
-                    in1=r2.unsqueeze(2).to_broadcast([P, (hi_o - lo) * T, NPHI]),
+                    in1=r2.unsqueeze(2).to_broadcast([P, (hi - lo) * T * 2, NPHI]),
                     op0=ALU.mult,
                     op1=ALU.add,
                 )
 
         def to_components(n, pair):
-            tcp_t[(n, pair)] = ps_t.tile([P, 2, 2, P], F32, tag="tcp", name="tcp")
-            for o in range(2):
-                for h in range(2):
-                    nc.tensor.transpose(
-                        out=tcp_t[(n, pair)][:, o, h, :],
-                        in_=ta_t[n][:, 2 * pair + o, h, :, :, :].rearrange("p l d f -> p (l d f)"),
-                        identity=identf[:],
-                    )
+            tcp_t[(n, pair)] = ps_t.tile([P, T, P], F32, tag="tcp", name="tcp")
+            for t in range(T):
+                nc.tensor.transpose(
+                    out=tcp_t[(n, pair)][:, t, :],
+                    in_=ta_t[n][:, pair, t, :, :, :].rearrange("p o d f -> p (o d f)"),
+                    identity=identf[:],
+                )
 
         def exponentials(n, pair):
             if pair == 0:
-                gc_t[n] = work.tile([P, BN, 2, P, 2], F32, name="gc")
-                part_t[n] = work.tile([P, BN * 2], F32, name="part")
-            for o in range(2):
-                for s in range(2):
-                    col = 2 * (2 * pair + o) + s
-                    nc.scalar.activation(
-                        out=gc_t[n][:, 2 * pair + o, s, :, :],
-                        in_=tcp_t[(n, pair)][:, o, :, :].rearrange("q h p -> q p h"),
-                        func=ACT.Exp,
-                        bias=bias[:, s : s + 1],
-                        scale=na[:, s : s + 1],
-                        accum_out=part_t[n][:, col : col + 1],
-                    )
-
-        def sums(n):
-            stot_t[n] = ps_s.tile([P, BN * 2], F32, tag="s", name="stot")
-            nc.tensor.matmul(
-                out=stot_t[n][:], lhsT=fold[:].rearrange("q h c -> q (h c)"), rhs=part_t[n][:], start=True, stop=True
-            )
+                gc_t[n] = work.tile([P, BN // 2, 2, 2, P, 2], F32, name="gc")
+                part_t[n] = work.tile([P, BN], F32, name="part")
+            for s in range(2):
+                col = 2 * pair + s
+                nc.scalar.activation(
+                    out=gc_t[n][:, pair, s, :, :, :],
+                    in_=tcp_t[(n, pair)][:].rearrange("q (l h) p -> q l p h", h=2),
+                    func=ACT.Exp,
+                    bias=bias[:, s : s + 1],
+                    scale=na[:, s : s + 1],
+                    accum_out=part_t[n][:, col : col + 1],
+                )
 
         def denominators(n):
-            den_t[n] = work.tile([P, BN * 2], F32, name="den")
-            nc.vector.tensor_scalar(out=den_t[n][:], in0=stot_t[n][:], scalar1=1e-20, scalar2=None, op0=ALU.add)
+            den_t[n] = work.tile([P, BN], F32, name="den")
+            nc.vector.tensor_scalar(out=den_t[n][:], in0=part_t[n][:], scalar1=1e-20, scalar2=None, op0=ALU.add)
 
         def reciprocals(n):
-            inv_t[n] = work.tile([P, BN * 2], F32, name="inv")
+            inv_t[n] = work.tile([P, BN], F32, name="inv")
             nc.vector.reciprocal(out=inv_t[n][:], in_=den_t[n][:])
-            wc_t[n] = work.tile([P, BN, 2, 2 * P], BF16, name="wc")
+            wc_t[n] = work.tile([P, BN // 2, 2, 2, 2 * P], BF16, name="wc")
 
         def normalise(n, pair):
-            wps_t[(n, pair)] = ps_w.tile([P, 2, 64, 2, 2], F32, tag="wps", name="wps")
-            for o in range(2):
-                for s in range(2):
-                    node = 2 * pair + o
-                    nc.vector.tensor_scalar(
-                        out=wc_t[n][:, node, s, :],
-                        in0=gc_t[n][:, node, s, :, :].rearrange("q p h -> q (p h)"),
-                        scalar1=inv_t[n][:, 2 * node + s : 2 * node + s + 1],
-                        scalar2=None,
-                        op0=ALU.mult,
-                    )
+            wps_t[(n, pair)] = ps_w.tile([P, 2, 2, P], F32, tag="wps", name="wps")
+            for s in range(2):
+                nc.vector.tensor_scalar(
+                    out=wc_t[n][:, pair, s, :, :].rearrange("q l x -> q (l x)"),
+                    in0=gc_t[n][:, pair, s, :, :, :].rearrange("q l p h -> q (l p h)"),
+                    scalar1=inv_t[n][:, 2 * pair + s : 2 * pair + s + 1],
+                    scalar2=None,
+                    op0=ALU.mult,
+                )
+                for l in range(2):
                     nc.tensor.transpose(
-                        out=wps_t[(n, pair)][:, o, :, s, :], in_=wc_t[n][:, node, s, :].bitcast(F32), identity=perm[:]
+                        out=wps_t[(n, pair)][:, s, l, :],
+                        in_=wc_t[n][:, pair, s, l, :].bitcast(F32),
+                        identity=perm[:],
                     )
 
         def weights_out(n, pair):
             if pair == 0:
                 wsb_t[n] = work.tile([P, BN * 4 * P], BF16, align_bytes=64, name="wsb")
             words = wsb_t[n][:].bitcast(F32)[:, pair * 4 * P : (pair + 1) * 4 * P]
-            nc.scalar.copy(out=words, in_=wps_t[(n, pair)][:].rearrange("p o m s l -> p (o m s l)"))
+            nc.scalar.copy(
+                out=words.rearrange("p (m x) -> p m x", x=4),
+                in_=wps_t[(n, pair)][:].rearrange("p s l m -> p m (s l)"),
+            )
 
         def quantise_w(n, half):
             if half == 0:
@@ -369,12 +365,12 @@ def tile_polnormal_nolayer_t_kernel(tc, x, coords_x, coords_y, phis, dists_param
         project(0, 0)
         project(0, 1)
         load_x(0)
-        distances(0, 0, 4)
+        distances(0, 0, 2)
         project(1, 0)
         to_components(0, 0)
         to_components(0, 1)
         project(1, 1)
-        distances(0, 4, BN)
+        distances(0, 2, 4)
         load_rows(1)
         late_constants()
         load_x(1)
@@ -430,8 +426,6 @@ def tile_polnormal_nolayer_t_kernel(tc, x, coords_x, coords_y, phis, dists_param
                 weights_out(n - 1, 3)
             if live(n + 1):
                 to_components(n + 1, 0)
-            if live(n):
-                sums(n)
             if live(n - 2):
                 pool_nodes(n - 2, 1)
             if live(n + 1):

@@ -23,6 +23,9 @@ NDIST = 8
 T = 4
 BN = 8
 BLOCKS = NODES // BN
+PAIRS = BN // 2
+SUPER = 2 * BN
+G_UNIT = 20
 CELLS = P * T
 
 FLOPS = 2 * NODES * CELLS * 128 * (BATCH * CH)
@@ -34,7 +37,7 @@ TWO_PI_LO = TWO_PI - TWO_PI_HI
 
 def tile_polnormal_nolayer_t_kernel(tc, x, coords_x, coords_y, phis, dists_param, sigma_param, out):
     nc = tc.nc
-    xv = x.rearrange("b (o p t) u v c -> b p o (t u v c)", o=NODES, p=P, t=T)
+    xv = x.rearrange("b (o p t) u v c -> p o b (t u v c)", o=NODES, p=P, t=T)
     ov = out.rearrange("b o v f d s c -> b (v f d s) o c")
     coords = [c.rearrange("a o i j -> (a o) (i j)") for c in (coords_x, coords_y)]
 
@@ -44,9 +47,9 @@ def tile_polnormal_nolayer_t_kernel(tc, x, coords_x, coords_y, phis, dists_param
         xgp = ctx.enter_context(tc.tile_pool(name="xgp", bufs=1))
         xqp = ctx.enter_context(tc.tile_pool(name="xqp", bufs=3))
         work = ctx.enter_context(tc.tile_pool(name="work", bufs=2))
-        ps_s = ctx.enter_context(tc.psum_pool(name="ps_s", bufs=2))
+        ps_s = ctx.enter_context(tc.psum_pool(name="ps_s", bufs=1))
         ps_t = ctx.enter_context(tc.psum_pool(name="ps_t", bufs=2))
-        ps_w = ctx.enter_context(tc.psum_pool(name="ps_w", bufs=2))
+        ps_w = ctx.enter_context(tc.psum_pool(name="ps_w", bufs=3))
         ps_o = ctx.enter_context(tc.psum_pool(name="ps_o", bufs=2))
         ctx.enter_context(tc.manual_schedule())
 
@@ -72,16 +75,11 @@ def tile_polnormal_nolayer_t_kernel(tc, x, coords_x, coords_y, phis, dists_param
         seed = const.tile([P, 1], F32)
         nc.vector.memset(seed[:], 0.0)
         warm = const.tile([P, 2], F32)
-        nc.scalar.activation(out=warm[:, 0:1], in_=seed[:], func=ACT.Tanh)
+        nc.scalar.activation(out=warm[:, 0:1], in_=seed[:], func=ACT.Silu)
         identb = const.tile([P, P], BF16)
         nc.vector.tensor_copy(out=identb[:], in_=identf[:])
-        fold = const.tile([P, 2, 64], F32)
-        nc.vector.tensor_tensor(
-            out=fold[:],
-            in0=identf[:, 0:64].unsqueeze(1).to_broadcast([P, 2, 64]),
-            in1=identf[:, 64:128].unsqueeze(1).to_broadcast([P, 2, 64]),
-            op=ALU.add,
-        )
+        fold = const.tile([P, 64], F32)
+        nc.vector.tensor_tensor(out=fold[:], in0=identf[:, 0:64], in1=identf[:, 64:128], op=ALU.add)
         pick = const.tile([P, NDIST], F32)
         nc.vector.tensor_reduce(
             out=pick[:], in_=identf[:].rearrange("q (o d f) -> q d o f", o=2, d=NDIST), axis=AXES.XY, op=ALU.add
@@ -90,17 +88,17 @@ def tile_polnormal_nolayer_t_kernel(tc, x, coords_x, coords_y, phis, dists_param
         a0 = const.tile([P, NPHI], F32)
         nc.vector.tensor_scalar(out=a0[0:64, :], in0=ph_b[0:64, :], scalar1=0.5 * math.pi, scalar2=None, op0=ALU.add)
         nc.vector.tensor_copy(out=a0[64:128, :], in_=ph_b[64:128, :])
-        turns_i = const.tile([P, NPHI], I32)
-        nc.vector.tensor_scalar(out=turns_i[:], in0=a0[:], scalar1=1.0 / TWO_PI, scalar2=None, op0=ALU.mult)
         pr = const.tile([P, NDIST + 2], F32)
         nc.vector.tensor_copy(out=pr[:, 0:NDIST], in_=pr_b[:, 0:NDIST])
+        turns_i = const.tile([P, NPHI], I32)
+        nc.vector.tensor_scalar(out=turns_i[:], in0=a0[:], scalar1=1.0 / TWO_PI, scalar2=None, op0=ALU.mult)
+        nc.vector.tensor_copy(out=pr[:, NDIST : NDIST + 2], in_=sp_b[:])
         turns = const.tile([P, NPHI], F32)
         nc.vector.tensor_copy(out=turns[:], in_=turns_i[:])
-        nc.vector.tensor_copy(out=pr[:, NDIST : NDIST + 2], in_=sp_b[:])
-        a1 = const.tile([P, NPHI], F32)
-        nc.vector.scalar_tensor_tensor(out=a1[:], in0=turns[:], scalar=-TWO_PI_HI, in1=a0[:], op0=ALU.mult, op1=ALU.add)
         th = const.tile([P, NDIST + 2], F32)
         nc.scalar.activation(out=th[:], in_=pr[:], func=ACT.Tanh, scale=0.5)
+        a1 = const.tile([P, NPHI], F32)
+        nc.vector.scalar_tensor_tensor(out=a1[:], in0=turns[:], scalar=-TWO_PI_HI, in1=a0[:], op0=ALU.mult, op1=ALU.add)
 
         def rows_to_float(half):
             nc.scalar.copy(out=ccf[half][:], in_=ccb[half][:].rearrange("q (p t) -> q t p", t=T))
@@ -108,6 +106,8 @@ def tile_polnormal_nolayer_t_kernel(tc, x, coords_x, coords_y, phis, dists_param
         rows_to_float(0)
         a2 = const.tile([P, NPHI], F32)
         nc.vector.scalar_tensor_tensor(out=a2[:], in0=turns[:], scalar=-TWO_PI_LO, in1=a1[:], op0=ALU.mult, op1=ALU.add)
+        ds = const.tile([P, NDIST + 2], F32)
+        nc.vector.tensor_scalar(out=ds[:], in0=th[:], scalar1=1.0, scalar2=None, op0=ALU.add)
         over = const.tile([P, NPHI], F32)
         nc.vector.tensor_scalar(
             out=over[:], in0=a2[:], scalar1=math.pi, scalar2=-TWO_PI, op0=ALU.is_gt, op1=ALU.mult
@@ -116,18 +116,27 @@ def tile_polnormal_nolayer_t_kernel(tc, x, coords_x, coords_y, phis, dists_param
         nc.vector.tensor_scalar(
             out=under[:], in0=a2[:], scalar1=-math.pi, scalar2=TWO_PI, op0=ALU.is_lt, op1=ALU.mult
         )
-        a3 = const.tile([P, NPHI], F32)
-        nc.vector.tensor_tensor(out=a3[:], in0=over[:], in1=a2[:], op=ALU.add)
-        ds = const.tile([P, NDIST + 2], F32)
-        nc.vector.tensor_scalar(out=ds[:], in0=th[:], scalar1=1.0, scalar2=None, op0=ALU.add)
-        ang = const.tile([P, NPHI], F32)
-        nc.vector.tensor_tensor(out=ang[:], in0=under[:], in1=a3[:], op=ALU.add)
-        trig = const.tile([P, NPHI], F32)
-        nc.scalar.activation(out=trig[:], in_=ang[:], func=ACT.Sin)
         m2d = const.tile([P, NDIST], F32)
         nc.vector.tensor_scalar(out=m2d[:], in0=ds[:, 0:NDIST], scalar1=-2.0, scalar2=None, op0=ALU.mult)
+        a3 = const.tile([P, NPHI], F32)
+        nc.vector.tensor_tensor(out=a3[:], in0=over[:], in1=a2[:], op=ALU.add)
+        sg = const.tile([P, 2], F32)
+        nc.vector.tensor_scalar(out=sg[:], in0=ds[:, NDIST : NDIST + 2], scalar1=1e-10, scalar2=None, op0=ALU.max)
         d2 = const.tile([P, NDIST], F32)
         nc.vector.tensor_tensor(out=d2[:], in0=ds[:, 0:NDIST], in1=ds[:, 0:NDIST], op=ALU.mult)
+        ang = const.tile([P, NPHI], F32)
+        nc.vector.tensor_tensor(out=ang[:], in0=under[:], in1=a3[:], op=ALU.add)
+        sg2 = const.tile([P, 2], F32)
+        nc.vector.tensor_tensor(out=sg2[:], in0=sg[:], in1=sg[:], op=ALU.mult)
+        d2_of = const.tile([P, NDIST], F32)
+        nc.vector.tensor_tensor(out=d2_of[:], in0=pick[:], in1=d2[:], op=ALU.mult)
+        trig = const.tile([P, NPHI], F32)
+        nc.scalar.activation(out=trig[:], in_=ang[:], func=ACT.Sin)
+        d2_q = const.tile([P, 1], F32)
+        nc.vector.reduce_sum(out=d2_q[:], in_=d2_of[:], axis=AXES.X)
+        rsg = const.tile([P, 2], F32)
+        na = const.tile([P, 2], F32)
+        bias = const.tile([P, 2], F32)
 
         r2_t = {}
 
@@ -160,29 +169,19 @@ def tile_polnormal_nolayer_t_kernel(tc, x, coords_x, coords_y, phis, dists_param
 
         proj = const.tile([P, 64, NPHI], F32)
 
-        def project_table(lo, hi):
-            nc.vector.tensor_tensor(
+        def project_table(engine, lo, hi):
+            engine.tensor_tensor(
                 out=proj[:, lo:hi, :],
-                in0=fold[:, 0, lo:hi].unsqueeze(2).to_broadcast([P, hi - lo, NPHI]),
+                in0=fold[:, lo:hi].unsqueeze(2).to_broadcast([P, hi - lo, NPHI]),
                 in1=trig[:].unsqueeze(1).to_broadcast([P, hi - lo, NPHI]),
                 op=ALU.mult,
             )
 
-        project_table(0, 2 * BN)
-        sg = const.tile([P, 2], F32)
-        nc.vector.tensor_scalar(out=sg[:], in0=ds[:, NDIST : NDIST + 2], scalar1=1e-10, scalar2=None, op0=ALU.max)
-        add_squares(nc.vector, 0, sq0)
-        sg2 = const.tile([P, 2], F32)
-        nc.vector.tensor_tensor(out=sg2[:], in0=sg[:], in1=sg[:], op=ALU.mult)
-        d2_of = const.tile([P, NDIST], F32)
-        nc.vector.tensor_tensor(out=d2_of[:], in0=pick[:], in1=d2[:], op=ALU.mult)
-        rsg = const.tile([P, 2], F32)
+        project_table(nc.vector, 0, 4)
         nc.vector.reciprocal(out=rsg[:], in_=sg2[:])
-        d2_q = const.tile([P, 1], F32)
-        nc.vector.reduce_sum(out=d2_q[:], in_=d2_of[:], axis=AXES.X)
-        na = const.tile([P, 2], F32)
+        add_squares(nc.vector, 0, sq0)
         nc.vector.tensor_scalar(out=na[:], in0=rsg[:], scalar1=-0.5, scalar2=None, op0=ALU.mult)
-        bias = const.tile([P, 2], F32)
+        project_table(nc.vector, 4, SUPER)
         nc.vector.tensor_scalar(out=bias[:], in0=na[:], scalar1=d2_q[:, 0:1], scalar2=None, op0=ALU.mult)
 
         xr_t, xg_t, xq_t, xs_t, ups_t, ta_t, tcp_t, gc_t, part_t = {}, {}, {}, {}, {}, {}, {}, {}, {}
@@ -191,8 +190,8 @@ def tile_polnormal_nolayer_t_kernel(tc, x, coords_x, coords_y, phis, dists_param
         perm = const.tile([P, P], F32)
 
         def late_constants():
-            project_table(2 * BN, 64)
-            nc.vector.tensor_copy(
+            project_table(nc.gpsimd, SUPER, 64)
+            nc.gpsimd.tensor_copy(
                 out=perm[:].rearrange("q (o f d) -> q o f d", o=2, f=NPHI),
                 in_=identf[:].rearrange("q (o d f) -> q o f d", o=2, d=NDIST),
             )
@@ -201,26 +200,26 @@ def tile_polnormal_nolayer_t_kernel(tc, x, coords_x, coords_y, phis, dists_param
             return 0 <= n < BLOCKS
 
         def load_x(n):
-            xr_t[n] = xin.tile([P, BATCH, BN, T * CH], BF16, name="xr")
-            for lo in range(0, BN, 4):
-                for b in range(BATCH):
-                    nc.sync.dma_start(
-                        out=xr_t[n][:, b, lo : lo + 4, :], in_=xv[b, :, n * BN + lo : n * BN + lo + 4, :]
-                    )
+            xr_t[n] = xin.tile([P, BN, BATCH, T * CH], BF16, name="xr")
+            for o in range(BN):
+                nc.sync.dma_start(out=xr_t[n][:, o, :, :], in_=xv[:, n * BN + o, :, :])
+
+        def g_unit(n):
+            return G_UNIT if n < BLOCKS - 2 else BN * BATCH
 
         def interleave_on_gpsimd(n):
             xg_t[n] = xgp.tile([P, BN, BATCH, CH, T], BF16, align_bytes=64, name="xg")
-            for b, nodes in ((0, BN), (1, 4)):
-                nc.gpsimd.tensor_copy(
-                    out=xg_t[n][:, 0:nodes, b, :, :],
-                    in_=xr_t[n][:, b, 0:nodes, :].rearrange("p o (t c) -> p o c t", t=T),
-                )
+            if g_unit(n) == BN * BATCH:
+                return
+            nc.gpsimd.tensor_copy(
+                out=xg_t[n][:].rearrange("p o b c t -> p (o b) c t")[:, G_UNIT:, :, :],
+                in_=xr_t[n][:].rearrange("p o b (t c) -> p (o b) c t", t=T)[:, G_UNIT:, :, :],
+            )
 
-        def interleave_on_vector(n, b):
-            lo = 4 if b == 1 else 0
+        def interleave_on_vector(n):
             nc.vector.tensor_copy(
-                out=xg_t[n][:, lo:BN, b, :, :].rearrange("p o (g i) t -> p o g t i", i=4),
-                in_=xr_t[n][:, b, lo:BN, :].rearrange("p o (t g i) -> p o g t i", t=T, i=4),
+                out=xg_t[n][:].rearrange("p o b (g i) t -> p (o b) g t i", i=4)[:, 0 : g_unit(n), :, :, :],
+                in_=xr_t[n][:].rearrange("p o b (t g i) -> p (o b) g t i", t=T, i=4)[:, 0 : g_unit(n), :, :, :],
             )
 
         def quantise_x(n):
@@ -232,28 +231,28 @@ def tile_polnormal_nolayer_t_kernel(tc, x, coords_x, coords_y, phis, dists_param
                 in_=xg_t[n][:].rearrange("p o b c t -> p (o b c t)"),
             )
 
-        def project(n, h):
-            half, first = divmod(n * BN, 64)
-            if h == 0:
-                ups_t[n] = ps_s.tile([P, BN // 2, T, 2, NPHI], F32, tag="s", name="ups")
-            for t in (2 * h, 2 * h + 1):
+        def project(m, lo=0, hi=SUPER // 2):
+            half, first = divmod(m * SUPER, 64)
+            if lo == 0:
+                ups_t[m] = ps_s.tile([P, SUPER // 2, T, 2, NPHI], F32, tag="s", name="ups")
+            for t in range(T):
                 nc.tensor.matmul(
-                    out=ups_t[n][:, :, t, :, :],
+                    out=ups_t[m][:, lo:hi, t, :, :],
                     lhsT=ccf[half][:, t, :],
-                    rhs=proj[:, first : first + BN, :],
+                    rhs=proj[:, first + 2 * lo : first + 2 * hi, :],
                     start=True,
                     stop=True,
                 )
 
-        def distances(n, lo=0, hi=BN // 2):
-            if lo == 0:
-                ta_t[n] = work.tile([P, BN // 2, T, 2, NDIST, NPHI], F32, name="ta")
-            half, first = divmod(n * BN // 2, 32)
+        def distances(m, d_range, lo=0, hi=SUPER // 2):
+            if m not in ta_t:
+                ta_t[m] = work.tile([P, SUPER // 2, T, 2, NDIST, NPHI], F32, name="ta")
+            half, first = divmod(m * SUPER // 2, 32)
             r2 = r2_t[half][:, first + lo : first + hi, :, :].rearrange("p r t o -> p (r t o)")
-            for d in range(NDIST):
+            for d in d_range:
                 nc.vector.scalar_tensor_tensor(
-                    out=ta_t[n][:, lo:hi, :, :, d, :].rearrange("p r t o f -> p (r t o) f"),
-                    in0=ups_t[n][:, lo:hi, :, :, :].rearrange("p r t o f -> p (r t o) f"),
+                    out=ta_t[m][:, lo:hi, :, :, d, :].rearrange("p r t o f -> p (r t o) f"),
+                    in0=ups_t[m][:, lo:hi, :, :, :].rearrange("p r t o f -> p (r t o) f"),
                     scalar=m2d[:, d : d + 1],
                     in1=r2.unsqueeze(2).to_broadcast([P, (hi - lo) * T * 2, NPHI]),
                     op0=ALU.mult,
@@ -265,13 +264,13 @@ def tile_polnormal_nolayer_t_kernel(tc, x, coords_x, coords_y, phis, dists_param
             for t in range(T):
                 nc.tensor.transpose(
                     out=tcp_t[(n, pair)][:, t, :],
-                    in_=ta_t[n][:, pair, t, :, :, :].rearrange("p o d f -> p (o d f)"),
+                    in_=ta_t[n // 2][:, n % 2 * PAIRS + pair, t, :, :, :].rearrange("p o d f -> p (o d f)"),
                     identity=identf[:],
                 )
 
         def exponentials(n, pair):
             if pair == 0:
-                gc_t[n] = work.tile([P, BN // 2, 2, 2, P, 2], F32, name="gc")
+                gc_t[n] = work.tile([P, PAIRS, 2, 2, P, 2], F32, name="gc")
                 part_t[n] = work.tile([P, BN], F32, name="part")
             for s in range(2):
                 col = 2 * pair + s
@@ -291,9 +290,10 @@ def tile_polnormal_nolayer_t_kernel(tc, x, coords_x, coords_y, phis, dists_param
         def reciprocals(n):
             inv_t[n] = work.tile([P, BN], F32, name="inv")
             nc.vector.reciprocal(out=inv_t[n][:], in_=den_t[n][:])
-            wc_t[n] = work.tile([P, BN // 2, 2, 2, 2 * P], BF16, name="wc")
 
         def normalise(n, pair):
+            if pair == 0:
+                wc_t[n] = work.tile([P, PAIRS, 2, 2, 2 * P], BF16, name="wc")
             wps_t[(n, pair)] = ps_w.tile([P, 2, 2, P], F32, tag="wps", name="wps")
             for s in range(2):
                 nc.vector.tensor_scalar(
@@ -319,15 +319,15 @@ def tile_polnormal_nolayer_t_kernel(tc, x, coords_x, coords_y, phis, dists_param
                 in_=wps_t[(n, pair)][:].rearrange("p s l m -> p m (s l)"),
             )
 
-        def quantise_w(n, half):
-            if half == 0:
+        def quantise_w(n, lo, hi):
+            if lo == 0:
                 wq_t[n] = work.tile([P, BN * P], U32, align_bytes=64, name="wq")
                 ws_t[n] = work.tile([P, BN * P], U8, align_bytes=64, name="ws")
-            cols = slice(half * 4 * P, (half + 1) * 4 * P)
+            cols = slice(lo * P, hi * P)
             nc.vector.quantize_mx(
                 out=wq_t[n][:, cols].bitcast(FP8X4),
                 scales=ws_t[n][:, cols],
-                in_=wsb_t[n][:, half * 16 * P : (half + 1) * 16 * P],
+                in_=wsb_t[n][:, lo * 4 * P : hi * 4 * P],
             )
 
         def pool_nodes(n, half):
@@ -362,82 +362,79 @@ def tile_polnormal_nolayer_t_kernel(tc, x, coords_x, coords_y, phis, dists_param
                     in_=osb_t[n][:, lo : lo + 4, b * CH : (b + 1) * CH],
                 )
 
-        project(0, 0)
-        project(0, 1)
+        def finish(n, half, on_vector=False):
+            rows_out(n, half, on_vector)
+            store(n, half)
+
+        def when(n, stage, *args):
+            if live(n):
+                stage(n, *args)
+
+        ALL_D, LOW_D, HIGH_D = range(NDIST), range(4), range(4, NDIST)
+        project(0, 0, 2)
+        project(0, 2, 4)
         load_x(0)
-        distances(0, 0, 2)
-        project(1, 0)
-        to_components(0, 0)
-        to_components(0, 1)
-        project(1, 1)
-        distances(0, 2, 4)
         load_rows(1)
+        distances(0, ALL_D, 0, 1)
+        to_components(0, 0)
+        project(0, 4, 8)
+        distances(0, ALL_D, 1, 2)
+        to_components(0, 1)
+        interleave_on_gpsimd(0)
         late_constants()
+        distances(0, ALL_D, 2, 4)
         load_x(1)
-        for n in range(BLOCKS + 2):
-            if live(n + 2):
-                load_x(n + 2)
-            if live(n):
-                interleave_on_gpsimd(n)
+        exponentials(0, 0)
+        to_components(0, 2)
+        exponentials(0, 1)
+        to_components(0, 3)
+        distances(0, ALL_D, 4, 8)
+        load_x(2)
+        project(1)
+        exponentials(0, 2)
+        to_components(1, 0)
+        exponentials(0, 3)
+        to_components(1, 1)
+        interleave_on_vector(0)
+        quantise_x(0)
+        interleave_on_gpsimd(1)
+        distances(1, LOW_D)
+        for n in range(1, BLOCKS + 2):
+            m = n // 2 + 1
+            when(n + 2, load_x)
+            when(n - 1, denominators)
+            when(n - 2, quantise_w, 0, 4)
+            when(n - 1, reciprocals)
+            when(n - 2, quantise_w, 4, 8)
+            when(n, exponentials, 0)
+            when(n, to_components, 2)
+            when(n, exponentials, 1)
+            when(n, to_components, 3)
+            when(n, exponentials, 2)
+            when(n, exponentials, 3)
+            when(n - 1, normalise, 0)
+            when(n - 1, normalise, 1)
+            when(n - 1, normalise, 2)
+            when(n - 2, pool_nodes, 0)
+            when(n - 2, pool_nodes, 1)
+            when(n - 1, weights_out, 0)
+            when(n - 1, weights_out, 1)
+            when(n - 1, weights_out, 2)
+            when(n, interleave_on_vector)
+            when(n - 1, normalise, 3)
+            when(n - 1, weights_out, 3)
+            when(n, quantise_x)
+            when(n + 1, interleave_on_gpsimd)
+            if m < BLOCKS // 2:
+                distances(m, HIGH_D if n % 2 else LOW_D)
+            when(n + 1, to_components, 0)
+            when(n + 1, to_components, 1)
             if n == 1:
-                add_squares(nc.gpsimd, 1, sq1)
-            if live(n + 1):
-                distances(n + 1)
-            if n > 0 and live(n + 2):
-                project(n + 2, 0)
-                project(n + 2, 1)
-            if live(n - 1):
-                denominators(n - 1)
-            if live(n - 2):
-                quantise_w(n - 2, 0)
-            if live(n - 1):
-                reciprocals(n - 1)
-            if live(n):
-                interleave_on_vector(n, 2)
-                interleave_on_vector(n, 1)
-            if live(n):
-                exponentials(n, 0)
-                to_components(n, 2)
-                exponentials(n, 1)
-                to_components(n, 3)
-                if n == 0:
-                    project(2, 0)
-                    project(2, 1)
-                exponentials(n, 2)
-            if live(n - 1):
-                normalise(n - 1, 0)
-                weights_out(n - 1, 0)
-            if live(n - 2):
-                quantise_w(n - 2, 1)
-            if live(n - 1):
-                normalise(n - 1, 1)
-                weights_out(n - 1, 1)
-            if live(n - 2):
-                pool_nodes(n - 2, 0)
-            if live(n):
-                exponentials(n, 3)
-            if live(n - 1):
-                normalise(n - 1, 2)
-                weights_out(n - 1, 2)
-            if live(n):
-                interleave_on_vector(n, 3)
-            if live(n - 1):
-                normalise(n - 1, 3)
-                weights_out(n - 1, 3)
-            if live(n + 1):
-                to_components(n + 1, 0)
-            if live(n - 2):
-                pool_nodes(n - 2, 1)
-            if live(n + 1):
-                to_components(n + 1, 1)
-            if n == 0:
                 sq1 = squares(1)
-            if n == 1:
                 rows_to_float(1)
-            if live(n - 2):
-                rows_out(n - 2, 0)
-                store(n - 2, 0)
-                rows_out(n - 2, 1, on_vector=n - 2 == BLOCKS - 1)
-                store(n - 2, 1)
-            if live(n):
-                quantise_x(n)
+            if n % 2 and m + 1 < BLOCKS // 2:
+                project(m + 1)
+            if n == 2:
+                add_squares(nc.gpsimd, 1, sq1)
+            when(n - 2, finish, 0, n == BLOCKS)
+            when(n - 2, finish, 1, n >= BLOCKS - 1)

@@ -54,13 +54,10 @@ def tile_polnormal_nolayer_t_kernel(tc, x, coords_x, coords_y, phis, dists_param
         ctx.enter_context(tc.manual_schedule())
 
         ph_b = const.tile([P, NPHI], BF16)
-        pr_b = const.tile([P, NDIST + 2], BF16, name="pr_b")
+        pr_b = const.tile([P, NDIST], BF16, name="pr_b")
         sp_b = const.tile([P, 2], BF16, name="sp_b")
         ccb = [const.tile([P, CELLS], BF16, name="ccb%d" % half) for half in range(2)]
         ccf = [const.tile([P, T, P], F32, name="ccf%d" % half) for half in range(2)]
-        nc.sync.dma_start(out=ph_b[:], in_=phis.partition_broadcast(P))
-        nc.sync.dma_start(out=pr_b[:, 0:NDIST], in_=dists_param.partition_broadcast(P))
-        nc.sync.dma_start(out=sp_b[:], in_=sigma_param.partition_broadcast(P))
 
         def load_rows(half):
             for c in range(2):
@@ -68,14 +65,17 @@ def tile_polnormal_nolayer_t_kernel(tc, x, coords_x, coords_y, phis, dists_param
                     out=ccb[half][c * 64 : (c + 1) * 64, :], in_=coords[c][half * 64 : (half + 1) * 64, :]
                 )
 
+        nc.sync.dma_start(out=ph_b[:], in_=phis.partition_broadcast(P))
+        nc.sync.dma_start(out=pr_b[:], in_=dists_param.partition_broadcast(P))
         load_rows(0)
+        nc.sync.dma_start(out=sp_b[:], in_=sigma_param.partition_broadcast(P))
 
-        identf = const.tile([P, P], F32)
-        make_identity(nc, identf[:])
         seed = const.tile([P, 1], F32)
         nc.vector.memset(seed[:], 0.0)
         warm = const.tile([P, 2], F32)
         nc.scalar.activation(out=warm[:, 0:1], in_=seed[:], func=ACT.Silu)
+        identf = const.tile([P, P], F32)
+        make_identity(nc, identf[:])
         identb = const.tile([P, P], BF16)
         nc.vector.tensor_copy(out=identb[:], in_=identf[:])
         fold = const.tile([P, 64], F32)
@@ -85,58 +85,48 @@ def tile_polnormal_nolayer_t_kernel(tc, x, coords_x, coords_y, phis, dists_param
             out=pick[:], in_=identf[:].rearrange("q (o d f) -> q d o f", o=2, d=NDIST), axis=AXES.XY, op=ALU.add
         )
 
-        a0 = const.tile([P, NPHI], F32)
-        nc.vector.tensor_scalar(out=a0[0:64, :], in0=ph_b[0:64, :], scalar1=0.5 * math.pi, scalar2=None, op0=ALU.add)
-        nc.vector.tensor_copy(out=a0[64:128, :], in_=ph_b[64:128, :])
-        pr = const.tile([P, NDIST + 2], F32)
-        nc.vector.tensor_copy(out=pr[:, 0:NDIST], in_=pr_b[:, 0:NDIST])
-        turns_i = const.tile([P, NPHI], I32)
-        nc.vector.tensor_scalar(out=turns_i[:], in0=a0[:], scalar1=1.0 / TWO_PI, scalar2=None, op0=ALU.mult)
-        nc.vector.tensor_copy(out=pr[:, NDIST : NDIST + 2], in_=sp_b[:])
-        turns = const.tile([P, NPHI], F32)
-        nc.vector.tensor_copy(out=turns[:], in_=turns_i[:])
-        th = const.tile([P, NDIST + 2], F32)
-        nc.scalar.activation(out=th[:], in_=pr[:], func=ACT.Tanh, scale=0.5)
-        a1 = const.tile([P, NPHI], F32)
-        nc.vector.scalar_tensor_tensor(out=a1[:], in0=turns[:], scalar=-TWO_PI_HI, in1=a0[:], op0=ALU.mult, op1=ALU.add)
-
-        def rows_to_float(half):
-            nc.scalar.copy(out=ccf[half][:], in_=ccb[half][:].rearrange("q (p t) -> q t p", t=T))
-
-        rows_to_float(0)
-        a2 = const.tile([P, NPHI], F32)
-        nc.vector.scalar_tensor_tensor(out=a2[:], in0=turns[:], scalar=-TWO_PI_LO, in1=a1[:], op0=ALU.mult, op1=ALU.add)
-        ds = const.tile([P, NDIST + 2], F32)
-        nc.vector.tensor_scalar(out=ds[:], in0=th[:], scalar1=1.0, scalar2=None, op0=ALU.add)
-        over = const.tile([P, NPHI], F32)
-        nc.vector.tensor_scalar(
-            out=over[:], in0=a2[:], scalar1=math.pi, scalar2=-TWO_PI, op0=ALU.is_gt, op1=ALU.mult
-        )
-        under = const.tile([P, NPHI], F32)
-        nc.vector.tensor_scalar(
-            out=under[:], in0=a2[:], scalar1=-math.pi, scalar2=TWO_PI, op0=ALU.is_lt, op1=ALU.mult
-        )
-        m2d = const.tile([P, NDIST], F32)
-        nc.vector.tensor_scalar(out=m2d[:], in0=ds[:, 0:NDIST], scalar1=-2.0, scalar2=None, op0=ALU.mult)
-        a3 = const.tile([P, NPHI], F32)
-        nc.vector.tensor_tensor(out=a3[:], in0=over[:], in1=a2[:], op=ALU.add)
-        sg = const.tile([P, 2], F32)
-        nc.vector.tensor_scalar(out=sg[:], in0=ds[:, NDIST : NDIST + 2], scalar1=1e-10, scalar2=None, op0=ALU.max)
-        d2 = const.tile([P, NDIST], F32)
-        nc.vector.tensor_tensor(out=d2[:], in0=ds[:, 0:NDIST], in1=ds[:, 0:NDIST], op=ALU.mult)
-        ang = const.tile([P, NPHI], F32)
-        nc.vector.tensor_tensor(out=ang[:], in0=under[:], in1=a3[:], op=ALU.add)
-        sg2 = const.tile([P, 2], F32)
-        nc.vector.tensor_tensor(out=sg2[:], in0=sg[:], in1=sg[:], op=ALU.mult)
-        d2_of = const.tile([P, NDIST], F32)
-        nc.vector.tensor_tensor(out=d2_of[:], in0=pick[:], in1=d2[:], op=ALU.mult)
+        turns = const.tile([P, NPHI], I32)
+        rest = const.tile([P, NPHI], F32)
+        angle = const.tile([P, NPHI], F32)
         trig = const.tile([P, NPHI], F32)
-        nc.scalar.activation(out=trig[:], in_=ang[:], func=ACT.Sin)
+        th = const.tile([P, NDIST + 2], F32)
+        ds = const.tile([P, NDIST], F32)
+        m2d = const.tile([P, NDIST], F32)
+        d2 = const.tile([P, NDIST], F32)
+        d2_of = const.tile([P, NDIST], F32)
         d2_q = const.tile([P, 1], F32)
-        nc.vector.reduce_sum(out=d2_q[:], in_=d2_of[:], axis=AXES.X)
-        rsg = const.tile([P, 2], F32)
+        sg = const.tile([P, 2], F32)
+        sg2 = const.tile([P, 2], F32)
         na = const.tile([P, 2], F32)
         bias = const.tile([P, 2], F32)
+
+        def rows_to_float(copy, half):
+            copy(out=ccf[half][:], in_=ccb[half][:].rearrange("q (p t) -> q t p", t=T))
+
+        nc.vector.tensor_scalar(
+            out=turns[0:64, :], in0=ph_b[0:64, :], scalar1=1.0 / TWO_PI, scalar2=0.25, op0=ALU.mult, op1=ALU.add
+        )
+        nc.vector.tensor_scalar(
+            out=turns[64:128, :], in0=ph_b[64:128, :], scalar1=1.0 / TWO_PI, scalar2=None, op0=ALU.mult
+        )
+        nc.scalar.activation(out=th[:, 0:NDIST], in_=pr_b[:], func=ACT.Tanh, scale=0.5)
+        nc.vector.scalar_tensor_tensor(
+            out=rest[:], in0=turns[:], scalar=-TWO_PI_HI, in1=ph_b[:], op0=ALU.mult, op1=ALU.add
+        )
+        nc.scalar.activation(out=th[:, NDIST:], in_=sp_b[:], func=ACT.Tanh, scale=0.5)
+        nc.vector.tensor_scalar(out=ds[:], in0=th[:, 0:NDIST], scalar1=1.0, scalar2=None, op0=ALU.add)
+        nc.vector.scalar_tensor_tensor(
+            out=angle[:], in0=turns[:], scalar=-TWO_PI_LO, in1=rest[:], op0=ALU.mult, op1=ALU.add
+        )
+        nc.scalar.activation(out=trig[0:64, :], in_=angle[0:64, :], func=ACT.Sin, bias=0.5 * math.pi)
+        nc.scalar.activation(out=trig[64:128, :], in_=angle[64:128, :], func=ACT.Sin)
+        nc.vector.tensor_scalar(
+            out=sg[:], in0=th[:, NDIST:], scalar1=1.0, scalar2=1e-10, op0=ALU.add, op1=ALU.max
+        )
+        rows_to_float(nc.vector.tensor_copy, 0)
+        nc.vector.tensor_scalar(out=m2d[:], in0=ds[:], scalar1=-2.0, scalar2=None, op0=ALU.mult)
+        nc.vector.scalar_tensor_tensor(out=sg2[:], in0=sg[:], scalar=-2.0, in1=sg[:], op0=ALU.mult, op1=ALU.mult)
+        nc.vector.tensor_tensor(out=d2[:], in0=ds[:], in1=ds[:], op=ALU.mult)
 
         r2_t = {}
 
@@ -178,10 +168,11 @@ def tile_polnormal_nolayer_t_kernel(tc, x, coords_x, coords_y, phis, dists_param
             )
 
         project_table(nc.vector, 0, 4)
-        nc.vector.reciprocal(out=rsg[:], in_=sg2[:])
-        add_squares(nc.vector, 0, sq0)
-        nc.vector.tensor_scalar(out=na[:], in0=rsg[:], scalar1=-0.5, scalar2=None, op0=ALU.mult)
+        nc.vector.reciprocal(out=na[:], in_=sg2[:])
+        nc.vector.tensor_tensor(out=d2_of[:], in0=pick[:], in1=d2[:], op=ALU.mult)
         project_table(nc.vector, 4, SUPER)
+        nc.vector.reduce_sum(out=d2_q[:], in_=d2_of[:], axis=AXES.X)
+        add_squares(nc.vector, 0, sq0)
         nc.vector.tensor_scalar(out=bias[:], in0=na[:], scalar1=d2_q[:, 0:1], scalar2=None, op0=ALU.mult)
 
         xr_t, xg_t, xq_t, xs_t, ups_t, ta_t, tcp_t, gc_t, part_t = {}, {}, {}, {}, {}, {}, {}, {}, {}
@@ -331,7 +322,10 @@ def tile_polnormal_nolayer_t_kernel(tc, x, coords_x, coords_y, phis, dists_param
             )
 
         def pool_nodes(n, half):
-            ops_t[(n, half)] = ps_o.tile([P, 4, BATCH * CH], F32, name="ops")
+            if n == BLOCKS - 1:
+                ops_t[(n, half)] = ps_t.tile([P, 4, BATCH * CH], F32, tag="tcp", name="ops_end")
+            else:
+                ops_t[(n, half)] = ps_o.tile([P, 4, BATCH * CH], F32, name="ops")
             for i in range(4):
                 cols = slice((half * 4 + i) * P, (half * 4 + i + 1) * P)
                 nc.tensor.matmul_mx(
@@ -399,31 +393,36 @@ def tile_polnormal_nolayer_t_kernel(tc, x, coords_x, coords_y, phis, dists_param
         quantise_x(0)
         interleave_on_gpsimd(1)
         distances(1, LOW_D)
-        for n in range(1, BLOCKS + 2):
+        last = BLOCKS - 1
+        for n in range(1, BLOCKS):
             m = n // 2 + 1
             when(n + 2, load_x)
-            when(n - 1, denominators)
-            when(n - 2, quantise_w, 0, 4)
-            when(n - 1, reciprocals)
-            when(n - 2, quantise_w, 4, 8)
-            when(n, exponentials, 0)
-            when(n, to_components, 2)
-            when(n, exponentials, 1)
-            when(n, to_components, 3)
-            when(n, exponentials, 2)
-            when(n, exponentials, 3)
-            when(n - 1, normalise, 0)
-            when(n - 1, normalise, 1)
-            when(n - 1, normalise, 2)
+            denominators(n - 1)
+            if n < last:
+                when(n - 2, quantise_w, 0, 4)
+            reciprocals(n - 1)
+            if n < last:
+                when(n - 2, quantise_w, 4, 8)
+            exponentials(n, 0)
+            normalise(n - 1, 0)
+            to_components(n, 2)
+            exponentials(n, 1)
+            normalise(n - 1, 1)
+            to_components(n, 3)
+            exponentials(n, 2)
+            exponentials(n, 3)
+            normalise(n - 1, 2)
+            if n == last:
+                quantise_w(n - 2, 0, 8)
             when(n - 2, pool_nodes, 0)
             when(n - 2, pool_nodes, 1)
-            when(n - 1, weights_out, 0)
-            when(n - 1, weights_out, 1)
-            when(n - 1, weights_out, 2)
-            when(n, interleave_on_vector)
-            when(n - 1, normalise, 3)
-            when(n - 1, weights_out, 3)
-            when(n, quantise_x)
+            weights_out(n - 1, 0)
+            weights_out(n - 1, 1)
+            weights_out(n - 1, 2)
+            interleave_on_vector(n)
+            normalise(n - 1, 3)
+            weights_out(n - 1, 3)
+            quantise_x(n)
             when(n + 1, interleave_on_gpsimd)
             if m < BLOCKS // 2:
                 distances(m, HIGH_D if n % 2 else LOW_D)
@@ -431,10 +430,34 @@ def tile_polnormal_nolayer_t_kernel(tc, x, coords_x, coords_y, phis, dists_param
             when(n + 1, to_components, 1)
             if n == 1:
                 sq1 = squares(1)
-                rows_to_float(1)
+                rows_to_float(nc.scalar.copy, 1)
             if n % 2 and m + 1 < BLOCKS // 2:
                 project(m + 1)
             if n == 2:
                 add_squares(nc.gpsimd, 1, sq1)
-            when(n - 2, finish, 0, n == BLOCKS)
-            when(n - 2, finish, 1, n >= BLOCKS - 1)
+            if n < last:
+                when(n - 2, finish, 0)
+                when(n - 2, finish, 1)
+        denominators(last)
+        reciprocals(last)
+        normalise(last, 0)
+        normalise(last, 1)
+        finish(last - 2, 0, True)
+        weights_out(last, 0)
+        weights_out(last, 1)
+        normalise(last, 2)
+        finish(last - 2, 1, True)
+        weights_out(last, 2)
+        normalise(last, 3)
+        weights_out(last, 3)
+        quantise_w(last - 1, 0, 8)
+        pool_nodes(last - 1, 0)
+        pool_nodes(last - 1, 1)
+        quantise_w(last, 0, 4)
+        finish(last - 1, 0)
+        pool_nodes(last, 0)
+        quantise_w(last, 4, 8)
+        finish(last - 1, 1, True)
+        pool_nodes(last, 1)
+        finish(last, 0)
+        finish(last, 1, True)

@@ -196,7 +196,7 @@ def tile_polnormal_nolayer_t_kernel(tc, x, coords_x, coords_y, phis, dists_param
                 nc.sync.dma_start(out=xr_t[n][:, o, :, :], in_=xv[:, n * BN + o, :, :])
 
         def g_unit(n):
-            return G_UNIT if n < BLOCKS - 2 else BN * BATCH
+            return G_UNIT if n < BLOCKS - 1 else BN * BATCH
 
         def interleave_on_gpsimd(n):
             xg_t[n] = xgp.tile([P, BN, BATCH, CH, T], BF16, align_bytes=64, name="xg")
@@ -209,8 +209,8 @@ def tile_polnormal_nolayer_t_kernel(tc, x, coords_x, coords_y, phis, dists_param
 
         def interleave_on_vector(n):
             nc.vector.tensor_copy(
-                out=xg_t[n][:].rearrange("p o b (g i) t -> p (o b) g t i", i=4)[:, 0 : g_unit(n), :, :, :],
-                in_=xr_t[n][:].rearrange("p o b (t g i) -> p (o b) g t i", t=T, i=4)[:, 0 : g_unit(n), :, :, :],
+                out=xg_t[n][:].rearrange("p o b (g i) t -> p (o b) g t i", i=8)[:, 0 : g_unit(n), :, :, :],
+                in_=xr_t[n][:].rearrange("p o b (t g i) -> p (o b) g t i", t=T, i=8)[:, 0 : g_unit(n), :, :, :],
             )
 
         def quantise_x(n):
@@ -274,13 +274,17 @@ def tile_polnormal_nolayer_t_kernel(tc, x, coords_x, coords_y, phis, dists_param
                     accum_out=part_t[n][:, col : col + 1],
                 )
 
-        def denominators(n):
-            den_t[n] = work.tile([P, BN], F32, name="den")
-            nc.vector.tensor_scalar(out=den_t[n][:], in0=part_t[n][:], scalar1=1e-20, scalar2=None, op0=ALU.add)
+        def denominators(n, lo=0, hi=BN):
+            if lo == 0:
+                den_t[n] = work.tile([P, BN], F32, name="den")
+            nc.vector.tensor_scalar(
+                out=den_t[n][:, lo:hi], in0=part_t[n][:, lo:hi], scalar1=1e-20, scalar2=None, op0=ALU.add
+            )
 
-        def reciprocals(n):
-            inv_t[n] = work.tile([P, BN], F32, name="inv")
-            nc.vector.reciprocal(out=inv_t[n][:], in_=den_t[n][:])
+        def reciprocals(n, lo=0, hi=BN):
+            if lo == 0:
+                inv_t[n] = work.tile([P, BN], F32, name="inv")
+            nc.vector.reciprocal(out=inv_t[n][:, lo:hi], in_=den_t[n][:, lo:hi])
 
         def normalise(n, pair):
             if pair == 0:
@@ -394,15 +398,13 @@ def tile_polnormal_nolayer_t_kernel(tc, x, coords_x, coords_y, phis, dists_param
         interleave_on_gpsimd(1)
         distances(1, LOW_D)
         last = BLOCKS - 1
-        for n in range(1, BLOCKS):
+        for n in range(1, last):
             m = n // 2 + 1
             when(n + 2, load_x)
             denominators(n - 1)
-            if n < last:
-                when(n - 2, quantise_w, 0, 4)
+            when(n - 2, quantise_w, 0, 4)
             reciprocals(n - 1)
-            if n < last:
-                when(n - 2, quantise_w, 4, 8)
+            when(n - 2, quantise_w, 4, 8)
             exponentials(n, 0)
             normalise(n - 1, 0)
             to_components(n, 2)
@@ -412,8 +414,6 @@ def tile_polnormal_nolayer_t_kernel(tc, x, coords_x, coords_y, phis, dists_param
             exponentials(n, 2)
             exponentials(n, 3)
             normalise(n - 1, 2)
-            if n == last:
-                quantise_w(n - 2, 0, 8)
             when(n - 2, pool_nodes, 0)
             when(n - 2, pool_nodes, 1)
             weights_out(n - 1, 0)
@@ -435,29 +435,52 @@ def tile_polnormal_nolayer_t_kernel(tc, x, coords_x, coords_y, phis, dists_param
                 project(m + 1)
             if n == 2:
                 add_squares(nc.gpsimd, 1, sq1)
-            if n < last:
-                when(n - 2, finish, 0)
-                when(n - 2, finish, 1)
-        denominators(last)
-        reciprocals(last)
-        normalise(last, 0)
-        normalise(last, 1)
-        finish(last - 2, 0, True)
-        weights_out(last, 0)
-        weights_out(last, 1)
-        normalise(last, 2)
-        finish(last - 2, 1, True)
-        weights_out(last, 2)
-        normalise(last, 3)
-        weights_out(last, 3)
-        quantise_w(last - 1, 0, 8)
-        pool_nodes(last - 1, 0)
-        pool_nodes(last - 1, 1)
-        quantise_w(last, 0, 4)
-        finish(last - 1, 0)
-        pool_nodes(last, 0)
-        quantise_w(last, 4, 8)
-        finish(last - 1, 1, True)
-        pool_nodes(last, 1)
-        finish(last, 0)
-        finish(last, 1, True)
+            when(n - 2, finish, 0, n == last - 1)
+            when(n - 2, finish, 1, n == last - 1)
+        n = last
+        denominators(n - 1)
+        reciprocals(n - 1)
+        exponentials(n, 0)
+        normalise(n - 1, 0)
+        to_components(n, 2)
+        exponentials(n, 1)
+        normalise(n - 1, 1)
+        to_components(n, 3)
+        normalise(n - 1, 2)
+        quantise_w(n - 2, 0, 8)
+        pool_nodes(n - 2, 0)
+        pool_nodes(n - 2, 1)
+        weights_out(n - 1, 0)
+        normalise(n - 1, 3)
+        weights_out(n - 1, 1)
+        weights_out(n - 1, 2)
+        denominators(n, 0, 4)
+        weights_out(n - 1, 3)
+        exponentials(n, 2)
+        exponentials(n, 3)
+        interleave_on_vector(n)
+        reciprocals(n, 0, 4)
+        finish(n - 2, 0, True)
+        normalise(n, 0)
+        finish(n - 2, 1, True)
+        normalise(n, 1)
+        weights_out(n, 0)
+        weights_out(n, 1)
+        quantise_w(n - 1, 0, 8)
+        pool_nodes(n - 1, 0)
+        pool_nodes(n - 1, 1)
+        denominators(n, 4, 8)
+        quantise_x(n)
+        reciprocals(n, 4, 8)
+        finish(n - 1, 0)
+        normalise(n, 2)
+        normalise(n, 3)
+        weights_out(n, 2)
+        weights_out(n, 3)
+        quantise_w(n, 0, 4)
+        pool_nodes(n, 0)
+        finish(n - 1, 1, True)
+        quantise_w(n, 4, 8)
+        pool_nodes(n, 1)
+        finish(n, 0)
+        finish(n, 1, True)

@@ -25,6 +25,7 @@ BN = 8
 BLOCKS = NODES // BN
 PAIRS = BN // 2
 SUPER = 2 * BN
+S_UNITS = 2
 G_UNIT = 20
 CELLS = P * T
 
@@ -196,7 +197,7 @@ def tile_polnormal_nolayer_t_kernel(tc, x, coords_x, coords_y, phis, dists_param
                 nc.sync.dma_start(out=xr_t[n][:, o, :, :], in_=xv[:, n * BN + o, :, :])
 
         def g_unit(n):
-            return G_UNIT if n < BLOCKS - 1 else BN * BATCH
+            return G_UNIT if n < BLOCKS - 2 else BN * BATCH
 
         def interleave_on_gpsimd(n):
             xg_t[n] = xgp.tile([P, BN, BATCH, CH, T], BF16, align_bytes=64, name="xg")
@@ -209,8 +210,14 @@ def tile_polnormal_nolayer_t_kernel(tc, x, coords_x, coords_y, phis, dists_param
 
         def interleave_on_vector(n):
             nc.vector.tensor_copy(
-                out=xg_t[n][:].rearrange("p o b (g i) t -> p (o b) g t i", i=8)[:, 0 : g_unit(n), :, :, :],
-                in_=xr_t[n][:].rearrange("p o b (t g i) -> p (o b) g t i", t=T, i=8)[:, 0 : g_unit(n), :, :, :],
+                out=xg_t[n][:].rearrange("p o b (g i) t -> p (o b) g t i", i=8)[:, S_UNITS : g_unit(n), :, :, :],
+                in_=xr_t[n][:].rearrange("p o b (t g i) -> p (o b) g t i", t=T, i=8)[:, S_UNITS : g_unit(n), :, :, :],
+            )
+
+        def interleave_on_scalar(n):
+            nc.scalar.copy(
+                out=xg_t[n][:].rearrange("p o b (g i) t -> p (o b) g t i", i=8)[:, 0:S_UNITS, :, :, :],
+                in_=xr_t[n][:].rearrange("p o b (t g i) -> p (o b) g t i", t=T, i=8)[:, 0:S_UNITS, :, :, :],
             )
 
         def quantise_x(n):
@@ -393,26 +400,55 @@ def tile_polnormal_nolayer_t_kernel(tc, x, coords_x, coords_y, phis, dists_param
         to_components(1, 0)
         exponentials(0, 3)
         to_components(1, 1)
+        interleave_on_scalar(0)
         interleave_on_vector(0)
         quantise_x(0)
         interleave_on_gpsimd(1)
         distances(1, LOW_D)
+        interleave_on_scalar(1)
+        exponentials(1, 0)
+        to_components(1, 2)
+        exponentials(1, 1)
+        to_components(1, 3)
+        denominators(0)
+        reciprocals(0)
+        exponentials(1, 2)
+        exponentials(1, 3)
+        for pair in range(PAIRS):
+            normalise(0, pair)
+            weights_out(0, pair)
+        distances(1, HIGH_D)
+        sq1 = squares(1)
+        rows_to_float(nc.scalar.copy, 1)
+        project(2)
+        to_components(2, 0)
+        to_components(2, 1)
+        interleave_on_vector(1)
+        load_x(3)
+        quantise_x(1)
+        interleave_on_gpsimd(2)
+        add_squares(nc.gpsimd, 1, sq1)
+        distances(2, LOW_D)
         last = BLOCKS - 1
-        for n in range(1, last):
-            m = n // 2 + 1
+        for n in range(2, last):
+            m, high = divmod(n + 3, 2)
             when(n + 2, load_x)
             denominators(n - 1)
             when(n - 2, quantise_w, 0, 4)
             reciprocals(n - 1)
             when(n - 2, quantise_w, 4, 8)
+            interleave_on_scalar(n)
             exponentials(n, 0)
-            normalise(n - 1, 0)
             to_components(n, 2)
             exponentials(n, 1)
-            normalise(n - 1, 1)
-            to_components(n, 3)
+            if n == 2:
+                to_components(n, 3)
+            normalise(n - 1, 0)
+            if n > 2:
+                to_components(n, 3)
             exponentials(n, 2)
             exponentials(n, 3)
+            normalise(n - 1, 1)
             normalise(n - 1, 2)
             when(n - 2, pool_nodes, 0)
             when(n - 2, pool_nodes, 1)
@@ -425,21 +461,17 @@ def tile_polnormal_nolayer_t_kernel(tc, x, coords_x, coords_y, phis, dists_param
             quantise_x(n)
             when(n + 1, interleave_on_gpsimd)
             if m < BLOCKS // 2:
-                distances(m, HIGH_D if n % 2 else LOW_D)
+                distances(m, HIGH_D if high else LOW_D)
             when(n + 1, to_components, 0)
             when(n + 1, to_components, 1)
-            if n == 1:
-                sq1 = squares(1)
-                rows_to_float(nc.scalar.copy, 1)
-            if n % 2 and m + 1 < BLOCKS // 2:
+            if high and m + 1 < BLOCKS // 2:
                 project(m + 1)
-            if n == 2:
-                add_squares(nc.gpsimd, 1, sq1)
             when(n - 2, finish, 0, n == last - 1)
             when(n - 2, finish, 1, n == last - 1)
         n = last
         denominators(n - 1)
         reciprocals(n - 1)
+        interleave_on_scalar(n)
         exponentials(n, 0)
         normalise(n - 1, 0)
         to_components(n, 2)
@@ -447,11 +479,11 @@ def tile_polnormal_nolayer_t_kernel(tc, x, coords_x, coords_y, phis, dists_param
         normalise(n - 1, 1)
         to_components(n, 3)
         normalise(n - 1, 2)
+        weights_out(n - 1, 0)
+        normalise(n - 1, 3)
         quantise_w(n - 2, 0, 8)
         pool_nodes(n - 2, 0)
         pool_nodes(n - 2, 1)
-        weights_out(n - 1, 0)
-        normalise(n - 1, 3)
         weights_out(n - 1, 1)
         weights_out(n - 1, 2)
         denominators(n, 0, 4)

@@ -54,9 +54,10 @@ def tile_polnormal_nolayer_t_kernel(tc, x, coords_x, coords_y, phis, dists_param
         ps_o = ctx.enter_context(tc.psum_pool(name="ps_o", bufs=2))
         ctx.enter_context(tc.manual_schedule())
 
-        ph_b = const.tile([P, NPHI], BF16)
-        pr_b = const.tile([P, NDIST], BF16, name="pr_b")
-        sp_b = const.tile([P, 2], BF16, name="sp_b")
+        row = const.tile([P, 3 * 16], BF16)
+        nc.vector.memset(row[:], 0.0)
+        ones = const.tile([P, P], BF16)
+        nc.vector.memset(ones[:], 1.0)
         ccb = [const.tile([P, CELLS], BF16, name="ccb%d" % half) for half in range(2)]
         ccf = [const.tile([P, T, P], F32, name="ccf%d" % half) for half in range(2)]
 
@@ -66,10 +67,9 @@ def tile_polnormal_nolayer_t_kernel(tc, x, coords_x, coords_y, phis, dists_param
                     out=ccb[half][c * 64 : (c + 1) * 64, :], in_=coords[c][half * 64 : (half + 1) * 64, :]
                 )
 
-        nc.sync.dma_start(out=ph_b[:], in_=phis.partition_broadcast(P))
-        nc.sync.dma_start(out=pr_b[:], in_=dists_param.partition_broadcast(P))
         load_rows(0)
-        nc.sync.dma_start(out=sp_b[:], in_=sigma_param.partition_broadcast(P))
+        for vec, lo, hi in ((phis, 0, NPHI), (dists_param, 16, 16 + NDIST), (sigma_param, 32, 34)):
+            nc.sync.dma_start(out=row[0:1, lo:hi], in_=vec.unsqueeze(0))
 
         seed = const.tile([P, 1], F32)
         nc.vector.memset(seed[:], 0.0)
@@ -104,17 +104,20 @@ def tile_polnormal_nolayer_t_kernel(tc, x, coords_x, coords_y, phis, dists_param
         def rows_to_float(copy, half):
             copy(out=ccf[half][:], in_=ccb[half][:].rearrange("q (p t) -> q t p", t=T))
 
+        pars = ps_o.tile([P, 3 * 16], F32, tag="ops", name="pars")
+        nc.tensor.matmul(out=pars[:], lhsT=ones[:], rhs=row[:], start=True, stop=True)
+        ph_b, pr_b, sp_b = pars[:, 0:NPHI], pars[:, 16 : 16 + NDIST], pars[:, 32:34]
         nc.vector.tensor_scalar(
             out=turns[0:64, :], in0=ph_b[0:64, :], scalar1=1.0 / TWO_PI, scalar2=0.25, op0=ALU.mult, op1=ALU.add
         )
         nc.vector.tensor_scalar(
             out=turns[64:128, :], in0=ph_b[64:128, :], scalar1=1.0 / TWO_PI, scalar2=None, op0=ALU.mult
         )
-        nc.scalar.activation(out=th[:, 0:NDIST], in_=pr_b[:], func=ACT.Tanh, scale=0.5)
+        nc.scalar.activation(out=th[:, 0:NDIST], in_=pr_b, func=ACT.Tanh, scale=0.5)
         nc.vector.scalar_tensor_tensor(
-            out=rest[:], in0=turns[:], scalar=-TWO_PI_HI, in1=ph_b[:], op0=ALU.mult, op1=ALU.add
+            out=rest[:], in0=turns[:], scalar=-TWO_PI_HI, in1=ph_b, op0=ALU.mult, op1=ALU.add
         )
-        nc.scalar.activation(out=th[:, NDIST:], in_=sp_b[:], func=ACT.Tanh, scale=0.5)
+        nc.scalar.activation(out=th[:, NDIST:], in_=sp_b, func=ACT.Tanh, scale=0.5)
         nc.vector.tensor_scalar(out=ds[:], in0=th[:, 0:NDIST], scalar1=1.0, scalar2=None, op0=ALU.add)
         nc.vector.scalar_tensor_tensor(
             out=angle[:], in0=turns[:], scalar=-TWO_PI_LO, in1=rest[:], op0=ALU.mult, op1=ALU.add
@@ -208,10 +211,11 @@ def tile_polnormal_nolayer_t_kernel(tc, x, coords_x, coords_y, phis, dists_param
                 in_=xr_t[n][:].rearrange("p o b (t c) -> p (o b) c t", t=T)[:, G_UNIT:, :, :],
             )
 
-        def interleave_on_vector(n):
+        def interleave_on_vector(n, lo=S_UNITS, hi=None):
+            hi = hi or g_unit(n)
             nc.vector.tensor_copy(
-                out=xg_t[n][:].rearrange("p o b (g i) t -> p (o b) g t i", i=8)[:, S_UNITS : g_unit(n), :, :, :],
-                in_=xr_t[n][:].rearrange("p o b (t g i) -> p (o b) g t i", t=T, i=8)[:, S_UNITS : g_unit(n), :, :, :],
+                out=xg_t[n][:].rearrange("p o b (g i) t -> p (o b) g t i", i=8)[:, lo:hi, :, :, :],
+                in_=xr_t[n][:].rearrange("p o b (t g i) -> p (o b) g t i", t=T, i=8)[:, lo:hi, :, :, :],
             )
 
         def interleave_on_scalar(n):
@@ -336,7 +340,7 @@ def tile_polnormal_nolayer_t_kernel(tc, x, coords_x, coords_y, phis, dists_param
             if n == BLOCKS - 1:
                 ops_t[(n, half)] = ps_t.tile([P, 4, BATCH * CH], F32, tag="tcp", name="ops_end")
             else:
-                ops_t[(n, half)] = ps_o.tile([P, 4, BATCH * CH], F32, name="ops")
+                ops_t[(n, half)] = ps_o.tile([P, 4, BATCH * CH], F32, tag="ops", name="ops")
             for i in range(4):
                 cols = slice((half * 4 + i) * P, (half * 4 + i + 1) * P)
                 nc.tensor.matmul_mx(
@@ -380,13 +384,15 @@ def tile_polnormal_nolayer_t_kernel(tc, x, coords_x, coords_y, phis, dists_param
         project(0, 2, 4)
         load_x(0)
         load_rows(1)
+        interleave_on_gpsimd(0)
+        interleave_on_vector(0, S_UNITS, 8)
         distances(0, ALL_D, 0, 1)
         to_components(0, 0)
         project(0, 4, 8)
         distances(0, ALL_D, 1, 2)
         to_components(0, 1)
-        interleave_on_gpsimd(0)
         late_constants()
+        interleave_on_scalar(0)
         distances(0, ALL_D, 2, 4)
         load_x(1)
         exponentials(0, 0)
@@ -400,8 +406,7 @@ def tile_polnormal_nolayer_t_kernel(tc, x, coords_x, coords_y, phis, dists_param
         to_components(1, 0)
         exponentials(0, 3)
         to_components(1, 1)
-        interleave_on_scalar(0)
-        interleave_on_vector(0)
+        interleave_on_vector(0, 8)
         quantise_x(0)
         interleave_on_gpsimd(1)
         distances(1, LOW_D)
@@ -448,10 +453,10 @@ def tile_polnormal_nolayer_t_kernel(tc, x, coords_x, coords_y, phis, dists_param
                 to_components(n, 3)
             exponentials(n, 2)
             exponentials(n, 3)
-            normalise(n - 1, 1)
-            normalise(n - 1, 2)
             when(n - 2, pool_nodes, 0)
             when(n - 2, pool_nodes, 1)
+            normalise(n - 1, 1)
+            normalise(n - 1, 2)
             weights_out(n - 1, 0)
             weights_out(n - 1, 1)
             weights_out(n - 1, 2)

@@ -28,6 +28,9 @@ SUPER = 2 * BN
 S_UNITS = 2
 G_UNIT = 20
 CELLS = P * T
+RUN = P // 2
+SPREAD = 6 * RUN
+SPREAD_FROM = BLOCKS - 2
 
 FLOPS = 2 * NODES * CELLS * 128 * (BATCH * CH)
 
@@ -40,6 +43,7 @@ def tile_polnormal_nolayer_t_kernel(tc, x, coords_x, coords_y, phis, dists_param
     nc = tc.nc
     xv = x.rearrange("b (o p t) u v c -> p o b (t u v c)", o=NODES, p=P, t=T)
     ov = out.rearrange("b o v f d s c -> b (v f d s) o c")
+    ov2 = out.rearrange("b o v f d s c -> o (v f d) b (s c)")
     coords = [c.rearrange("a o i j -> (a o) (i j)") for c in (coords_x, coords_y)]
 
     with ExitStack() as ctx:
@@ -85,6 +89,14 @@ def tile_polnormal_nolayer_t_kernel(tc, x, coords_x, coords_y, phis, dists_param
         nc.vector.tensor_reduce(
             out=pick[:], in_=identf[:].rearrange("q (o d f) -> q d o f", o=2, d=NDIST), axis=AXES.XY, op=ALU.add
         )
+
+        wide_q = [const.tile([P, PAIRS * SPREAD], U32, align_bytes=64, name="wide_q%d" % i) for i in range(2)]
+        wide_s = [const.tile([P, PAIRS * SPREAD], U8, align_bytes=64, name="wide_s%d" % i) for i in range(2)]
+        for i in range(2):
+            gaps = wide_q[i][:].rearrange("p (g k) -> p g k", k=3 * RUN)[:, :, RUN : 2 * RUN]
+            nc.gpsimd.memset(gaps, 0)
+            gaps = wide_s[i][:].bitcast(U32).rearrange("p (g k) -> p g k", k=3 * RUN // 4)
+            nc.gpsimd.memset(gaps[:, :, RUN // 4 : 2 * RUN // 4], 0)
 
         turns = const.tile([P, NPHI], I32)
         rest = const.tile([P, NPHI], F32)
@@ -320,12 +332,33 @@ def tile_polnormal_nolayer_t_kernel(tc, x, coords_x, coords_y, phis, dists_param
             if pair == 0:
                 wsb_t[n] = work.tile([P, BN * 4 * P], BF16, align_bytes=64, name="wsb")
             words = wsb_t[n][:].bitcast(F32)[:, pair * 4 * P : (pair + 1) * 4 * P]
-            nc.scalar.copy(
-                out=words.rearrange("p (m x) -> p m x", x=4),
-                in_=wps_t[(n, pair)][:].rearrange("p s l m -> p m (s l)"),
-            )
+            if n < SPREAD_FROM:
+                dst = words.rearrange("p (m x) -> p m x", x=4)
+                src = wps_t[(n, pair)][:].rearrange("p s l m -> p m (s l)")
+            else:
+                dst = words.rearrange("p (e m l) -> p e m l", e=2, l=2)
+                src = wps_t[(n, pair)][:].rearrange("p s l m -> p s m l")
+            nc.scalar.copy(out=dst, in_=src)
+
+        def quantise_spread(n, lo, hi):
+            i = n - SPREAD_FROM
+            wq_t[n], ws_t[n] = wide_q[i], wide_s[i]
+            runs = []
+            for pair in range(lo // 2, hi // 2):
+                if pair == lo // 2:
+                    runs.append((4 * pair, 1, pair * SPREAD))
+                runs.append((4 * pair + 1, 2, pair * SPREAD + 2 * RUN))
+                runs.append((4 * pair + 3, 2 if 2 * pair + 2 < hi else 1, pair * SPREAD + 5 * RUN))
+            for first, count, col in runs:
+                nc.vector.quantize_mx(
+                    out=wq_t[n][:, col : col + count * RUN].bitcast(FP8X4),
+                    scales=ws_t[n][:, col : col + count * RUN],
+                    in_=wsb_t[n][:, first * 4 * RUN : (first + count) * 4 * RUN],
+                )
 
         def quantise_w(n, lo, hi):
+            if n >= SPREAD_FROM:
+                return quantise_spread(n, lo, hi)
             if lo == 0:
                 wq_t[n] = work.tile([P, BN * P], U32, align_bytes=64, name="wq")
                 ws_t[n] = work.tile([P, BN * P], U8, align_bytes=64, name="ws")
@@ -341,6 +374,22 @@ def tile_polnormal_nolayer_t_kernel(tc, x, coords_x, coords_y, phis, dists_param
                 ops_t[(n, half)] = ps_t.tile([P, 4, BATCH * CH], F32, tag="tcp", name="ops_end")
             else:
                 ops_t[(n, half)] = ps_o.tile([P, 4, BATCH * CH], F32, tag="ops", name="ops")
+            if n >= SPREAD_FROM:
+                for r in range(2):
+                    for s in range(2):
+                        for o in range(2):
+                            at = (2 * half + r) * SPREAD + (3 * s + o) * RUN
+                            node = half * 4 + 2 * r + o
+                            nc.tensor.matmul_mx(
+                                out=ops_t[(n, half)][:, 2 * r + s, :],
+                                lhsT=wq_t[n][:, at : at + P].bitcast(FP8X4),
+                                lhsT_scale=ws_t[n][:, at : at + P],
+                                rhs=xq_t[n][:, node * P : (node + 1) * P].bitcast(FP8X4),
+                                rhs_scale=xs_t[n][:, node * P : (node + 1) * P],
+                                start=o == 0,
+                                stop=o == 1,
+                            )
+                return
             for i in range(4):
                 cols = slice((half * 4 + i) * P, (half * 4 + i + 1) * P)
                 nc.tensor.matmul_mx(
@@ -356,8 +405,13 @@ def tile_polnormal_nolayer_t_kernel(tc, x, coords_x, coords_y, phis, dists_param
         def rows_out(n, half, on_vector=False):
             if half == 0:
                 osb_t[n] = work.tile([P, BN, BATCH * CH], F32, name="osb")
-            dst = osb_t[n][:, half * 4 : half * 4 + 4, :].rearrange("m o n -> m (o n)")
-            src = ops_t[(n, half)][:].rearrange("m o n -> m (o n)")
+            if n < SPREAD_FROM:
+                dst = osb_t[n][:, half * 4 : half * 4 + 4, :].rearrange("m o n -> m (o n)")
+                src = ops_t[(n, half)][:].rearrange("m o n -> m (o n)")
+            else:
+                dst = osb_t[n][:].rearrange("m o n -> m (o n)").rearrange("m (r b e c) -> m r b e c", b=BATCH, e=2, c=CH)
+                dst = dst[:, 2 * half : 2 * half + 2, :, :, :]
+                src = ops_t[(n, half)][:].rearrange("m (r e) (b c) -> m r b e c", e=2, b=BATCH)
             if on_vector:
                 nc.vector.tensor_copy(out=dst, in_=src)
             else:
@@ -365,6 +419,14 @@ def tile_polnormal_nolayer_t_kernel(tc, x, coords_x, coords_y, phis, dists_param
 
         def store(n, half):
             lo = half * 4
+            if n >= SPREAD_FROM:
+                rows = osb_t[n][:].rearrange("m o n -> m (o n)").rearrange("m (r b k) -> m r b k", b=BATCH, k=2 * CH)
+                for r in range(2):
+                    for o in range(2):
+                        nc.sync.dma_start(
+                            out=ov2[n * BN + lo + 2 * r + o], in_=rows[o * RUN : (o + 1) * RUN, 2 * half + r, :, :]
+                        )
+                return
             for b in range(BATCH):
                 nc.sync.dma_start(
                     out=ov[b, :, n * BN + lo : n * BN + lo + 4, :],

import math
from contextlib import ExitStack

import concourse.mybir as mybir
from concourse.masks import make_identity

F32 = mybir.dt.float32
BF16 = mybir.dt.bfloat16
I32 = mybir.dt.int32
U32 = mybir.dt.uint32
U8 = mybir.dt.uint8
FP8X4 = mybir.dt.float8_e4m3fn_x4
ALU = mybir.AluOpType
ACT = mybir.ActivationFunctionType
AXES = mybir.AxisListType

P = 128
NODES = 128
BATCH = 4
CH = 32
NPHI = 8
NDIST = 8
T = 4
BN = 8
BLOCKS = NODES // BN
PAIRS = BN // 2
SUPER = 2 * BN
S_UNITS = 2
G_UNIT = 20
CELLS = P * T
RUN = P // 2
SPREAD = 6 * RUN
SPREAD_FROM = BLOCKS - 2

FLOPS = 2 * NODES * CELLS * 128 * (BATCH * CH)

TWO_PI = 2.0 * math.pi
TWO_PI_HI = 6.28125
TWO_PI_LO = TWO_PI - TWO_PI_HI


def tile_polnormal_nolayer_t_kernel(tc, x, coords_x, coords_y, phis, dists_param, sigma_param, out):
    nc = tc.nc
    xv = x.rearrange("b (o p t) u v c -> p o b (t u v c)", o=NODES, p=P, t=T)
    ov = out.rearrange("b o v f d s c -> b (v f d s) o c")
    ov2 = out.rearrange("b o v f d s c -> o (v f d) b (s c)")
    coords = [c.rearrange("a o i j -> (a o) (i j)") for c in (coords_x, coords_y)]

    with ExitStack() as ctx:
        const = ctx.enter_context(tc.tile_pool(name="const", bufs=1))
        xin = ctx.enter_context(tc.tile_pool(name="xin", bufs=4))
        xgp = ctx.enter_context(tc.tile_pool(name="xgp", bufs=1))
        xqp = ctx.enter_context(tc.tile_pool(name="xqp", bufs=3))
        work = ctx.enter_context(tc.tile_pool(name="work", bufs=2))
        ps_s = ctx.enter_context(tc.psum_pool(name="ps_s", bufs=1))
        ps_t = ctx.enter_context(tc.psum_pool(name="ps_t", bufs=2))
        ps_w = ctx.enter_context(tc.psum_pool(name="ps_w", bufs=3))
        ps_o = ctx.enter_context(tc.psum_pool(name="ps_o", bufs=2))
        ctx.enter_context(tc.manual_schedule())

        row = const.tile([P, 3 * 16], BF16)
        nc.vector.memset(row[:], 0.0)
        ones = const.tile([P, P], BF16)
        nc.vector.memset(ones[:], 1.0)
        ccb = [const.tile([P, CELLS], BF16, name="ccb%d" % half) for half in range(2)]
        ccf = [const.tile([P, T, P], F32, name="ccf%d" % half) for half in range(2)]

        def load_rows(half):
            for c in range(2):
                nc.sync.dma_start(
                    out=ccb[half][c * 64 : (c + 1) * 64, :], in_=coords[c][half * 64 : (half + 1) * 64, :]
                )

        load_rows(0)
        for vec, lo, hi in ((phis, 0, NPHI), (dists_param, 16, 16 + NDIST), (sigma_param, 32, 34)):
            nc.sync.dma_start(out=row[0:1, lo:hi], in_=vec.unsqueeze(0))

        seed = const.tile([P, 1], F32)
        nc.vector.memset(seed[:], 0.0)
        warm = const.tile([P, 2], F32)
        nc.scalar.activation(out=warm[:, 0:1], in_=seed[:], func=ACT.Silu)
        identf = const.tile([P, P], F32)
        make_identity(nc, identf[:])
        identb = const.tile([P, P], BF16)
        nc.vector.tensor_copy(out=identb[:], in_=identf[:])
        fold = const.tile([P, 64], F32)
        nc.vector.tensor_tensor(out=fold[:], in0=identf[:, 0:64], in1=identf[:, 64:128], op=ALU.add)
        pick = const.tile([P, NDIST], F32)
        nc.vector.tensor_reduce(
            out=pick[:], in_=identf[:].rearrange("q (o d f) -> q d o f", o=2, d=NDIST), axis=AXES.XY, op=ALU.add
        )

        wide_q = [const.tile([P, PAIRS * SPREAD], U32, align_bytes=64, name="wide_q%d" % i) for i in range(2)]
        wide_s = [const.tile([P, PAIRS * SPREAD], U8, align_bytes=64, name="wide_s%d" % i) for i in range(2)]
        for i in range(2):
            gaps = wide_q[i][:].rearrange("p (g k) -> p g k", k=3 * RUN)[:, :, RUN : 2 * RUN]
            nc.gpsimd.memset(gaps, 0)
            gaps = wide_s[i][:].bitcast(U32).rearrange("p (g k) -> p g k", k=3 * RUN // 4)
            nc.gpsimd.memset(gaps[:, :, RUN // 4 : 2 * RUN // 4], 0)

        turns = const.tile([P, NPHI], I32)
        rest = const.tile([P, NPHI], F32)
        angle = const.tile([P, NPHI], F32)
        trig = const.tile([P, NPHI], F32)
        th = const.tile([P, NDIST + 2], F32)
        ds = const.tile([P, NDIST], F32)
        m2d = const.tile([P, NDIST], F32)
        d2 = const.tile([P, NDIST], F32)
        d2_of = const.tile([P, NDIST], F32)
        d2_q = const.tile([P, 1], F32)
        sg = const.tile([P, 2], F32)
        sg2 = const.tile([P, 2], F32)
        na = const.tile([P, 2], F32)
        bias = const.tile([P, 2], F32)

        def rows_to_float(copy, half):
            copy(out=ccf[half][:], in_=ccb[half][:].rearrange("q (p t) -> q t p", t=T))

        pars = ps_o.tile([P, 3 * 16], F32, tag="ops", name="pars")
        nc.tensor.matmul(out=pars[:], lhsT=ones[:], rhs=row[:], start=True, stop=True)
        ph_b, pr_b, sp_b = pars[:, 0:NPHI], pars[:, 16 : 16 + NDIST], pars[:, 32:34]
        nc.vector.tensor_scalar(
            out=turns[0:64, :], in0=ph_b[0:64, :], scalar1=1.0 / TWO_PI, scalar2=0.25, op0=ALU.mult, op1=ALU.add
        )
        nc.vector.tensor_scalar(
            out=turns[64:128, :], in0=ph_b[64:128, :], scalar1=1.0 / TWO_PI, scalar2=None, op0=ALU.mult
        )
        nc.scalar.activation(out=th[:, 0:NDIST], in_=pr_b, func=ACT.Tanh, scale=0.5)
        nc.vector.scalar_tensor_tensor(
            out=rest[:], in0=turns[:], scalar=-TWO_PI_HI, in1=ph_b, op0=ALU.mult, op1=ALU.add
        )
        nc.scalar.activation(out=th[:, NDIST:], in_=sp_b, func=ACT.Tanh, scale=0.5)
        nc.vector.tensor_scalar(out=ds[:], in0=th[:, 0:NDIST], scalar1=1.0, scalar2=None, op0=ALU.add)
        nc.vector.scalar_tensor_tensor(
            out=angle[:], in0=turns[:], scalar=-TWO_PI_LO, in1=rest[:], op0=ALU.mult, op1=ALU.add
        )
        nc.scalar.activation(out=trig[0:64, :], in_=angle[0:64, :], func=ACT.Sin, bias=0.5 * math.pi)
        nc.scalar.activation(out=trig[64:128, :], in_=angle[64:128, :], func=ACT.Sin)
        nc.vector.tensor_scalar(
            out=sg[:], in0=th[:, NDIST:], scalar1=1.0, scalar2=1e-10, op0=ALU.add, op1=ALU.max
        )
        rows_to_float(nc.vector.tensor_copy, 0)
        nc.vector.tensor_scalar(out=m2d[:], in0=ds[:], scalar1=-2.0, scalar2=None, op0=ALU.mult)
        nc.vector.scalar_tensor_tensor(out=sg2[:], in0=sg[:], scalar=-2.0, in1=sg[:], op0=ALU.mult, op1=ALU.mult)
        nc.vector.tensor_tensor(out=d2[:], in0=ds[:], in1=ds[:], op=ALU.mult)

        r2_t = {}

        def squares(half):
            cps = ps_w.tile([P, T, 2, 64], BF16, tag="wps", name="cps")
            view = ccb[half][:].rearrange("q (p t) -> q t p", t=T)
            for t in range(T):
                nc.tensor.transpose(
                    out=cps[:, t, :, :].rearrange("p c o -> p (c o)"), in_=view[:, t, :], identity=identb[:]
                )
            sq = work.tile([P, T, 2, 64], F32, name="sq")
            nc.scalar.activation(
                out=sq[:].rearrange("p t c o -> p (t c o)"),
                in_=cps[:].rearrange("p t c o -> p (t c o)"),
                func=ACT.Square,
            )
            return sq

        def add_squares(engine, half, sq):
            r2_t[half] = const.tile([P, 32, T, 2], F32, name="r2_%d" % half)
            engine.tensor_tensor(
                out=r2_t[half][:],
                in0=sq[:, :, 0, :].rearrange("p t (r o) -> p r t o", o=2),
                in1=sq[:, :, 1, :].rearrange("p t (r o) -> p r t o", o=2),
                op=ALU.add,
            )

        sq0 = squares(0)
        nc.scalar.activation(out=warm[:, 1:2], in_=seed[:], func=ACT.Exp)

        proj = const.tile([P, 64, NPHI], F32)

        def project_table(engine, lo, hi):
            engine.tensor_tensor(
                out=proj[:, lo:hi, :],
                in0=fold[:, lo:hi].unsqueeze(2).to_broadcast([P, hi - lo, NPHI]),
                in1=trig[:].unsqueeze(1).to_broadcast([P, hi - lo, NPHI]),
                op=ALU.mult,
            )

        project_table(nc.vector, 0, 4)
        nc.vector.reciprocal(out=na[:], in_=sg2[:])
        nc.vector.tensor_tensor(out=d2_of[:], in0=pick[:], in1=d2[:], op=ALU.mult)
        project_table(nc.vector, 4, SUPER)
        nc.vector.reduce_sum(out=d2_q[:], in_=d2_of[:], axis=AXES.X)
        add_squares(nc.vector, 0, sq0)
        nc.vector.tensor_scalar(out=bias[:], in0=na[:], scalar1=d2_q[:, 0:1], scalar2=None, op0=ALU.mult)

        xr_t, xg_t, xq_t, xs_t, ups_t, ta_t, tcp_t, gc_t, part_t = {}, {}, {}, {}, {}, {}, {}, {}, {}
        den_t, inv_t, wc_t, wps_t, wsb_t, wq_t, ws_t, ops_t, osb_t = {}, {}, {}, {}, {}, {}, {}, {}, {}

        perm = const.tile([P, P], F32)

        def late_constants():
            project_table(nc.gpsimd, SUPER, 64)
            nc.gpsimd.tensor_copy(
                out=perm[:].rearrange("q (o f d) -> q o f d", o=2, f=NPHI),
                in_=identf[:].rearrange("q (o d f) -> q o f d", o=2, d=NDIST),
            )

        def live(n):
            return 0 <= n < BLOCKS

        def load_x(n):
            xr_t[n] = xin.tile([P, BN, BATCH, T * CH], BF16, name="xr")
            for o in range(BN):
                nc.sync.dma_start(out=xr_t[n][:, o, :, :], in_=xv[:, n * BN + o, :, :])

        def g_unit(n):
            return G_UNIT if n < BLOCKS - 2 else BN * BATCH

        def interleave_on_gpsimd(n):
            xg_t[n] = xgp.tile([P, BN, BATCH, CH, T], BF16, align_bytes=64, name="xg")
            if g_unit(n) == BN * BATCH:
                return
            nc.gpsimd.tensor_copy(
                out=xg_t[n][:].rearrange("p o b c t -> p (o b) c t")[:, G_UNIT:, :, :],
                in_=xr_t[n][:].rearrange("p o b (t c) -> p (o b) c t", t=T)[:, G_UNIT:, :, :],
            )

        def interleave_on_vector(n, lo=S_UNITS, hi=None):
            hi = hi or g_unit(n)
            nc.vector.tensor_copy(
                out=xg_t[n][:].rearrange("p o b (g i) t -> p (o b) g t i", i=8)[:, lo:hi, :, :, :],
                in_=xr_t[n][:].rearrange("p o b (t g i) -> p (o b) g t i", t=T, i=8)[:, lo:hi, :, :, :],
            )

        def interleave_on_scalar(n):
            nc.scalar.copy(
                out=xg_t[n][:].rearrange("p o b (g i) t -> p (o b) g t i", i=8)[:, 0:S_UNITS, :, :, :],
                in_=xr_t[n][:].rearrange("p o b (t g i) -> p (o b) g t i", t=T, i=8)[:, 0:S_UNITS, :, :, :],
            )

        def quantise_x(n):
            xq_t[n] = xqp.tile([P, BN * P], U32, align_bytes=64, name="xq")
            xs_t[n] = xqp.tile([P, BN * P], U8, align_bytes=64, name="xs")
            nc.vector.quantize_mx(
                out=xq_t[n][:].bitcast(FP8X4),
                scales=xs_t[n][:],
                in_=xg_t[n][:].rearrange("p o b c t -> p (o b c t)"),
            )

        def project(m, lo=0, hi=SUPER // 2):
            half, first = divmod(m * SUPER, 64)
            if lo == 0:
                ups_t[m] = ps_s.tile([P, SUPER // 2, T, 2, NPHI], F32, tag="s", name="ups")
            for t in range(T):
                nc.tensor.matmul(
                    out=ups_t[m][:, lo:hi, t, :, :],
                    lhsT=ccf[half][:, t, :],
                    rhs=proj[:, first + 2 * lo : first + 2 * hi, :],
                    start=True,
                    stop=True,
                )

        def distances(m, d_range, lo=0, hi=SUPER // 2):
            if m not in ta_t:
                ta_t[m] = work.tile([P, SUPER // 2, T, 2, NDIST, NPHI], F32, name="ta")
            half, first = divmod(m * SUPER // 2, 32)
            r2 = r2_t[half][:, first + lo : first + hi, :, :].rearrange("p r t o -> p (r t o)")
            for d in d_range:
                nc.vector.scalar_tensor_tensor(
                    out=ta_t[m][:, lo:hi, :, :, d, :].rearrange("p r t o f -> p (r t o) f"),
                    in0=ups_t[m][:, lo:hi, :, :, :].rearrange("p r t o f -> p (r t o) f"),
                    scalar=m2d[:, d : d + 1],
                    in1=r2.unsqueeze(2).to_broadcast([P, (hi - lo) * T * 2, NPHI]),
                    op0=ALU.mult,
                    op1=ALU.add,
                )

        def to_components(n, pair):
            tcp_t[(n, pair)] = ps_t.tile([P, T, P], F32, tag="tcp", name="tcp")
            for t in range(T):
                nc.tensor.transpose(
                    out=tcp_t[(n, pair)][:, t, :],
                    in_=ta_t[n // 2][:, n % 2 * PAIRS + pair, t, :, :, :].rearrange("p o d f -> p (o d f)"),
                    identity=identf[:],
                )

        def exponentials(n, pair):
            if pair == 0:
                gc_t[n] = work.tile([P, PAIRS, 2, 2, P, 2], F32, name="gc")
                part_t[n] = work.tile([P, BN], F32, name="part")
            for s in range(2):
                col = 2 * pair + s
                nc.scalar.activation(
                    out=gc_t[n][:, pair, s, :, :, :],
                    in_=tcp_t[(n, pair)][:].rearrange("q (l h) p -> q l p h", h=2),
                    func=ACT.Exp,
                    bias=bias[:, s : s + 1],
                    scale=na[:, s : s + 1],
                    accum_out=part_t[n][:, col : col + 1],
                )

        def denominators(n, lo=0, hi=BN):
            if lo == 0:
                den_t[n] = work.tile([P, BN], F32, name="den")
            nc.vector.tensor_scalar(
                out=den_t[n][:, lo:hi], in0=part_t[n][:, lo:hi], scalar1=1e-20, scalar2=None, op0=ALU.add
            )

        def reciprocals(n, lo=0, hi=BN):
            if lo == 0:
                inv_t[n] = work.tile([P, BN], F32, name="inv")
            nc.vector.reciprocal(out=inv_t[n][:, lo:hi], in_=den_t[n][:, lo:hi])

        def normalise(n, pair):
            if pair == 0:
                wc_t[n] = work.tile([P, PAIRS, 2, 2, 2 * P], BF16, name="wc")
            wps_t[(n, pair)] = ps_w.tile([P, 2, 2, P], F32, tag="wps", name="wps")
            for s in range(2):
                nc.vector.tensor_scalar(
                    out=wc_t[n][:, pair, s, :, :].rearrange("q l x -> q (l x)"),
                    in0=gc_t[n][:, pair, s, :, :, :].rearrange("q l p h -> q (l p h)"),
                    scalar1=inv_t[n][:, 2 * pair + s : 2 * pair + s + 1],
                    scalar2=None,
                    op0=ALU.mult,
                )
                for l in range(2):
                    nc.tensor.transpose(
                        out=wps_t[(n, pair)][:, s, l, :],
                        in_=wc_t[n][:, pair, s, l, :].bitcast(F32),
                        identity=perm[:],
                    )

        def weights_out(n, pair):
            if pair == 0:
                wsb_t[n] = work.tile([P, BN * 4 * P], BF16, align_bytes=64, name="wsb")
            words = wsb_t[n][:].bitcast(F32)[:, pair * 4 * P : (pair + 1) * 4 * P]
            if n < SPREAD_FROM:
                dst = words.rearrange("p (m x) -> p m x", x=4)
                src = wps_t[(n, pair)][:].rearrange("p s l m -> p m (s l)")
            else:
                dst = words.rearrange("p (e m l) -> p e m l", e=2, l=2)
                src = wps_t[(n, pair)][:].rearrange("p s l m -> p s m l")
            nc.scalar.copy(out=dst, in_=src)

        def quantise_spread(n, lo, hi):
            i = n - SPREAD_FROM
            wq_t[n], ws_t[n] = wide_q[i], wide_s[i]
            runs = []
            for pair in range(lo // 2, hi // 2):
                if pair == lo // 2:
                    runs.append((4 * pair, 1, pair * SPREAD))
                runs.append((4 * pair + 1, 2, pair * SPREAD + 2 * RUN))
                runs.append((4 * pair + 3, 2 if 2 * pair + 2 < hi else 1, pair * SPREAD + 5 * RUN))
            for first, count, col in runs:
                nc.vector.quantize_mx(
                    out=wq_t[n][:, col : col + count * RUN].bitcast(FP8X4),
                    scales=ws_t[n][:, col : col + count * RUN],
                    in_=wsb_t[n][:, first * 4 * RUN : (first + count) * 4 * RUN],
                )

        def quantise_w(n, lo, hi):
            if n >= SPREAD_FROM:
                return quantise_spread(n, lo, hi)
            if lo == 0:
                wq_t[n] = work.tile([P, BN * P], U32, align_bytes=64, name="wq")
                ws_t[n] = work.tile([P, BN * P], U8, align_bytes=64, name="ws")
            cols = slice(lo * P, hi * P)
            nc.vector.quantize_mx(
                out=wq_t[n][:, cols].bitcast(FP8X4),
                scales=ws_t[n][:, cols],
                in_=wsb_t[n][:, lo * 4 * P : hi * 4 * P],
            )

        def pool_nodes(n, half):
            if n == BLOCKS - 1:
                ops_t[(n, half)] = ps_t.tile([P, 4, BATCH * CH], F32, tag="tcp", name="ops_end")
            else:
                ops_t[(n, half)] = ps_o.tile([P, 4, BATCH * CH], F32, tag="ops", name="ops")
            if n >= SPREAD_FROM:
                for r in range(2):
                    for s in range(2):
                        for o in range(2):
                            at = (2 * half + r) * SPREAD + (3 * s + o) * RUN
                            node = half * 4 + 2 * r + o
                            nc.tensor.matmul_mx(
                                out=ops_t[(n, half)][:, 2 * r + s, :],
                                lhsT=wq_t[n][:, at : at + P].bitcast(FP8X4),
                                lhsT_scale=ws_t[n][:, at : at + P],
                                rhs=xq_t[n][:, node * P : (node + 1) * P].bitcast(FP8X4),
                                rhs_scale=xs_t[n][:, node * P : (node + 1) * P],
                                start=o == 0,
                                stop=o == 1,
                            )
                return
            for i in range(4):
                cols = slice((half * 4 + i) * P, (half * 4 + i + 1) * P)
                nc.tensor.matmul_mx(
                    out=ops_t[(n, half)][:, i, :],
                    lhsT=wq_t[n][:, cols].bitcast(FP8X4),
                    lhsT_scale=ws_t[n][:, cols],
                    rhs=xq_t[n][:, cols].bitcast(FP8X4),
                    rhs_scale=xs_t[n][:, cols],
                    start=True,
                    stop=True,
                )

        def rows_out(n, half, on_vector=False):
            if half == 0:
                osb_t[n] = work.tile([P, BN, BATCH * CH], F32, name="osb")
            if n < SPREAD_FROM:
                dst = osb_t[n][:, half * 4 : half * 4 + 4, :].rearrange("m o n -> m (o n)")
                src = ops_t[(n, half)][:].rearrange("m o n -> m (o n)")
            else:
                dst = osb_t[n][:].rearrange("m o n -> m (o n)").rearrange("m (r b e c) -> m r b e c", b=BATCH, e=2, c=CH)
                dst = dst[:, 2 * half : 2 * half + 2, :, :, :]
                src = ops_t[(n, half)][:].rearrange("m (r e) (b c) -> m r b e c", e=2, b=BATCH)
            if on_vector:
                nc.vector.tensor_copy(out=dst, in_=src)
            else:
                nc.scalar.copy(out=dst, in_=src)

        def store(n, half):
            lo = half * 4
            if n >= SPREAD_FROM:
                rows = osb_t[n][:].rearrange("m o n -> m (o n)").rearrange("m (r b k) -> m r b k", b=BATCH, k=2 * CH)
                for r in range(2):
                    for o in range(2):
                        nc.sync.dma_start(
                            out=ov2[n * BN + lo + 2 * r + o], in_=rows[o * RUN : (o + 1) * RUN, 2 * half + r, :, :]
                        )
                return
            for b in range(BATCH):
                nc.sync.dma_start(
                    out=ov[b, :, n * BN + lo : n * BN + lo + 4, :],
                    in_=osb_t[n][:, lo : lo + 4, b * CH : (b + 1) * CH],
                )

        def finish(n, half, on_vector=False):
            rows_out(n, half, on_vector)
            store(n, half)

        def when(n, stage, *args):
            if live(n):
                stage(n, *args)

        ALL_D, LOW_D, HIGH_D = range(NDIST), range(4), range(4, NDIST)
        project(0, 0, 2)
        project(0, 2, 4)
        load_x(0)
        load_rows(1)
        interleave_on_gpsimd(0)
        interleave_on_vector(0, S_UNITS, 8)
        distances(0, ALL_D, 0, 1)
        to_components(0, 0)
        project(0, 4, 8)
        distances(0, ALL_D, 1, 2)
        to_components(0, 1)
        late_constants()
        interleave_on_scalar(0)
        distances(0, ALL_D, 2, 4)
        load_x(1)
        exponentials(0, 0)
        to_components(0, 2)
        exponentials(0, 1)
        to_components(0, 3)
        distances(0, ALL_D, 4, 8)
        load_x(2)
        project(1)
        exponentials(0, 2)
        to_components(1, 0)
        exponentials(0, 3)
        to_components(1, 1)
        interleave_on_vector(0, 8)
        quantise_x(0)
        interleave_on_gpsimd(1)
        distances(1, LOW_D)
        interleave_on_scalar(1)
        exponentials(1, 0)
        to_components(1, 2)
        exponentials(1, 1)
        to_components(1, 3)
        denominators(0)
        reciprocals(0)
        exponentials(1, 2)
        exponentials(1, 3)
        for pair in range(PAIRS):
            normalise(0, pair)
            weights_out(0, pair)
        distances(1, HIGH_D)
        sq1 = squares(1)
        rows_to_float(nc.scalar.copy, 1)
        project(2)
        to_components(2, 0)
        to_components(2, 1)
        interleave_on_vector(1)
        load_x(3)
        quantise_x(1)
        interleave_on_gpsimd(2)
        add_squares(nc.gpsimd, 1, sq1)
        distances(2, LOW_D)
        last = BLOCKS - 1
        for n in range(2, last):
            m, high = divmod(n + 3, 2)
            when(n + 2, load_x)
            denominators(n - 1)
            when(n - 2, quantise_w, 0, 4)
            reciprocals(n - 1)
            when(n - 2, quantise_w, 4, 8)
            interleave_on_scalar(n)
            exponentials(n, 0)
            to_components(n, 2)
            exponentials(n, 1)
            if n == 2:
                to_components(n, 3)
            normalise(n - 1, 0)
            if n > 2:
                to_components(n, 3)
            exponentials(n, 2)
            exponentials(n, 3)
            when(n - 2, pool_nodes, 0)
            when(n - 2, pool_nodes, 1)
            normalise(n - 1, 1)
            normalise(n - 1, 2)
            weights_out(n - 1, 0)
            weights_out(n - 1, 1)
            weights_out(n - 1, 2)
            interleave_on_vector(n)
            normalise(n - 1, 3)
            weights_out(n - 1, 3)
            quantise_x(n)
            when(n + 1, interleave_on_gpsimd)
            if m < BLOCKS // 2:
                distances(m, HIGH_D if high else LOW_D)
            when(n + 1, to_components, 0)
            when(n + 1, to_components, 1)
            if high and m + 1 < BLOCKS // 2:
                project(m + 1)
            when(n - 2, finish, 0, n == last - 1)
            when(n - 2, finish, 1, n == last - 1)
        n = last
        denominators(n - 1)
        reciprocals(n - 1)
        interleave_on_scalar(n)
        exponentials(n, 0)
        normalise(n - 1, 0)
        to_components(n, 2)
        exponentials(n, 1)
        normalise(n - 1, 1)
        to_components(n, 3)
        normalise(n - 1, 2)
        weights_out(n - 1, 0)
        normalise(n - 1, 3)
        quantise_w(n - 2, 0, 8)
        pool_nodes(n - 2, 0)
        pool_nodes(n - 2, 1)
        weights_out(n - 1, 1)
        weights_out(n - 1, 2)
        denominators(n, 0, 4)
        weights_out(n - 1, 3)
        exponentials(n, 2)
        exponentials(n, 3)
        interleave_on_vector(n)
        reciprocals(n, 0, 4)
        finish(n - 2, 0, True)
        normalise(n, 0)
        finish(n - 2, 1, True)
        normalise(n, 1)
        weights_out(n, 0)
        weights_out(n, 1)
        quantise_w(n - 1, 0, 8)
        pool_nodes(n - 1, 0)
        pool_nodes(n - 1, 1)
        denominators(n, 4, 8)
        quantise_x(n)
        reciprocals(n, 4, 8)
        finish(n - 1, 0)
        normalise(n, 2)
        normalise(n, 3)
        weights_out(n, 2)
        weights_out(n, 3)
        quantise_w(n, 0, 4)
        pool_nodes(n, 0)
        finish(n - 1, 1, True)
        quantise_w(n, 4, 8)
        pool_nodes(n, 1)
        finish(n, 0)
        finish(n, 1, True)
